import numpy as np
import ml_dtypes


def mxq(x, axis, fmt="e4m3"):
    dtype, down = {"e4m3": (ml_dtypes.float8_e4m3fn, 7), "e5m2": (ml_dtypes.float8_e5m2, 14)}[fmt]
    v = np.moveaxis(np.asarray(x, np.float32).astype(ml_dtypes.bfloat16).astype(np.float64), axis, -1)
    blocks = v.reshape(v.shape[:-1] + (-1, 32))
    amax = np.abs(blocks).max(-1, keepdims=True)
    byte = np.maximum(np.where(amax > 0, np.frexp(amax)[1] - 1 + 127, 0) - down, 1)
    scale = np.exp2(byte - 127.0)
    codes = (blocks / scale).astype(np.float32).astype(dtype).astype(np.float64)
    return np.moveaxis((codes * scale).reshape(v.shape), -1, axis)


WIDE = False


def mx_kscale(k):
    if not WIDE:
        return np.ones(k)
    levels = np.array([18, -18])
    if k % 512:
        return np.exp2(np.random.permutation(np.resize(levels, k // 32))).repeat(32)
    a = np.empty((k // 512, 16))
    for p in range(k // 512):
        a[p, :8] = np.random.permutation(np.resize(levels, 8))
        for g in range(8):
            far = levels[np.abs(levels - a[p, g]) >= 10]
            a[p, g + 8] = far[np.random.randint(len(far))]
    return np.exp2(a.ravel()).repeat(32)


BF16 = ml_dtypes.bfloat16


def bf(x):
    return np.asarray(x, np.float32).astype(BF16)


def f64(x):
    return np.asarray(x).astype(np.float64)


B, S, M, H, HD = 2, 512, 1024, 12, 128
T = B * S
E = H * HD


def sigmoid(v):
    return 1.0 / (1.0 + np.exp(-v))


def setup_inputs():
    s = mx_kscale(T).reshape(B, S, 1)
    u = mx_kscale(M)
    v = mx_kscale(E).reshape(H, HD)
    x0 = bf(np.random.standard_normal((B, S, M)))
    wq0 = bf(np.random.standard_normal((M, H, HD)) / np.sqrt(M))
    attn = bf(np.random.standard_normal((B, S, H, HD)) * 0.5)
    wo0 = bf(np.random.standard_normal((H, HD, M)) * 2.0 / np.sqrt(E))
    g = bf(np.random.standard_normal((B, S, M)) * np.exp2(np.random.randint(-6, 1, (B, S, 1))) * 8.0 / s * u)
    gate = (f64(x0).reshape(T, M) @ f64(wq0).reshape(M, E)).reshape(B, S, H, HD)
    return {"hidden_states": bf(f64(x0) * s),
            "Wq_gate": bf(f64(wq0) / v),
            "attn": attn,
            "Wo": bf(f64(wo0) * v[:, :, None] / u),
            "gate": np.asarray(gate, np.float32),
            "grad_out": g}


def reference(hidden_states, Wq_gate, attn, Wo, gate, grad_out):
    sg = sigmoid(f64(gate).reshape(T, E))
    go = f64(grad_out).reshape(T, M)
    wo = f64(Wo).reshape(E, M)
    dg = mxq(go, 1, "e5m2") @ mxq(wo, 1, "e4m3").T
    dz = dg * f64(attn).reshape(T, E) * sg * (1.0 - sg)
    wq = f64(Wq_gate).reshape(M, E)
    x = f64(hidden_states).reshape(T, M)
    dx = mxq(dz, 1, "e5m2") @ mxq(wq, 1, "e4m3").T
    dw = mxq(x, 0, "e4m3").T @ mxq(dz, 0, "e5m2")
    return dx.reshape(B, S, M), dw.reshape(M, H, HD)

@@ -1,0 +1,338 @@
+from contextlib import ExitStack
+
+import concourse.mybir as mybir
+from concourse.masks import make_identity
+
+T, M, E = 1024, 1024, 1536
+FLOPS = 3 * 2 * T * M * E
+BYTES = 2 * (T * M + M * E + T * E + E * M + T * M) + 4 * T * E + 4 * (T * M + M * E)
+
+F32 = mybir.dt.float32
+BF16 = mybir.dt.bfloat16
+U32 = mybir.dt.uint32
+U8 = mybir.dt.uint8
+E4M3 = mybir.dt.float8_e4m3fn_x4
+E5M2 = mybir.dt.float8_e5m2_x4
+ALU = mybir.AluOpType
+ACT = mybir.ActivationFunctionType
+
+P = 128
+W = 512
+
+
+def tile_qwen3_5attention_pb_v_kernel(tc, hidden, wq, attn, wo, gate, gout, dx_out, dw_out):
+    nc = tc.nc
+    x_v = hidden.rearrange("b s m -> (b s) m").rearrange("(g p j) m -> g p j m", g=2, j=4)
+    g_v = gout.rearrange("b s m -> (b s) m").rearrange("(g p j) m -> g p j m", g=2, j=4)
+    wq_v = wq.rearrange("m u h -> m (u h)").rearrange("(r b q) e -> r q b e", r=4, q=P)
+    wo_v = wo.rearrange("u h m -> (u h) m").rearrange("(c b q) m -> c q b m", c=3, q=P)
+    at_v = attn.rearrange("b s u h -> (b s) (u h)").rearrange("(g p j) e -> g p j e", g=2, j=4)
+    ga_v = gate.rearrange("b s u h -> (b s) (u h)").rearrange("(g p j) e -> g p j e", g=2, j=4)
+    dx_v = dx_out.rearrange("b s m -> (b s) m").rearrange("(g p j) m -> g j p m", g=2, j=4)
+    dw_v = dw_out.rearrange("m u h -> m (u h)").rearrange("(t q) e -> t q e", q=P)
+
+    with ExitStack() as ctx:
+        keep = ctx.enter_context(tc.tile_pool(name="keep", bufs=1))
+        raw = ctx.enter_context(tc.tile_pool(name="raw", bufs=2))
+        ewp = ctx.enter_context(tc.tile_pool(name="ewp", bufs=3))
+        stage = ctx.enter_context(tc.tile_pool(name="stage", bufs=4))
+        stageq = ctx.enter_context(tc.tile_pool(name="stageq", bufs=1))
+        stagex = ctx.enter_context(tc.tile_pool(name="stagex", bufs=2))
+        mid = ctx.enter_context(tc.tile_pool(name="mid", bufs=2))
+        rot = ctx.enter_context(tc.tile_pool(name="rot", bufs=4))
+        outp = ctx.enter_context(tc.tile_pool(name="outp", bufs=6))
+        ps_dg = ctx.enter_context(tc.psum_pool(name="ps_dg", bufs=2))
+        ps_tr = ctx.enter_context(tc.psum_pool(name="ps_tr", bufs=3))
+        ps_out = ctx.enter_context(tc.psum_pool(name="ps_out", bufs=3))
+
+        ident = keep.tile([P, P], F32, name="ident")
+        make_identity(nc, ident[:])
+
+        def copy(eng, out, in_):
+            if eng == "S":
+                nc.scalar.copy(out=out, in_=in_)
+            else:
+                nc.vector.tensor_copy(out=out, in_=in_)
+
+        def new_codes(pool, cols, tag):
+            codes = pool.tile([P, cols], U32, name=tag + "_c", align_bytes=64)
+            scales = pool.tile([P, cols], U8, name=tag + "_s", align_bytes=64)
+            return codes, scales
+
+        def quantize(cs, c0, fmt, src):
+            codes, scales = cs
+            n = src.shape[1]
+            nc.vector.quantize_mx(
+                out=codes[:, c0:c0 + n].bitcast(fmt),
+                scales=scales[:, c0:c0 + n],
+                in_=src.rearrange("p n t -> p (n t)"),
+            )
+
+        def turn_bank(blocks, eng, dst):
+            bank = ps_tr.tile([P, 2, 2, P], F32, name="bank")
+            for i in range(2):
+                for u in range(2):
+                    nc.tensor.transpose(bank[:, i, u, :], blocks[i][:, u:256:2], ident[:])
+            copy(eng, dst.bitcast(F32).rearrange("p (i n) u -> p i n u", i=2), bank[:].rearrange("p i u n -> p i n u"))
+
+        steps = [(c, g) for g in range(2) for c in range(3)]
+        gate_t, attn_t, grad_t, wo_t, x_t, wq_t = {}, {}, {}, {}, {}, {}
+        gcod, wocod, wqcod, xcod, dzec, dztc, dz_t, grp = {}, {}, {}, {}, {}, {}, {}, {}
+
+        def load_ew(s, parts=1):
+            c, g = steps[s]
+            ec = slice(W * c, W * c + W)
+            gt = ewp.tile([P, 4, W], F32, name="gt", align_bytes=64)
+            at = ewp.tile([P, 4, W], BF16, name="at", align_bytes=64)
+            n = 4 // parts
+            for i in range(parts):
+                nc.sync.dma_start(out=gt[:, n * i:n * i + n, :], in_=ga_v[g][:, n * i:n * i + n, ec])
+            nc.sync.dma_start(out=at[:], in_=at_v[g][:, :, ec])
+            gate_t[s], attn_t[s] = gt, at
+
+        def load_grad(g):
+            gr = raw.tile([P, 4, M], BF16, name="gr", align_bytes=64)
+            for i in range(2):
+                nc.sync.dma_start(out=gr[:, 2 * i:2 * i + 2, :], in_=g_v[g][:, 2 * i:2 * i + 2, :])
+            grad_t[g] = gr
+
+        def load_wo(c):
+            t = raw.tile([P, 4, M], BF16, name="wor", align_bytes=64)
+            for i in range(2):
+                nc.sync.dma_start(out=t[:, 2 * i:2 * i + 2, :], in_=wo_v[c][:, 2 * i:2 * i + 2, :])
+            wo_t[c] = t
+
+        def load_wq(r):
+            t = raw.tile([P, 2, E], BF16, name="wqr", align_bytes=64)
+            nc.sync.dma_start(out=t[:], in_=wq_v[r])
+            wq_t[r] = t
+
+        def load_x(g):
+            t = mid.tile([P, 4, M], BF16, name="xr", align_bytes=64)
+            nc.sync.dma_start(out=t[:], in_=x_v[g])
+            x_t[g] = t
+
+        def ew(s):
+            gt, at = gate_t[s], attn_t[s]
+
+            def act(i, func):
+                js = slice(2 * i, 2 * i + 2)
+                sc = 0.5 if func == ACT.Tanh else 1.0
+                return lambda: nc.scalar.activation(out=gt[:, js, :], in_=gt[:, js, :], func=func, scale=sc)
+
+            def wgt(i):
+                js = slice(2 * i, 2 * i + 2)
+                return lambda: nc.vector.scalar_tensor_tensor(
+                    out=gt[:, js, :], in0=gt[:, js, :], scalar=1.0, in1=at[:, js, :], op0=ALU.subtract, op1=ALU.mult)
+
+            return [act(0, ACT.Tanh), act(0, ACT.Square), act(1, ACT.Tanh), wgt(0), act(1, ACT.Square), wgt(1)]
+
+        def prep(kind, raw_t, cods, key, fmt, engs):
+            words = raw_t[:].bitcast(F32)
+
+            def start():
+                for h in range(2):
+                    cods[key, h] = new_codes(keep, W, "%s%d%d" % (kind, key, h))
+                    grp[kind, key, h] = stage.tile([P, W, 4], BF16, name="grouped", align_bytes=64)
+
+            def unit(h, pair, eng):
+                return lambda: turn_bank([words[:, 2 * pair + i, 256 * h:256 * h + 256] for i in range(2)], eng,
+                                         grp[kind, key, h][:, 256 * pair:256 * pair + 256, :])
+
+            def q(h):
+                return lambda: quantize(cods[key, h], 0, fmt, grp[kind, key, h][:])
+
+            def first():
+                start()
+                unit(0, 0, engs[0])()
+
+            return [first, unit(1, 0, engs[1]), unit(0, 1, engs[2]), unit(1, 1, engs[3]), q(0), q(1)]
+
+        def prep_wq(r, engs):
+            words = wq_t[r][:].bitcast(F32)
+            n, o = r // 2, 256 * (r % 2)
+
+            def unit(c):
+                def run():
+                    if r % 2 == 0:
+                        wqcod[c, n] = new_codes(keep, W, "wq%d%d" % (c, n))
+                        grp["q", c, n] = stageq.tile([P, W, 4], BF16, name="gq%d" % c, align_bytes=64)
+                    turn_bank([words[:, i, 256 * c:256 * c + 256] for i in range(2)], engs[c],
+                              grp["q", c, n][:, o:o + 256, :])
+                return run
+
+            def q(c):
+                return lambda: quantize(wqcod[c, n], 0, E4M3, grp["q", c, n][:])
+
+            units = [unit(c) for c in range(3)]
+            if r % 2 == 1:
+                units = [units[0], units[1], q(0), units[2], q(1), q(2)]
+            return units
+
+        def interleave(dst, src):
+            nc.vector.tensor_copy(out=dst.rearrange("p (c i) t -> p c t i", i=4),
+                                  in_=src.rearrange("p t (c i) -> p c t i", i=4))
+
+        def prep_x(g):
+            xcod[g] = new_codes(keep, M, "x%d" % g)
+            gx = {}
+
+            def il(i):
+                def run():
+                    gx[i] = stage.tile([P, W, 4], BF16, name="grouped", align_bytes=64)
+                    interleave(gx[i][:], x_t[g][:, :, W * i:W * i + W])
+                return run
+
+            def q(i):
+                return lambda: quantize(xcod[g], W * i, E4M3, gx[i][:])
+
+            return [il(0), il(1), q(0), q(1)]
+
+        def dg(s):
+            c, g = steps[s]
+            dz_t[s] = mid.tile([P, 4, W], BF16, name="dz", align_bytes=64)
+
+            def unit(j):
+                def run():
+                    acc = ps_dg.tile([P, W], F32, name="acc")
+                    for h in range(2):
+                        gc, gs = gcod[g, h]
+                        wc, ws = wocod[c, h]
+                        js = slice(P * j, P * j + P)
+                        nc.tensor.matmul_mx(out=acc[:], lhsT=gc[:, js].bitcast(E5M2), lhsT_scale=gs[:, js],
+                                            rhs=wc[:].bitcast(E4M3), rhs_scale=ws[:], start=h == 0, stop=h == 1)
+                    nc.vector.scalar_tensor_tensor(out=dz_t[s][:, j, :], in0=acc[:], scalar=-0.25,
+                                                   in1=gate_t[s][:, j, :], op0=ALU.mult, op1=ALU.mult)
+                return run
+
+            return [unit(j) for j in range(4)]
+
+        def roads(s, engs):
+            c, g = steps[s]
+            words = dz_t[s][:].bitcast(F32)
+            dzec[c, g] = new_codes(keep, W, "dze%d%d" % (c, g))
+            dztc[c, g] = new_codes(keep, W, "dzt%d%d" % (c, g))
+            ge = stage.tile([P, W, 4], BF16, name="grouped", align_bytes=64)
+            gtok = stage.tile([P, W, 4], BF16, name="grouped", align_bytes=64)
+
+            def unit(pair):
+                return lambda: turn_bank([words[:, 2 * pair + i, :] for i in range(2)], engs[pair],
+                                         ge[:, 256 * pair:256 * pair + 256, :])
+
+            il = [lambda: interleave(gtok[:], dz_t[s][:])]
+            qe = [lambda: quantize(dzec[c, g], 0, E5M2, ge[:])]
+            qt = [lambda: quantize(dztc[c, g], 0, E5M2, gtok[:])]
+            return [unit(0), unit(1)], il, qe, qt
+
+        def dw(c, engs):
+            def unit(t):
+                def run():
+                    acc = ps_out.tile([P, W], F32, name="oacc")
+                    ms = slice(P * t, P * t + P)
+                    for g in range(2):
+                        xc, xs = xcod[g]
+                        zc, zs = dztc[c, g]
+                        nc.tensor.matmul_mx(out=acc[:], lhsT=xc[:, ms].bitcast(E4M3), lhsT_scale=xs[:, ms],
+                                            rhs=zc[:].bitcast(E5M2), rhs_scale=zs[:], start=g == 0, stop=g == 1)
+                    o = outp.tile([P, W], F32, name="dwo")
+                    copy(engs[t], o[:], acc[:])
+                    nc.sync.dma_start(out=dw_v[t][:, W * c:W * c + W], in_=o[:])
+                return run
+            return [unit(t) for t in range(8)]
+
+        def dx(g, engs, pools="o"):
+            acc = {}
+
+            def passes(j, n, cs):
+                js = slice(P * j, P * j + P)
+                for c in cs:
+                    zc, zs = dzec[c, g]
+                    qc, qs = wqcod[c, n]
+                    nc.tensor.matmul_mx(out=acc[j, n][:], lhsT=zc[:, js].bitcast(E5M2), lhsT_scale=zs[:, js],
+                                        rhs=qc[:].bitcast(E4M3), rhs_scale=qs[:], start=c == 0, stop=c == 2)
+
+            def begin(j, n, where):
+                def run():
+                    if where == "o":
+                        acc[j, n] = ps_out.tile([P, W], F32, name="oacc")
+                    else:
+                        acc[j, n] = ps_dg.tile([P, W], F32, name="acc")
+                    passes(j, n, [0, 1])
+                return run
+
+            def finish(j, n):
+                def run():
+                    passes(j, n, [2])
+                    o = outp.tile([P, W], F32, name="dwo")
+                    copy(engs[2 * j + n], o[:], acc[j, n][:])
+                    nc.sync.dma_start(out=dx_v[g, j][:, W * n:W * n + W], in_=o[:])
+                return run
+
+            def both(b, f):
+                def run():
+                    b()
+                    f()
+                return run
+
+            jn = [(j, n) for j in range(4) for n in range(2)]
+            bs = [begin(j, n, pools[i % len(pools)]) for i, (j, n) in enumerate(jn)]
+            fs = [finish(j, n) for j, n in jn]
+            return bs, fs, [both(b, f) for b, f in zip(bs, fs)]
+
+        def weave(main, fill):
+            out, k = [], 0
+            for i, f in enumerate(main):
+                out.append(f)
+                want = (i + 1) * len(fill) // len(main)
+                out += fill[k:want]
+                k = want
+            return out
+
+        def run(units):
+            for f in units:
+                f()
+
+        def step(s, early, fill, k, road_engs, nxt):
+            d = dg(s)
+            n = ew(nxt) if nxt is not None else []
+            run(weave(d, early + n[:2]))
+            run(fill[:k])
+            tr, il, qe, qt = roads(s, road_engs)
+            run(tr[:1] + il + tr[1:])
+            rest = weave(fill[k:], n[2:]) if len(fill) > k else n[2:]
+            cut = min(2, len(rest))
+            run(rest[:cut] + qt + qe + rest[cut:])
+
+        for once in range(1):
+            load_ew(0, 2)
+            load_grad(0)
+            load_wo(0)
+            load_ew(1)
+            load_wo(1)
+            load_wq(0)
+            load_x(0)
+            load_ew(2)
+            run(ew(0))
+            run(prep("g", grad_t[0], gcod, 0, E5M2, "VVVV"))
+            run(prep("w", wo_t[0], wocod, 0, E4M3, "SVSV"))
+            load_wo(2)
+            load_wq(1)
+            step(0, [], prep("w", wo_t[1], wocod, 1, E4M3, "SSSS") + prep_wq(0, "SSS") + prep_x(0), 3, "SS", 1)
+            load_grad(1)
+            load_wq(2)
+            load_ew(3)
+            step(1, [], prep("w", wo_t[2], wocod, 2, E4M3, "SSSS") + prep_wq(1, "SSS"), 3, "SS", 2)
+            load_wq(3)
+            load_x(1)
+            load_ew(4)
+            step(2, [], prep("g", grad_t[1], gcod, 1, E5M2, "SSSS") + prep_wq(2, "SVS"), 3, "SS", 3)
+            load_ew(5)
+            x0 = dx(0, "SSSSSSSS")[2]
+            step(3, [], prep_wq(3, "SSS") + prep_x(1) + x0[:6], 3, "SS", 4)
+            w0 = dw(0, "SSSSSSSS")
+            step(4, [], x0[6:] + w0[:6], 3, "SS", 5)
+            w1 = dw(1, "SSSVSSSV")
+            xb, xf, x1 = dx(1, "SVSVSVSV", "ooodd")
+            step(5, [], w0[6:] + w1 + xb[:3], 3, "SV", None)
+            w2 = dw(2, "SVSVSVSV")
+            run(xf[:3] + weave(x1[3:], w2))

@@ -18,35 +18,46 @@ ACT = mybir.ActivationFunctionType
 
 P = 128
 W = 512
+BANKS = 8
 
 
 def tile_qwen3_5attention_pb_v_kernel(tc, hidden, wq, attn, wo, gate, gout, dx_out, dw_out):
     nc = tc.nc
-    x_v = hidden.rearrange("b s m -> (b s) m").rearrange("(g p j) m -> g p j m", g=2, j=4)
-    g_v = gout.rearrange("b s m -> (b s) m").rearrange("(g p j) m -> g p j m", g=2, j=4)
-    wq_v = wq.rearrange("m u h -> m (u h)").rearrange("(r b q) e -> r q b e", r=4, q=P)
-    wo_v = wo.rearrange("u h m -> (u h) m").rearrange("(c b q) m -> c q b m", c=3, q=P)
+    x_v = hidden.rearrange("b s m -> (b s) m").rearrange("(g p j) m -> g p (j m)", g=2, j=4)
+    g_v = gout.rearrange("b s m -> (b s) m").rearrange("(g p a i) m -> g a p (i m)", g=2, a=2, i=2)
+    wo_v = wo.rearrange("u h m -> (u h) m").rearrange("(c p a i) m -> c a p (i m)", c=3, a=2, i=2)
+    wq_v = wq.rearrange("m u h -> m (u h)").rearrange("(r p i) e -> r p (i e)", r=4, i=2)
     at_v = attn.rearrange("b s u h -> (b s) (u h)").rearrange("(g p j) e -> g p j e", g=2, j=4)
     ga_v = gate.rearrange("b s u h -> (b s) (u h)").rearrange("(g p j) e -> g p j e", g=2, j=4)
     dx_v = dx_out.rearrange("b s m -> (b s) m").rearrange("(g p j) m -> g j p m", g=2, j=4)
-    dw_v = dw_out.rearrange("m u h -> m (u h)").rearrange("(t q) e -> t q e", q=P)
+    dw_v = dw_out.rearrange("m u h -> m (u h)").rearrange("(t i q) e -> t q i e", i=2, q=P)
 
     with ExitStack() as ctx:
-        keep = ctx.enter_context(tc.tile_pool(name="keep", bufs=1))
-        raw = ctx.enter_context(tc.tile_pool(name="raw", bufs=2))
-        ewp = ctx.enter_context(tc.tile_pool(name="ewp", bufs=3))
-        stage = ctx.enter_context(tc.tile_pool(name="stage", bufs=4))
-        stageq = ctx.enter_context(tc.tile_pool(name="stageq", bufs=1))
-        stagex = ctx.enter_context(tc.tile_pool(name="stagex", bufs=2))
-        mid = ctx.enter_context(tc.tile_pool(name="mid", bufs=2))
-        rot = ctx.enter_context(tc.tile_pool(name="rot", bufs=4))
-        outp = ctx.enter_context(tc.tile_pool(name="outp", bufs=6))
-        ps_dg = ctx.enter_context(tc.psum_pool(name="ps_dg", bufs=2))
-        ps_tr = ctx.enter_context(tc.psum_pool(name="ps_tr", bufs=3))
-        ps_out = ctx.enter_context(tc.psum_pool(name="ps_out", bufs=3))
+        sb = ctx.enter_context(tc.tile_pool(name="sb", bufs=1))
+        ps = ctx.enter_context(tc.psum_pool(name="ps", bufs=1))
+        ctx.enter_context(tc.manual_schedule())
 
-        ident = keep.tile([P, P], F32, name="ident")
+        ident = sb.tile([P, P], F32, name="ident")
         make_identity(nc, ident[:])
+
+        steps = [(c, g) for g in range(2) for c in range(3)]
+        tiles = {}
+        work = {}
+        users = {}
+        ring = {}
+
+        def unit(name, needs, uses, fn):
+            work[name] = (needs, uses, fn)
+            for t in uses:
+                users.setdefault(t, []).append(name)
+
+        def decl(key, shape, dtype, kind, depth):
+            ring[key] = (shape, dtype, kind, depth)
+
+        def codes(key, cols):
+            decl((key, "c"), [P, cols], U32, "%s_c" % (key,), 1)
+            decl((key, "s"), [P, cols], U8, "%s_s" % (key,), 1)
+            return [(key, "c"), (key, "s")]
 
         def copy(eng, out, in_):
             if eng == "S":
@@ -54,230 +65,213 @@ def tile_qwen3_5attention_pb_v_kernel(tc, hidden, wq, attn, wo, gate, gout, dx_o
             else:
                 nc.vector.tensor_copy(out=out, in_=in_)
 
-        def new_codes(pool, cols, tag):
-            codes = pool.tile([P, cols], U32, name=tag + "_c", align_bytes=64)
-            scales = pool.tile([P, cols], U8, name=tag + "_s", align_bytes=64)
-            return codes, scales
+        def negate(eng, out, in_):
+            if eng == "S":
+                nc.scalar.activation(out=out, in_=in_, func=ACT.Copy, scale=-1.0)
+            else:
+                nc.vector.tensor_scalar(out=out, in0=in_, scalar1=-1.0, scalar2=None, op0=ALU.mult)
 
-        def quantize(cs, c0, fmt, src):
-            codes, scales = cs
-            n = src.shape[1]
-            nc.vector.quantize_mx(
-                out=codes[:, c0:c0 + n].bitcast(fmt),
-                scales=scales[:, c0:c0 + n],
-                in_=src.rearrange("p n t -> p (n t)"),
-            )
+        def quantize(key, c0, fmt, src):
+            n = src.shape[1] // 4
+            nc.vector.quantize_mx(out=tiles[key, "c"][:, c0:c0 + n].bitcast(fmt), scales=tiles[key, "s"][:, c0:c0 + n], in_=src)
 
-        def turn_bank(blocks, eng, dst):
-            bank = ps_tr.tile([P, 2, 2, P], F32, name="bank")
+        def mx(acc, a, a0, afmt, b, b0, bfmt, start, stop):
+            nc.tensor.matmul_mx(out=acc, lhsT=tiles[a, "c"][:, a0:a0 + P].bitcast(afmt), lhsT_scale=tiles[a, "s"][:, a0:a0 + P],
+                                rhs=tiles[b, "c"][:, b0:b0 + W].bitcast(bfmt), rhs_scale=tiles[b, "s"][:, b0:b0 + W],
+                                start=start, stop=stop)
+
+        def load(name, key, src):
+            unit(name, [], [key], lambda eng: nc.sync.dma_start(out=tiles[key][:], in_=src))
+
+        def turn(name, raw, row, w0, step, drain, dst, d0, pattern, needs):
+            bank = ("bank", name)
+            decl(bank, [P, W], F32, "bank", BANKS)
+
+            def pe(eng):
+                words = tiles[raw][:].bitcast(F32)
+                for i in range(2):
+                    for u in range(2):
+                        if step == 2:
+                            src = words[:, row * i + w0 + u:row * i + w0 + 256:2]
+                        else:
+                            src = words[:, row * i + w0 + P * u:row * i + w0 + P * u + P]
+                        nc.tensor.transpose(tiles[bank][:, 256 * i + P * u:256 * i + P * u + P], src, ident[:])
+
+            def out(eng):
+                to = tiles[dst][:, d0:d0 + 1024].bitcast(F32)
+                if pattern == "i n u":
+                    copy(eng, to.rearrange("p (i n u) -> p i n u", i=2, u=2), tiles[bank][:].rearrange("p (i u n) -> p i n u", i=2, u=2))
+                else:
+                    copy(eng, to.rearrange("p (n i u) -> p n i u", i=2, u=2), tiles[bank][:].rearrange("p (i u n) -> p n i u", i=2, u=2))
+
+            unit(name, needs, [raw, bank], pe)
+            unit(drain, [name], [bank, dst], out)
+
+        def interleave(eng, dst, src):
+            nc.vector.tensor_copy(out=dst.rearrange("p (c i t) -> p c t i", i=4, t=4), in_=src.rearrange("p t (c i) -> p c t i", i=4))
+
+        for g in range(2):
+            gk = "g%d" % g
+            cs = codes(gk, 1024)
+            for a in range(2):
+                raw, stg = ("graw", g, a), ("gstg", g, a)
+                decl(raw, [P, 2048], BF16, "raw", 6)
+                decl(stg, [P, 2048], BF16, "stage", 4)
+                load(("LG", g, a), raw, g_v[g, a])
+                for h in range(2):
+                    turn(("TG", g, a, h), raw, 512, 256 * h, 2, ("CG", g, a, h), stg, 1024 * h, "i n u", [("LG", g, a)])
+                unit(("QG", g, a), [("CG", g, a, 0), ("CG", g, a, 1)], [stg] + cs,
+                     lambda eng, gk=gk, a=a, stg=stg: quantize(gk, W * a, E5M2, tiles[stg][:]))
+        for c in range(3):
+            wk = "w%d" % c
+            cs = codes(wk, 1024)
+            for h in range(2):
+                decl(("wstg", c, h), [P, 2048], BF16, "stage", 4)
+            for a in range(2):
+                raw = ("wraw", c, a)
+                decl(raw, [P, 2048], BF16, "raw", 6)
+                load(("LW", c, a), raw, wo_v[c, a])
+                for h in range(2):
+                    turn(("TW", c, a, h), raw, 512, 256 * h, 2, ("CW", c, a, h), ("wstg", c, h), 1024 * a, "n i u", [("LW", c, a)])
+            for h in range(2):
+                unit(("QW", c, h), [("CW", c, 0, h), ("CW", c, 1, h)], [("wstg", c, h)] + cs,
+                     lambda eng, wk=wk, c=c, h=h: quantize(wk, W * h, E4M3, tiles["wstg", c, h][:]))
+        for n in range(2):
+            qk = "q%d" % n
+            cs = codes(qk, 1536)
+            for c in range(3):
+                decl(("qstg", n, c), [P, 2048], BF16, "qstage", 3)
+            for r in (2 * n, 2 * n + 1):
+                raw = ("qraw", r)
+                decl(raw, [P, 3072], BF16, "qraw", 2)
+                load(("LQ", r), raw, wq_v[r])
+                for c in range(3):
+                    turn(("TQ", r, c), raw, 768, 256 * c, 2, ("CQ", r, c), ("qstg", n, c), 1024 * (r % 2), "n i u", [("LQ", r)])
+            for c in range(3):
+                unit(("QQ", n, c), [("CQ", 2 * n, c), ("CQ", 2 * n + 1, c)], [("qstg", n, c)] + cs,
+                     lambda eng, qk=qk, n=n, c=c: quantize(qk, W * c, E4M3, tiles["qstg", n, c][:]))
+        for g in range(2):
+            xk = "x%d" % g
+            cs = codes(xk, 1024)
+            raw = ("xraw", g)
+            decl(raw, [P, 4096], BF16, "xraw", 2)
+            load(("LX", g), raw, x_v[g])
             for i in range(2):
-                for u in range(2):
-                    nc.tensor.transpose(bank[:, i, u, :], blocks[i][:, u:256:2], ident[:])
-            copy(eng, dst.bitcast(F32).rearrange("p (i n) u -> p i n u", i=2), bank[:].rearrange("p i u n -> p i n u"))
+                stg = ("xstg", g, i)
+                decl(stg, [P, 2048], BF16, "tstage", 2)
+                unit(("IX", g, i), [("LX", g)], [raw, stg],
+                     lambda eng, raw=raw, stg=stg, i=i: interleave(eng, tiles[stg][:], tiles[raw][:].rearrange("p (t m) -> p t m", t=4)[:, :, W * i:W * i + W]))
+                unit(("QX", g, i), [("IX", g, i)], [stg] + cs,
+                     lambda eng, xk=xk, stg=stg, i=i: quantize(xk, W * i, E4M3, tiles[stg][:]))
 
-        steps = [(c, g) for g in range(2) for c in range(3)]
-        gate_t, attn_t, grad_t, wo_t, x_t, wq_t = {}, {}, {}, {}, {}, {}
-        gcod, wocod, wqcod, xcod, dzec, dztc, dz_t, grp = {}, {}, {}, {}, {}, {}, {}, {}
-
-        def load_ew(s, parts=1):
+        def step_units(s):
             c, g = steps[s]
             ec = slice(W * c, W * c + W)
-            gt = ewp.tile([P, 4, W], F32, name="gt", align_bytes=64)
-            at = ewp.tile([P, 4, W], BF16, name="at", align_bytes=64)
-            n = 4 // parts
-            for i in range(parts):
-                nc.sync.dma_start(out=gt[:, n * i:n * i + n, :], in_=ga_v[g][:, n * i:n * i + n, ec])
-            nc.sync.dma_start(out=at[:], in_=at_v[g][:, :, ec])
-            gate_t[s], attn_t[s] = gt, at
+            at, dz, ge, gt = ("attn", s), ("dz", s), ("ge", s), ("gt", s)
+            decl(at, [P, 2048], BF16, "attn", 3)
+            decl(dz, [P, 2048], BF16, "dz", 2)
+            decl(ge, [P, 2048], BF16, "estage", 2)
+            decl(gt, [P, 2048], BF16, "tstage", 2)
+            ek, tk = "e%d" % s, "t%d" % s
+            ecs, tcs = codes(ek, W), codes(tk, W)
+            unit(("LA", s), [], [at], lambda eng: nc.sync.dma_start(out=tiles[at][:].rearrange("p (j e) -> p j e", j=4), in_=at_v[g][:, :, ec]))
 
-        def load_grad(g):
-            gr = raw.tile([P, 4, M], BF16, name="gr", align_bytes=64)
-            for i in range(2):
-                nc.sync.dma_start(out=gr[:, 2 * i:2 * i + 2, :], in_=g_v[g][:, 2 * i:2 * i + 2, :])
-            grad_t[g] = gr
+            def half(a):
+                ga = ("gate", s, a)
+                decl(ga, [P, 1024], F32, "gate", 2 * 3)
+                unit(("LE", s, a), [], [ga],
+                     lambda eng: nc.sync.dma_start(out=tiles[ga][:].rearrange("p (j e) -> p j e", j=2), in_=ga_v[g][:, 2 * a:2 * a + 2, ec]))
+                unit(("TH", s, a), [("LE", s, a)], [ga],
+                     lambda eng: nc.scalar.activation(out=tiles[ga][:], in_=tiles[ga][:], func=ACT.Tanh, scale=0.5))
+                unit(("SQ", s, a), [("TH", s, a)], [ga],
+                     lambda eng: nc.scalar.activation(out=tiles[ga][:], in_=tiles[ga][:], func=ACT.Square, scale=0.5))
+                unit(("WM", s, a), [("SQ", s, a), ("LA", s)], [ga, at],
+                     lambda eng: nc.vector.scalar_tensor_tensor(out=tiles[ga][:], in0=tiles[ga][:], scalar=0.25, in1=tiles[at][:, 1024 * a:1024 * a + 1024],
+                                                                op0=ALU.subtract, op1=ALU.mult))
+                turn(("TZ", s, a), dz, 256, W * a, 1, ("CZ", s, a), ge, 1024 * a, "i n u", [("DZ", s, 2 * a), ("DZ", s, 2 * a + 1)])
+                unit(("QE", s, a), [("CZ", s, a)], [ge] + ecs, lambda eng: quantize(ek, 256 * a, E5M2, tiles[ge][:, 1024 * a:1024 * a + 1024]))
 
-        def load_wo(c):
-            t = raw.tile([P, 4, M], BF16, name="wor", align_bytes=64)
-            for i in range(2):
-                nc.sync.dma_start(out=t[:, 2 * i:2 * i + 2, :], in_=wo_v[c][:, 2 * i:2 * i + 2, :])
-            wo_t[c] = t
+            def slot(j):
+                bank = ("bank", "DG", s, j)
+                ga = ("gate", s, j // 2)
+                decl(bank, [P, W], F32, "bank", BANKS)
 
-        def load_wq(r):
-            t = raw.tile([P, 2, E], BF16, name="wqr", align_bytes=64)
-            nc.sync.dma_start(out=t[:], in_=wq_v[r])
-            wq_t[r] = t
-
-        def load_x(g):
-            t = mid.tile([P, 4, M], BF16, name="xr", align_bytes=64)
-            nc.sync.dma_start(out=t[:], in_=x_v[g])
-            x_t[g] = t
-
-        def ew(s):
-            gt, at = gate_t[s], attn_t[s]
-
-            def act(i, func):
-                js = slice(2 * i, 2 * i + 2)
-                sc = 0.5 if func == ACT.Tanh else 1.0
-                return lambda: nc.scalar.activation(out=gt[:, js, :], in_=gt[:, js, :], func=func, scale=sc)
-
-            def wgt(i):
-                js = slice(2 * i, 2 * i + 2)
-                return lambda: nc.vector.scalar_tensor_tensor(
-                    out=gt[:, js, :], in0=gt[:, js, :], scalar=1.0, in1=at[:, js, :], op0=ALU.subtract, op1=ALU.mult)
-
-            return [act(0, ACT.Tanh), act(0, ACT.Square), act(1, ACT.Tanh), wgt(0), act(1, ACT.Square), wgt(1)]
-
-        def prep(kind, raw_t, cods, key, fmt, engs):
-            words = raw_t[:].bitcast(F32)
-
-            def start():
-                for h in range(2):
-                    cods[key, h] = new_codes(keep, W, "%s%d%d" % (kind, key, h))
-                    grp[kind, key, h] = stage.tile([P, W, 4], BF16, name="grouped", align_bytes=64)
-
-            def unit(h, pair, eng):
-                return lambda: turn_bank([words[:, 2 * pair + i, 256 * h:256 * h + 256] for i in range(2)], eng,
-                                         grp[kind, key, h][:, 256 * pair:256 * pair + 256, :])
-
-            def q(h):
-                return lambda: quantize(cods[key, h], 0, fmt, grp[kind, key, h][:])
-
-            def first():
-                start()
-                unit(0, 0, engs[0])()
-
-            return [first, unit(1, 0, engs[1]), unit(0, 1, engs[2]), unit(1, 1, engs[3]), q(0), q(1)]
-
-        def prep_wq(r, engs):
-            words = wq_t[r][:].bitcast(F32)
-            n, o = r // 2, 256 * (r % 2)
-
-            def unit(c):
-                def run():
-                    if r % 2 == 0:
-                        wqcod[c, n] = new_codes(keep, W, "wq%d%d" % (c, n))
-                        grp["q", c, n] = stageq.tile([P, W, 4], BF16, name="gq%d" % c, align_bytes=64)
-                    turn_bank([words[:, i, 256 * c:256 * c + 256] for i in range(2)], engs[c],
-                              grp["q", c, n][:, o:o + 256, :])
-                return run
-
-            def q(c):
-                return lambda: quantize(wqcod[c, n], 0, E4M3, grp["q", c, n][:])
-
-            units = [unit(c) for c in range(3)]
-            if r % 2 == 1:
-                units = [units[0], units[1], q(0), units[2], q(1), q(2)]
-            return units
-
-        def interleave(dst, src):
-            nc.vector.tensor_copy(out=dst.rearrange("p (c i) t -> p c t i", i=4),
-                                  in_=src.rearrange("p t (c i) -> p c t i", i=4))
-
-        def prep_x(g):
-            xcod[g] = new_codes(keep, M, "x%d" % g)
-            gx = {}
-
-            def il(i):
-                def run():
-                    gx[i] = stage.tile([P, W, 4], BF16, name="grouped", align_bytes=64)
-                    interleave(gx[i][:], x_t[g][:, :, W * i:W * i + W])
-                return run
-
-            def q(i):
-                return lambda: quantize(xcod[g], W * i, E4M3, gx[i][:])
-
-            return [il(0), il(1), q(0), q(1)]
-
-        def dg(s):
-            c, g = steps[s]
-            dz_t[s] = mid.tile([P, 4, W], BF16, name="dz", align_bytes=64)
-
-            def unit(j):
-                def run():
-                    acc = ps_dg.tile([P, W], F32, name="acc")
+                def pe(eng):
                     for h in range(2):
-                        gc, gs = gcod[g, h]
-                        wc, ws = wocod[c, h]
-                        js = slice(P * j, P * j + P)
-                        nc.tensor.matmul_mx(out=acc[:], lhsT=gc[:, js].bitcast(E5M2), lhsT_scale=gs[:, js],
-                                            rhs=wc[:].bitcast(E4M3), rhs_scale=ws[:], start=h == 0, stop=h == 1)
-                    nc.vector.scalar_tensor_tensor(out=dz_t[s][:, j, :], in0=acc[:], scalar=-0.25,
-                                                   in1=gate_t[s][:, j, :], op0=ALU.mult, op1=ALU.mult)
-                return run
+                        mx(tiles[bank][:], "g%d" % g, W * (j // 2) + 256 * h + P * (j % 2), E5M2, "w%d" % c, W * h, E4M3, h == 0, h == 1)
 
-            return [unit(j) for j in range(4)]
+                def out(eng):
+                    nc.vector.tensor_tensor(
+                        out=tiles[dz][:, W * j:W * j + W].rearrange("p (u m i) -> p u m i", u=2, i=2),
+                        in0=tiles[bank][:].rearrange("p (u m i) -> p u m i", u=2, i=2),
+                        in1=tiles[ga][:, W * (j % 2):W * (j % 2) + W].rearrange("p (m u i) -> p u m i", u=2, i=2), op=ALU.mult)
 
-        def roads(s, engs):
-            c, g = steps[s]
-            words = dz_t[s][:].bitcast(F32)
-            dzec[c, g] = new_codes(keep, W, "dze%d%d" % (c, g))
-            dztc[c, g] = new_codes(keep, W, "dzt%d%d" % (c, g))
-            ge = stage.tile([P, W, 4], BF16, name="grouped", align_bytes=64)
-            gtok = stage.tile([P, W, 4], BF16, name="grouped", align_bytes=64)
+                unit(("DG", s, j), [("QG", g, j // 2), ("QW", c, 0), ("QW", c, 1)], [bank], pe)
+                unit(("DZ", s, j), [("DG", s, j), ("WM", s, j // 2)], [bank, dz, ga], out)
 
-            def unit(pair):
-                return lambda: turn_bank([words[:, 2 * pair + i, :] for i in range(2)], engs[pair],
-                                         ge[:, 256 * pair:256 * pair + 256, :])
+            for a in range(2):
+                half(a)
+            for j in range(4):
+                slot(j)
+            unit(("IZ", s), [("DZ", s, j) for j in range(4)], [dz, gt],
+                 lambda eng: interleave(eng, tiles[gt][:], tiles[dz][:].rearrange("p (t m) -> p t m", t=4)))
+            unit(("QT", s), [("IZ", s)], [gt] + tcs, lambda eng: quantize(tk, 0, E5M2, tiles[gt][:]))
 
-            il = [lambda: interleave(gtok[:], dz_t[s][:])]
-            qe = [lambda: quantize(dzec[c, g], 0, E5M2, ge[:])]
-            qt = [lambda: quantize(dztc[c, g], 0, E5M2, gtok[:])]
-            return [unit(0), unit(1)], il, qe, qt
+        for s in range(6):
+            step_units(s)
 
-        def dw(c, engs):
-            def unit(t):
-                def run():
-                    acc = ps_out.tile([P, W], F32, name="oacc")
-                    ms = slice(P * t, P * t + P)
-                    for g in range(2):
-                        xc, xs = xcod[g]
-                        zc, zs = dztc[c, g]
-                        nc.tensor.matmul_mx(out=acc[:], lhsT=xc[:, ms].bitcast(E4M3), lhsT_scale=xs[:, ms],
-                                            rhs=zc[:].bitcast(E5M2), rhs_scale=zs[:], start=g == 0, stop=g == 1)
-                    o = outp.tile([P, W], F32, name="dwo")
-                    copy(engs[t], o[:], acc[:])
-                    nc.sync.dma_start(out=dw_v[t][:, W * c:W * c + W], in_=o[:])
-                return run
-            return [unit(t) for t in range(8)]
+        def dx_units(g, j):
+            o = ("xo", g, j)
+            decl(o, [P, 1024], F32, "out", 4)
+            ss = [steps.index((c, g)) for c in range(3)]
 
-        def dx(g, engs, pools="o"):
-            acc = {}
+            def half(n):
+                bank = ("bank", "DX", g, j, n)
+                decl(bank, [P, W], F32, "bank", BANKS)
 
-            def passes(j, n, cs):
-                js = slice(P * j, P * j + P)
-                for c in cs:
-                    zc, zs = dzec[c, g]
-                    qc, qs = wqcod[c, n]
-                    nc.tensor.matmul_mx(out=acc[j, n][:], lhsT=zc[:, js].bitcast(E5M2), lhsT_scale=zs[:, js],
-                                        rhs=qc[:].bitcast(E4M3), rhs_scale=qs[:], start=c == 0, stop=c == 2)
+                def passes(cs):
+                    def pe(eng):
+                        for c in cs:
+                            mx(tiles[bank][:], "e%d" % ss[c], P * j, E5M2, "q%d" % n, W * c, E4M3, c == 0, c == 2)
+                    return pe
 
-            def begin(j, n, where):
-                def run():
-                    if where == "o":
-                        acc[j, n] = ps_out.tile([P, W], F32, name="oacc")
-                    else:
-                        acc[j, n] = ps_dg.tile([P, W], F32, name="acc")
-                    passes(j, n, [0, 1])
-                return run
+                unit(("DXa", g, j, n), [("QE", ss[c], j // 2) for c in range(2)] + [("QQ", n, c) for c in range(2)], [bank], passes([0, 1]))
+                unit(("DXb", g, j, n), [("DXa", g, j, n), ("QE", ss[2], j // 2), ("QQ", n, 2)], [bank], passes([2]))
+                unit(("OX", g, j, n), [("DXb", g, j, n)], [bank, o], lambda eng: negate(eng, tiles[o][:, W * n:W * n + W], tiles[bank][:]))
 
-            def finish(j, n):
-                def run():
-                    passes(j, n, [2])
-                    o = outp.tile([P, W], F32, name="dwo")
-                    copy(engs[2 * j + n], o[:], acc[j, n][:])
-                    nc.sync.dma_start(out=dx_v[g, j][:, W * n:W * n + W], in_=o[:])
-                return run
+            for n in range(2):
+                half(n)
+            unit(("SX", g, j), [("OX", g, j, 0), ("OX", g, j, 1)], [o], lambda eng: nc.sync.dma_start(out=dx_v[g, j], in_=tiles[o][:]))
 
-            def both(b, f):
-                def run():
-                    b()
-                    f()
-                return run
+        def dw_units(c, t):
+            o = ("wo", c, t)
+            decl(o, [P, 1024], F32, "out", 4)
+            ss = [steps.index((c, g)) for g in range(2)]
 
-            jn = [(j, n) for j in range(4) for n in range(2)]
-            bs = [begin(j, n, pools[i % len(pools)]) for i, (j, n) in enumerate(jn)]
-            fs = [finish(j, n) for j, n in jn]
-            return bs, fs, [both(b, f) for b, f in zip(bs, fs)]
+            def half(i):
+                bank = ("bank", "DW", c, t, i)
+                decl(bank, [P, W], F32, "bank", BANKS)
+
+                def passes(g):
+                    return lambda eng: mx(tiles[bank][:], "x%d" % g, 256 * t + P * i, E4M3, "t%d" % ss[g], 0, E5M2, g == 0, g == 1)
+
+                unit(("DWa", c, t, i), [("QT", ss[0]), ("QX", 0, t // 2)], [bank], passes(0))
+                unit(("DWb", c, t, i), [("DWa", c, t, i), ("QT", ss[1]), ("QX", 1, t // 2)], [bank], passes(1))
+                unit(("OW", c, t, i), [("DWb", c, t, i)], [bank, o],
+                     lambda eng: negate(eng, tiles[o][:, W * i:W * i + W].rearrange("p (m u i) -> p m u i", u=2, i=2),
+                                        tiles[bank][:].rearrange("p (u m i) -> p m u i", u=2, i=2)))
+
+            for i in range(2):
+                half(i)
+            unit(("SW", c, t), [("OW", c, t, 0), ("OW", c, t, 1)], [o],
+                 lambda eng: nc.sync.dma_start(out=dw_v[t][:, :, W * c:W * c + W], in_=tiles[o][:].rearrange("p (i e) -> p i e", i=2)))
+
+        for g in range(2):
+            for j in range(4):
+                dx_units(g, j)
+        for c in range(3):
+            for t in range(4):
+                dw_units(c, t)
 
         def weave(main, fill):
             out, k = [], 0
@@ -288,51 +282,136 @@ def tile_qwen3_5attention_pb_v_kernel(tc, hidden, wq, attn, wo, gate, gout, dx_o
                 k = want
             return out
 
-        def run(units):
-            for f in units:
-                f()
 
-        def step(s, early, fill, k, road_engs, nxt):
-            d = dg(s)
-            n = ew(nxt) if nxt is not None else []
-            run(weave(d, early + n[:2]))
-            run(fill[:k])
-            tr, il, qe, qt = roads(s, road_engs)
-            run(tr[:1] + il + tr[1:])
-            rest = weave(fill[k:], n[2:]) if len(fill) > k else n[2:]
-            cut = min(2, len(rest))
-            run(rest[:cut] + qt + qe + rest[cut:])
+        def tg(g, a):
+            return [("TG", g, a, h) for h in range(2)]
 
-        for once in range(1):
-            load_ew(0, 2)
-            load_grad(0)
-            load_wo(0)
-            load_ew(1)
-            load_wo(1)
-            load_wq(0)
-            load_x(0)
-            load_ew(2)
-            run(ew(0))
-            run(prep("g", grad_t[0], gcod, 0, E5M2, "VVVV"))
-            run(prep("w", wo_t[0], wocod, 0, E4M3, "SVSV"))
-            load_wo(2)
-            load_wq(1)
-            step(0, [], prep("w", wo_t[1], wocod, 1, E4M3, "SSSS") + prep_wq(0, "SSS") + prep_x(0), 3, "SS", 1)
-            load_grad(1)
-            load_wq(2)
-            load_ew(3)
-            step(1, [], prep("w", wo_t[2], wocod, 2, E4M3, "SSSS") + prep_wq(1, "SSS"), 3, "SS", 2)
-            load_wq(3)
-            load_x(1)
-            load_ew(4)
-            step(2, [], prep("g", grad_t[1], gcod, 1, E5M2, "SSSS") + prep_wq(2, "SVS"), 3, "SS", 3)
-            load_ew(5)
-            x0 = dx(0, "SSSSSSSS")[2]
-            step(3, [], prep_wq(3, "SSS") + prep_x(1) + x0[:6], 3, "SS", 4)
-            w0 = dw(0, "SSSSSSSS")
-            step(4, [], x0[6:] + w0[:6], 3, "SS", 5)
-            w1 = dw(1, "SSSVSSSV")
-            xb, xf, x1 = dx(1, "SVSVSVSV", "ooodd")
-            step(5, [], w0[6:] + w1 + xb[:3], 3, "SV", None)
-            w2 = dw(2, "SVSVSVSV")
-            run(xf[:3] + weave(x1[3:], w2))
+        def tw(c):
+            return [("TW", c, a, h) for a in range(2) for h in range(2)]
+
+        def tq(r):
+            return [("TQ", r, c) for c in range(3)]
+
+        def dx(g, part="ab"):
+            return [[("DX" + k, g, j, n) for k in part] for j in range(4) for n in range(2)]
+
+        def dw(c, part="ab"):
+            return [[("DW" + k, c, t, i) for k in part] for t in range(4) for i in range(2)]
+
+        def ew(s):
+            return [(k, s, a) for a in range(2) for k in ("TH", "SQ")]
+
+        def flat(ls):
+            return [x for l in ls for x in (l if isinstance(l, list) else [l])]
+
+        drain = {"TG": "CG", "TW": "CW", "TQ": "CQ", "TZ": "CZ", "DXb": "OX", "DWb": "OW"}
+
+        def drains(q):
+            return [(drain[n[0]],) + n[1:] for n in q if n[0] in drain]
+
+
+        def ew_loads(s):
+            return [("LE", s, 0), ("LA", s), ("LE", s, 1)]
+
+        loads = [("LG", 0, 0), ("LE", 0, 0), ("LW", 0, 0), ("LW", 0, 1), ("LA", 0), ("LG", 0, 1), ("LE", 0, 1)]
+        loads += [("LW", 1, 0), ("LW", 1, 1)] + ew_loads(1) + [("LQ", 0), ("LX", 0)]
+        loads += [("LW", 2, 0), ("LW", 2, 1)] + ew_loads(2) + [("LQ", 1)]
+        loads += [("LG", 1, 0), ("LG", 1, 1), ("LQ", 2)] + ew_loads(3) + [("LQ", 3), ("LX", 1)]
+        loads += ew_loads(4) + ew_loads(5)
+        stores = [("SX", 0, j) for j in range(4)] + [("SW", c, t) for c in range(2) for t in range(4)]
+        stores += [x for j in range(4) for x in (("SX", 1, j), ("SW", 2, j))]
+
+        def xprep(g, i):
+            return [("IX", g, i), ("QX", g, i)]
+
+        turns = tw(1) + tq(0) + tw(2) + tq(1) + tg(1, 0) + tg(1, 1) + tq(2) + tq(3)
+        fill = [turns[0:8], turns[8:16], turns[16:24], dx(0), dw(0), dw(1)]
+        qq = [[("QQ", n, c) for c in range(3)] for n in range(2)]
+        vfill = [[[], [], [("QW", 1, 0), ("QW", 1, 1)], [("IX", 0, 0)]],
+                 [[("QX", 0, 0)], [("IX", 0, 1), ("QW", 2, 0)], [("QW", 2, 1), ("QX", 0, 1)], []],
+                 [[("QG", 1, 0)] + qq[0][:1], qq[0][1:], [("QG", 1, 1)], []],
+                 [qq[1], [("IX", 1, 0), ("IX", 1, 1)], [("QX", 1, 0), ("QX", 1, 1)], []],
+                 [[], [], [], []], [[], [], [], []]]
+        share = [0, 0, 0, 0, 3, 0]
+        cuts = [0, 2, 4, 5, 8]
+        pe = tg(0, 0) + tw(0) + tg(0, 1)
+        head = drains(pe)
+        sc = ew(0)[:2] + [head[3], head[5]] + ew(0)[2:] + ew(1)[:1]
+        ve = head[:2] + [head[2], ("QG", 0, 0), head[4], ("WM", 0, 0), ("QW", 0, 0), ("QW", 0, 1), head[6], head[7], ("QG", 0, 1)]
+        acts = [a for s in range(1, 6) for a in ew(s)][1:]
+        count = 0
+        for s in range(6):
+            for j in range(4):
+                q = [("DG", s, j)]
+                f = flat(fill[s][cuts[j]:cuts[j + 1]])
+                q += f
+                if j >= 2:
+                    q += [("TZ", s, j - 2)]
+                pe += q
+                mine = []
+                for d in drains(q):
+                    count += 1
+                    if share[s] and count % share[s] == 0 and d[0] != "CZ":
+                        mine.append(d)
+                    else:
+                        sc.append(d)
+                sc += acts[4 * s + j:4 * s + j + 1]
+                ve += [("DZ", s, j)]
+                if j == 0:
+                    ve += [("WM", s, 1)]
+                    if s:
+                        ve += [("QE", s - 1, 1)]
+                if j == 3:
+                    ve += [("IZ", s), ("QE", s, 0), ("QT", s)]
+                ve += vfill[s][j] + mine
+                if j == 2 and s < 5:
+                    ve += [("WM", s + 1, 0)]
+        tail = flat(weave(dx(1), dw(2)))
+        pe += tail
+        d = drains(tail)
+        sc += d[1::2]
+        ve += [("QE", 5, 1)] + d[0::2]
+        queues = {"D": loads + stores, "P": pe, "S": sc, "V": ve}
+
+        done = set()
+        taken = {}
+        heads = {eng: 0 for eng in queues}
+
+        def ready(name):
+            needs, uses, fn = work[name]
+            if not all(n in done for n in needs):
+                return False
+            fresh = {}
+            for t in uses:
+                if t not in tiles:
+                    kind, depth = ring[t][2], ring[t][3]
+                    held = taken.setdefault(kind, [])
+                    k = len(held) + fresh.get(kind, 0)
+                    fresh[kind] = fresh.get(kind, 0) + 1
+                    if k >= depth and not all(u in done for u in users[held[k - depth]]):
+                        return False
+            return True
+
+        left = sum(len(q) for q in queues.values())
+        assert left == len(work)
+        while left:
+            moved = False
+            for eng, q in queues.items():
+                while heads[eng] < len(q) and ready(q[heads[eng]]):
+                    name = q[heads[eng]]
+                    needs, uses, fn = work[name]
+                    for t in uses:
+                        if t not in tiles:
+                            shape, dtype, kind, depth = ring[t]
+                            slot = "%s%d" % (kind, len(taken[kind]) % depth)
+                            taken[kind].append(t)
+                            if kind == "bank":
+                                tiles[t] = ps.tile(shape, dtype, name=slot)
+                            else:
+                                tiles[t] = sb.tile(shape, dtype, name=slot, align_bytes=64)
+                    fn(eng)
+                    done.add(name)
+                    heads[eng] += 1
+                    left -= 1
+                    moved = True
+            assert moved, [q[heads[e]] for e, q in queues.items() if heads[e] < len(q)]

@@ -25,7 +25,7 @@ def tile_qwen3_5attention_pb_v_kernel(tc, hidden, wq, attn, wo, gate, gout, dx_o
     nc = tc.nc
     x_v = hidden.rearrange("b s m -> (b s) m").rearrange("(g p j) m -> g p (j m)", g=2, j=4)
     g_v = gout.rearrange("b s m -> (b s) m").rearrange("(g p a i) m -> g a p (i m)", g=2, a=2, i=2)
-    wo_v = wo.rearrange("u h m -> (u h) m").rearrange("(c p a i) m -> c a p (i m)", c=3, a=2, i=2)
+    wo_v = wo.rearrange("u h m -> (u h) m").rearrange("(c a p i) m -> c a p (i m)", c=3, a=2, i=2)
     wq_v = wq.rearrange("m u h -> m (u h)").rearrange("(r p i) e -> r p (i e)", r=4, i=2)
     at_v = attn.rearrange("b s u h -> (b s) (u h)").rearrange("(g p j) e -> g p j e", g=2, j=4)
     ga_v = gate.rearrange("b s u h -> (b s) (u h)").rearrange("(g p j) e -> g p j e", g=2, j=4)
@@ -35,7 +35,7 @@ def tile_qwen3_5attention_pb_v_kernel(tc, hidden, wq, attn, wo, gate, gout, dx_o
     with ExitStack() as ctx:
         sb = ctx.enter_context(tc.tile_pool(name="sb", bufs=1))
         ps = ctx.enter_context(tc.psum_pool(name="ps", bufs=1))
-        ctx.enter_context(tc.manual_schedule())
+        ctx.enter_context(tc.manual_schedule(engines={mybir.EngineType.PE, mybir.EngineType.SP}))
 
         ident = sb.tile([P, P], F32, name="ident")
         make_identity(nc, ident[:])
@@ -64,12 +64,6 @@ def tile_qwen3_5attention_pb_v_kernel(tc, hidden, wq, attn, wo, gate, gout, dx_o
                 nc.scalar.copy(out=out, in_=in_)
             else:
                 nc.vector.tensor_copy(out=out, in_=in_)
-
-        def negate(eng, out, in_):
-            if eng == "S":
-                nc.scalar.activation(out=out, in_=in_, func=ACT.Copy, scale=-1.0)
-            else:
-                nc.vector.tensor_scalar(out=out, in0=in_, scalar1=-1.0, scalar2=None, op0=ALU.mult)
 
         def quantize(key, c0, fmt, src):
             n = src.shape[1] // 4
@@ -108,14 +102,14 @@ def tile_qwen3_5attention_pb_v_kernel(tc, hidden, wq, attn, wo, gate, gout, dx_o
             unit(drain, [name], [bank, dst], out)
 
         def interleave(eng, dst, src):
-            nc.vector.tensor_copy(out=dst.rearrange("p (c i t) -> p c t i", i=4, t=4), in_=src.rearrange("p t (c i) -> p c t i", i=4))
+            copy(eng, dst.rearrange("p (c i t) -> p c t i", i=4, t=4), src.rearrange("p t (c i) -> p c t i", i=4))
 
         for g in range(2):
             gk = "g%d" % g
             cs = codes(gk, 1024)
             for a in range(2):
                 raw, stg = ("graw", g, a), ("gstg", g, a)
-                decl(raw, [P, 2048], BF16, "raw", 6)
+                decl(raw, [P, 2048], BF16, "raw", 4)
                 decl(stg, [P, 2048], BF16, "stage", 4)
                 load(("LG", g, a), raw, g_v[g, a])
                 for h in range(2):
@@ -129,7 +123,7 @@ def tile_qwen3_5attention_pb_v_kernel(tc, hidden, wq, attn, wo, gate, gout, dx_o
                 decl(("wstg", c, h), [P, 2048], BF16, "stage", 4)
             for a in range(2):
                 raw = ("wraw", c, a)
-                decl(raw, [P, 2048], BF16, "raw", 6)
+                decl(raw, [P, 2048], BF16, "raw", 4)
                 load(("LW", c, a), raw, wo_v[c, a])
                 for h in range(2):
                     turn(("TW", c, a, h), raw, 512, 256 * h, 2, ("CW", c, a, h), ("wstg", c, h), 1024 * a, "n i u", [("LW", c, a)])
@@ -143,7 +137,7 @@ def tile_qwen3_5attention_pb_v_kernel(tc, hidden, wq, attn, wo, gate, gout, dx_o
                 decl(("qstg", n, c), [P, 2048], BF16, "qstage", 3)
             for r in (2 * n, 2 * n + 1):
                 raw = ("qraw", r)
-                decl(raw, [P, 3072], BF16, "qraw", 2)
+                decl(raw, [P, 3072], BF16, "big", 3)
                 load(("LQ", r), raw, wq_v[r])
                 for c in range(3):
                     turn(("TQ", r, c), raw, 768, 256 * c, 2, ("CQ", r, c), ("qstg", n, c), 1024 * (r % 2), "n i u", [("LQ", r)])
@@ -154,7 +148,7 @@ def tile_qwen3_5attention_pb_v_kernel(tc, hidden, wq, attn, wo, gate, gout, dx_o
             xk = "x%d" % g
             cs = codes(xk, 1024)
             raw = ("xraw", g)
-            decl(raw, [P, 4096], BF16, "xraw", 2)
+            decl(raw, [P, 4096], BF16, "xraw", 1)
             load(("LX", g), raw, x_v[g])
             for i in range(2):
                 stg = ("xstg", g, i)
@@ -169,7 +163,7 @@ def tile_qwen3_5attention_pb_v_kernel(tc, hidden, wq, attn, wo, gate, gout, dx_o
             ec = slice(W * c, W * c + W)
             at, dz, ge, gt = ("attn", s), ("dz", s), ("ge", s), ("gt", s)
             decl(at, [P, 2048], BF16, "attn", 3)
-            decl(dz, [P, 2048], BF16, "dz", 2)
+            decl(dz, [P, 2048], BF16, "dz", 4)
             decl(ge, [P, 2048], BF16, "estage", 2)
             decl(gt, [P, 2048], BF16, "tstage", 2)
             ek, tk = "e%d" % s, "t%d" % s
@@ -188,7 +182,7 @@ def tile_qwen3_5attention_pb_v_kernel(tc, hidden, wq, attn, wo, gate, gout, dx_o
                 unit(("WM", s, a), [("SQ", s, a), ("LA", s)], [ga, at],
                      lambda eng: nc.vector.scalar_tensor_tensor(out=tiles[ga][:], in0=tiles[ga][:], scalar=0.25, in1=tiles[at][:, 1024 * a:1024 * a + 1024],
                                                                 op0=ALU.subtract, op1=ALU.mult))
-                turn(("TZ", s, a), dz, 256, W * a, 1, ("CZ", s, a), ge, 1024 * a, "i n u", [("DZ", s, 2 * a), ("DZ", s, 2 * a + 1)])
+                turn(("TZ", s, a), dz, 256, W * a, 2, ("CZ", s, a), ge, 1024 * a, "i n u", [("DZ", s, 2 * a), ("DZ", s, 2 * a + 1)])
                 unit(("QE", s, a), [("CZ", s, a)], [ge] + ecs, lambda eng: quantize(ek, 256 * a, E5M2, tiles[ge][:, 1024 * a:1024 * a + 1024]))
 
             def slot(j):
@@ -201,10 +195,8 @@ def tile_qwen3_5attention_pb_v_kernel(tc, hidden, wq, attn, wo, gate, gout, dx_o
                         mx(tiles[bank][:], "g%d" % g, W * (j // 2) + 256 * h + P * (j % 2), E5M2, "w%d" % c, W * h, E4M3, h == 0, h == 1)
 
                 def out(eng):
-                    nc.vector.tensor_tensor(
-                        out=tiles[dz][:, W * j:W * j + W].rearrange("p (u m i) -> p u m i", u=2, i=2),
-                        in0=tiles[bank][:].rearrange("p (u m i) -> p u m i", u=2, i=2),
-                        in1=tiles[ga][:, W * (j % 2):W * (j % 2) + W].rearrange("p (m u i) -> p u m i", u=2, i=2), op=ALU.mult)
+                    nc.vector.scalar_tensor_tensor(out=tiles[dz][:, W * j:W * j + W], in0=tiles[bank][:], scalar=-1.0,
+                                                   in1=tiles[ga][:, W * (j % 2):W * (j % 2) + W], op0=ALU.mult, op1=ALU.mult)
 
                 unit(("DG", s, j), [("QG", g, j // 2), ("QW", c, 0), ("QW", c, 1)], [bank], pe)
                 unit(("DZ", s, j), [("DG", s, j), ("WM", s, j // 2)], [bank, dz, ga], out)
@@ -237,11 +229,16 @@ def tile_qwen3_5attention_pb_v_kernel(tc, hidden, wq, attn, wo, gate, gout, dx_o
 
                 unit(("DXa", g, j, n), [("QE", ss[c], j // 2) for c in range(2)] + [("QQ", n, c) for c in range(2)], [bank], passes([0, 1]))
                 unit(("DXb", g, j, n), [("DXa", g, j, n), ("QE", ss[2], j // 2), ("QQ", n, 2)], [bank], passes([2]))
-                unit(("OX", g, j, n), [("DXb", g, j, n)], [bank, o], lambda eng: negate(eng, tiles[o][:, W * n:W * n + W], tiles[bank][:]))
+                unit(("OX", g, j, n), [("DXb", g, j, n)], [bank, o], lambda eng: copy(eng, tiles[o][:, W * n:W * n + W], tiles[bank][:]))
 
             for n in range(2):
                 half(n)
-            unit(("SX", g, j), [("OX", g, j, 0), ("OX", g, j, 1)], [o], lambda eng: nc.sync.dma_start(out=dx_v[g, j], in_=tiles[o][:]))
+            if (g, j) != (1, 3):
+                unit(("SX", g, j), [("OX", g, j, 0), ("OX", g, j, 1)], [o], lambda eng: nc.sync.dma_start(out=dx_v[g, j], in_=tiles[o][:]))
+            else:
+                for n in range(2):
+                    unit(("SY", n), [("OX", g, j, n)], [o],
+                         lambda eng, n=n: nc.sync.dma_start(out=dx_v[g, j][:, W * n:W * n + W], in_=tiles[o][:, W * n:W * n + W]))
 
         def dw_units(c, t):
             o = ("wo", c, t)
@@ -258,8 +255,7 @@ def tile_qwen3_5attention_pb_v_kernel(tc, hidden, wq, attn, wo, gate, gout, dx_o
                 unit(("DWa", c, t, i), [("QT", ss[0]), ("QX", 0, t // 2)], [bank], passes(0))
                 unit(("DWb", c, t, i), [("DWa", c, t, i), ("QT", ss[1]), ("QX", 1, t // 2)], [bank], passes(1))
                 unit(("OW", c, t, i), [("DWb", c, t, i)], [bank, o],
-                     lambda eng: negate(eng, tiles[o][:, W * i:W * i + W].rearrange("p (m u i) -> p m u i", u=2, i=2),
-                                        tiles[bank][:].rearrange("p (u m i) -> p m u i", u=2, i=2)))
+                     lambda eng: copy(eng, tiles[o][:, W * i:W * i + W], tiles[bank][:]))
 
             for i in range(2):
                 half(i)
@@ -304,7 +300,7 @@ def tile_qwen3_5attention_pb_v_kernel(tc, hidden, wq, attn, wo, gate, gout, dx_o
         def flat(ls):
             return [x for l in ls for x in (l if isinstance(l, list) else [l])]
 
-        drain = {"TG": "CG", "TW": "CW", "TQ": "CQ", "TZ": "CZ", "DXb": "OX", "DWb": "OW"}
+        drain = {"DG": "DZ", "TG": "CG", "TW": "CW", "TQ": "CQ", "TZ": "CZ", "DXb": "OX", "DWb": "OW"}
 
         def drains(q):
             return [(drain[n[0]],) + n[1:] for n in q if n[0] in drain]
@@ -313,105 +309,112 @@ def tile_qwen3_5attention_pb_v_kernel(tc, hidden, wq, attn, wo, gate, gout, dx_o
         def ew_loads(s):
             return [("LE", s, 0), ("LA", s), ("LE", s, 1)]
 
-        loads = [("LG", 0, 0), ("LE", 0, 0), ("LW", 0, 0), ("LW", 0, 1), ("LA", 0), ("LG", 0, 1), ("LE", 0, 1)]
-        loads += [("LW", 1, 0), ("LW", 1, 1)] + ew_loads(1) + [("LQ", 0), ("LX", 0)]
-        loads += [("LW", 2, 0), ("LW", 2, 1)] + ew_loads(2) + [("LQ", 1)]
-        loads += [("LG", 1, 0), ("LG", 1, 1), ("LQ", 2)] + ew_loads(3) + [("LQ", 3), ("LX", 1)]
-        loads += ew_loads(4) + ew_loads(5)
+        def dxn(g, n):
+            return [[("DXa", g, j, n), ("DXb", g, j, n)] for j in range(4)]
+
+        def tz(s):
+            return [("TZ", s, 0), ("TZ", s, 1)]
+
+        def dg(s, *js):
+            return [("DG", s, j) for j in js]
+
+        loads = [("LG", 0, 0), ("LE", 0, 0), ("LW", 0, 0), ("LW", 0, 1), ("LX", 0), ("LA", 0), ("LG", 0, 1), ("LE", 0, 1)]
+        for s in (1, 2):
+            loads += [("LW", s, 0), ("LW", s, 1), ("LE", s, 0), ("LA", s), ("LQ", s - 1), ("LE", s, 1)]
+        for a in range(2):
+            loads += [("LG", 1, a), ("LQ", 2 + a)]
+        loads += ew_loads(3) + [("LX", 1)] + ew_loads(4) + ew_loads(5)
         stores = [("SX", 0, j) for j in range(4)] + [("SW", c, t) for c in range(2) for t in range(4)]
-        stores += [x for j in range(4) for x in (("SX", 1, j), ("SW", 2, j))]
-
-        def xprep(g, i):
-            return [("IX", g, i), ("QX", g, i)]
-
-        turns = tw(1) + tq(0) + tw(2) + tq(1) + tg(1, 0) + tg(1, 1) + tq(2) + tq(3)
-        fill = [turns[0:8], turns[8:16], turns[16:24], dx(0), dw(0), dw(1)]
-        qq = [[("QQ", n, c) for c in range(3)] for n in range(2)]
-        vfill = [[[], [], [("QW", 1, 0), ("QW", 1, 1)], [("IX", 0, 0)]],
-                 [[("QX", 0, 0)], [("IX", 0, 1), ("QW", 2, 0)], [("QW", 2, 1), ("QX", 0, 1)], []],
-                 [[("QG", 1, 0)] + qq[0][:1], qq[0][1:], [("QG", 1, 1)], []],
-                 [qq[1], [("IX", 1, 0), ("IX", 1, 1)], [("QX", 1, 0), ("QX", 1, 1)], []],
-                 [[], [], [], []], [[], [], [], []]]
-        share = [0, 0, 0, 0, 3, 0]
-        cuts = [0, 2, 4, 5, 8]
+        stores += [("SX", 1, 0), ("SX", 1, 1)] + [("SW", 2, t) for t in range(4)] + [("SX", 1, 2), ("SY", 0), ("SY", 1)]
+        x0, x1, ends = dxn(0, 0), dxn(0, 1), dx(1)
         pe = tg(0, 0) + tw(0) + tg(0, 1)
-        head = drains(pe)
-        sc = ew(0)[:2] + [head[3], head[5]] + ew(0)[2:] + ew(1)[:1]
-        ve = head[:2] + [head[2], ("QG", 0, 0), head[4], ("WM", 0, 0), ("QW", 0, 0), ("QW", 0, 1), head[6], head[7], ("QG", 0, 1)]
-        acts = [a for s in range(1, 6) for a in ew(s)][1:]
-        count = 0
+        pe += dg(0, 0) + tw(1)[:2] + dg(0, 1) + tw(1)[2:] + dg(0, 2, 3) + tq(0)
+        pe += dg(1, 0) + tw(2)[:2] + dg(1, 1) + tw(2)[2:] + dg(1, 2) + tz(0) + dg(1, 3) + tq(1)
+        pe += dg(2, 0) + tz(1) + tg(1, 0) + dg(2, 1) + tq(2) + dg(2, 2) + tz(2)[:1] + tg(1, 1) + dg(2, 3) + tq(3) + tz(2)[1:]
+        pe += x0[:2] + dg(3, 0, 1) + x0[2:] + dg(3, 2, 3) + x1 + tz(3)
+        pe += dg(4, 0, 1) + dw(0)[:2] + dg(4, 2, 3) + dw(0)[2:] + tz(4)
+        pe += dg(5, 0, 1) + dw(1)[:2] + dg(5, 2, 3) + tz(5)[:1] + dw(1)[2:] + tz(5)[1:]
+        pe += ends[:4] + dw(2) + ends[4:]
+        pe = flat(pe)
+
+        pos, count = {}, 0
+        for n in pe:
+            pos[n] = count
+            if n[0] not in ("DXa", "DWa"):
+                count += 1
+        place = {}
+        for n in pe:
+            if n[0] in drain:
+                place[(drain[n[0]],) + n[1:]] = pos[n] + 0.5
+        copies = [n for n in place if n[0] != "DZ"]
+
+        def behind(n):
+            first = max(place[m] for m in work[n][0])
+            due = min([pos[m] for m in pos if n in work[m][0]] + [len(pe)])
+            place[n] = max(first + 0.01, min(first + 1, due))
+
+        def spread(names, s):
+            first, last = pos["DG", s, 0], pos["DG", s, 3]
+            for i, n in enumerate(names):
+                place[n] = first + (last - first) * i / len(names)
+
         for s in range(6):
-            for j in range(4):
-                q = [("DG", s, j)]
-                f = flat(fill[s][cuts[j]:cuts[j + 1]])
-                q += f
-                if j >= 2:
-                    q += [("TZ", s, j - 2)]
-                pe += q
-                mine = []
-                for d in drains(q):
-                    count += 1
-                    if share[s] and count % share[s] == 0 and d[0] != "CZ":
-                        mine.append(d)
-                    else:
-                        sc.append(d)
-                sc += acts[4 * s + j:4 * s + j + 1]
-                ve += [("DZ", s, j)]
-                if j == 0:
-                    ve += [("WM", s, 1)]
-                    if s:
-                        ve += [("QE", s - 1, 1)]
-                if j == 3:
-                    ve += [("IZ", s), ("QE", s, 0), ("QT", s)]
-                ve += vfill[s][j] + mine
-                if j == 2 and s < 5:
-                    ve += [("WM", s + 1, 0)]
-        tail = flat(weave(dx(1), dw(2)))
-        pe += tail
-        d = drains(tail)
-        sc += d[1::2]
-        ve += [("QE", 5, 1)] + d[0::2]
+            for a in range(2):
+                k = pos["DG", s, 2 * a]
+                place["WM", s, a], place["SQ", s, a], place["TH", s, a] = k - 2, k - 5, k - 7
+        for n in work:
+            if n[0] in ("QG", "QW", "QQ", "QE"):
+                behind(n)
+        for g in range(2):
+            spread([(k, g, i) for i in range(2) for k in ("IX", "QX")], 3 * g)
+        for c in range(3):
+            spread([("IZ", c), ("QT", c)], c + 3)
+            place["IZ", c + 3], place["QT", c + 3] = place["DZ", c + 3, 3] + 0.1, place["DZ", c + 3, 3] + 0.2
+        busy = range(pos["DG", 0, 0], pos["TZ", 5, 1] + 1)
+        sc, ve = [], []
+        for n in sorted(place, key=lambda n: place[n]):
+            if n in copies:
+                share = 20 if int(place[n]) in busy else 2
+                (ve if copies.index(n) % share == 0 else sc).append(n)
+            else:
+                (sc if n[0] in ("TH", "SQ") else ve).append(n)
         queues = {"D": loads + stores, "P": pe, "S": sc, "V": ve}
 
-        done = set()
-        taken = {}
+        done = {}
+        last = {}
         heads = {eng: 0 for eng in queues}
+
+        def free_slot(kind, depth):
+            free = []
+            for k in range(depth):
+                held = users[last[kind, k]] if (kind, k) in last else []
+                if all(u in done for u in held):
+                    free.append((max([done[u] for u in held] + [-1]), k))
+            return min(free)[1] if free else None
 
         def ready(name):
             needs, uses, fn = work[name]
-            if not all(n in done for n in needs):
-                return False
-            fresh = {}
-            for t in uses:
-                if t not in tiles:
-                    kind, depth = ring[t][2], ring[t][3]
-                    held = taken.setdefault(kind, [])
-                    k = len(held) + fresh.get(kind, 0)
-                    fresh[kind] = fresh.get(kind, 0) + 1
-                    if k >= depth and not all(u in done for u in users[held[k - depth]]):
-                        return False
-            return True
+            return all(n in done for n in needs) and all(t in tiles or free_slot(*ring[t][2:]) is not None for t in uses)
 
         left = sum(len(q) for q in queues.values())
         assert left == len(work)
+        place.update(pos)
         while left:
-            moved = False
-            for eng, q in queues.items():
-                while heads[eng] < len(q) and ready(q[heads[eng]]):
-                    name = q[heads[eng]]
-                    needs, uses, fn = work[name]
-                    for t in uses:
-                        if t not in tiles:
-                            shape, dtype, kind, depth = ring[t]
-                            slot = "%s%d" % (kind, len(taken[kind]) % depth)
-                            taken[kind].append(t)
-                            if kind == "bank":
-                                tiles[t] = ps.tile(shape, dtype, name=slot)
-                            else:
-                                tiles[t] = sb.tile(shape, dtype, name=slot, align_bytes=64)
-                    fn(eng)
-                    done.add(name)
-                    heads[eng] += 1
-                    left -= 1
-                    moved = True
-            assert moved, [q[heads[e]] for e, q in queues.items() if heads[e] < len(q)]
+            free = [eng for eng, q in queues.items() if heads[eng] < len(q) and ready(q[heads[eng]])]
+            assert free, [q[heads[e]] for e, q in queues.items() if heads[e] < len(q)]
+            eng = min(free, key=lambda e: place.get(queues[e][heads[e]], -9))
+            name = queues[eng][heads[eng]]
+            needs, uses, fn = work[name]
+            for t in uses:
+                if t not in tiles:
+                    shape, dtype, kind, depth = ring[t]
+                    k = free_slot(kind, depth)
+                    last[kind, k] = t
+                    if kind == "bank":
+                        tiles[t] = ps.tile(shape, dtype, name="bank%d" % k)
+                    else:
+                        tiles[t] = sb.tile(shape, dtype, name="%s%d" % (kind, k), align_bytes=64)
+            fn(eng)
+            done[name] = len(done)
+            heads[eng] += 1
+            left -= 1

@@ -35,7 +35,7 @@ def tile_qwen3_5attention_pb_v_kernel(tc, hidden, wq, attn, wo, gate, gout, dx_o
     with ExitStack() as ctx:
         sb = ctx.enter_context(tc.tile_pool(name="sb", bufs=1))
         ps = ctx.enter_context(tc.psum_pool(name="ps", bufs=1))
-        ctx.enter_context(tc.manual_schedule(engines={mybir.EngineType.PE, mybir.EngineType.SP}))
+        ctx.enter_context(tc.manual_schedule(engines={mybir.EngineType.PE, mybir.EngineType.SP, mybir.EngineType.Activation}))
 
         ident = sb.tile([P, P], F32, name="ident")
         make_identity(nc, ident[:])
@@ -342,21 +342,24 @@ def tile_qwen3_5attention_pb_v_kernel(tc, hidden, wq, attn, wo, gate, gout, dx_o
             pos[n] = count
             if n[0] not in ("DXa", "DWa"):
                 count += 1
-        place = {}
+        place, source = {}, {}
         for n in pe:
             if n[0] in drain:
                 place[(drain[n[0]],) + n[1:]] = pos[n] + 0.5
+                source[(drain[n[0]],) + n[1:]] = n
         copies = [n for n in place if n[0] != "DZ"]
 
         def behind(n):
             first = max(place[m] for m in work[n][0])
             due = min([pos[m] for m in pos if n in work[m][0]] + [len(pe)])
-            place[n] = max(first + 0.01, min(first + 1, due))
+            later = [k for m, k in place.items() if m[0] == "DZ" and k > first]
+            soon = min(later) + 0.01 if later and first > pos["DG", 0, 0] else first + 0.9
+            place[n] = max(first + 0.01, min(soon, due))
 
         def spread(names, s):
             first, last = pos["DG", s, 0], pos["DG", s, 3]
             for i, n in enumerate(names):
-                place[n] = first + (last - first) * i / len(names)
+                place[n] = first + (last - first) * i / len(names) + 0.6
 
         for s in range(6):
             for a in range(2):
@@ -365,17 +368,22 @@ def tile_qwen3_5attention_pb_v_kernel(tc, hidden, wq, attn, wo, gate, gout, dx_o
         for n in work:
             if n[0] in ("QG", "QW", "QQ", "QE"):
                 behind(n)
-        for g in range(2):
-            spread([(k, g, i) for i in range(2) for k in ("IX", "QX")], 3 * g)
+        for i in range(2):
+            place["IX", 0, i], place["QX", 0, i] = pos["TG", 0, 1, i] - 0.05, pos["DG", 0, i] + 0.6
+        spread([("IX", 1, 0), ("QX", 1, 0)], 3)
+        place["IX", 1, 1], place["QX", 1, 1] = pos["TZ", 3, 0], pos["DG", 4, 0]
+        for c in range(2):
+            spread([("IZ", c), ("QT", c)], c + 1)
+        place["IZ", 2], place["QT", 2] = pos["TZ", 5, 1] + 1, pos["TZ", 5, 1] + 1.1
         for c in range(3):
-            spread([("IZ", c), ("QT", c)], c + 3)
             place["IZ", c + 3], place["QT", c + 3] = place["DZ", c + 3, 3] + 0.1, place["DZ", c + 3, 3] + 0.2
         busy = range(pos["DG", 0, 0], pos["TZ", 5, 1] + 1)
         sc, ve = [], []
         for n in sorted(place, key=lambda n: place[n]):
             if n in copies:
-                share = 20 if int(place[n]) in busy else 2
-                (ve if copies.index(n) % share == 0 else sc).append(n)
+                i, k = copies.index(n), pos[source[n]]
+                mine = i % 16 == 0 if k in busy else i % 2 == (k > busy[0])
+                (ve if mine else sc).append(n)
             else:
                 (sc if n[0] in ("TH", "SQ") else ve).append(n)
         queues = {"D": loads + stores, "P": pe, "S": sc, "V": ve}
@@ -396,25 +404,28 @@ def tile_qwen3_5attention_pb_v_kernel(tc, hidden, wq, attn, wo, gate, gout, dx_o
             needs, uses, fn = work[name]
             return all(n in done for n in needs) and all(t in tiles or free_slot(*ring[t][2:]) is not None for t in uses)
 
-        left = sum(len(q) for q in queues.values())
-        assert left == len(work)
         place.update(pos)
-        while left:
-            free = [eng for eng, q in queues.items() if heads[eng] < len(q) and ready(q[heads[eng]])]
-            assert free, [q[heads[e]] for e, q in queues.items() if heads[e] < len(q)]
-            eng = min(free, key=lambda e: place.get(queues[e][heads[e]], -9))
-            name = queues[eng][heads[eng]]
-            needs, uses, fn = work[name]
-            for t in uses:
-                if t not in tiles:
-                    shape, dtype, kind, depth = ring[t]
-                    k = free_slot(kind, depth)
-                    last[kind, k] = t
-                    if kind == "bank":
-                        tiles[t] = ps.tile(shape, dtype, name="bank%d" % k)
-                    else:
-                        tiles[t] = sb.tile(shape, dtype, name="%s%d" % (kind, k), align_bytes=64)
-            fn(eng)
-            done[name] = len(done)
-            heads[eng] += 1
-            left -= 1
+
+        def emit(finished):
+            while not finished():
+                free = [eng for eng, q in queues.items() if heads[eng] < len(q) and ready(q[heads[eng]])]
+                assert free, [q[heads[e]] for e, q in queues.items() if heads[e] < len(q)]
+                eng = min(free, key=lambda e: place.get(queues[e][heads[e]], -9))
+                name = queues[eng][heads[eng]]
+                needs, uses, fn = work[name]
+                for t in uses:
+                    if t not in tiles:
+                        shape, dtype, kind, depth = ring[t]
+                        k = free_slot(kind, depth)
+                        last[kind, k] = t
+                        if kind == "bank":
+                            tiles[t] = ps.tile(shape, dtype, name="bank%d" % k)
+                        else:
+                            tiles[t] = sb.tile(shape, dtype, name="%s%d" % (kind, k), align_bytes=64)
+                fn(eng)
+                done[name] = len(done)
+                heads[eng] += 1
+
+        with tc.manual_schedule(engines={mybir.EngineType.DVE}):
+            emit(lambda: ("DZ", 0, 1) in done)
+        emit(lambda: len(done) == len(work))

@@ -35,7 +35,7 @@ def tile_qwen3_5attention_pb_v_kernel(tc, hidden, wq, attn, wo, gate, gout, dx_o
     with ExitStack() as ctx:
         sb = ctx.enter_context(tc.tile_pool(name="sb", bufs=1))
         ps = ctx.enter_context(tc.psum_pool(name="ps", bufs=1))
-        ctx.enter_context(tc.manual_schedule(engines={mybir.EngineType.PE, mybir.EngineType.SP, mybir.EngineType.Activation}))
+        ctx.enter_context(tc.manual_schedule(engines={mybir.EngineType.PE, mybir.EngineType.SP}))
 
         ident = sb.tile([P, P], F32, name="ident")
         make_identity(nc, ident[:])
@@ -312,6 +312,13 @@ def tile_qwen3_5attention_pb_v_kernel(tc, hidden, wq, attn, wo, gate, gout, dx_o
         def dxn(g, n):
             return [[("DXa", g, j, n), ("DXb", g, j, n)] for j in range(4)]
 
+
+        def first(jobs):
+            return [j[:1] for j in jobs]
+
+        def second(jobs):
+            return [j[1:] for j in jobs]
+
         def tz(s):
             return [("TZ", s, 0), ("TZ", s, 1)]
 
@@ -328,13 +335,13 @@ def tile_qwen3_5attention_pb_v_kernel(tc, hidden, wq, attn, wo, gate, gout, dx_o
         stores += [("SX", 1, 0), ("SX", 1, 1)] + [("SW", 2, t) for t in range(4)] + [("SX", 1, 2), ("SY", 0), ("SY", 1)]
         x0, x1, ends = dxn(0, 0), dxn(0, 1), dx(1)
         pe = tg(0, 0) + tw(0) + tg(0, 1)
-        pe += dg(0, 0) + tw(1)[:2] + dg(0, 1) + tw(1)[2:] + dg(0, 2, 3) + tq(0)
+        pe += dg(0, 0, 1) + tw(1)[:2] + dg(0, 2) + tw(1)[2:] + dg(0, 3) + tq(0)
         pe += dg(1, 0) + tw(2)[:2] + dg(1, 1) + tw(2)[2:] + dg(1, 2) + tz(0) + dg(1, 3) + tq(1)
-        pe += dg(2, 0) + tz(1) + tg(1, 0) + dg(2, 1) + tq(2) + dg(2, 2) + tz(2)[:1] + tg(1, 1) + dg(2, 3) + tq(3) + tz(2)[1:]
-        pe += x0[:2] + dg(3, 0, 1) + x0[2:] + dg(3, 2, 3) + x1 + tz(3)
-        pe += dg(4, 0, 1) + dw(0)[:2] + dg(4, 2, 3) + dw(0)[2:] + tz(4)
-        pe += dg(5, 0, 1) + dw(1)[:2] + dg(5, 2, 3) + tz(5)[:1] + dw(1)[2:] + tz(5)[1:]
-        pe += ends[:4] + dw(2) + ends[4:]
+        pe += dg(2, 0) + tz(1) + tg(1, 0) + dg(2, 1) + tq(2) + dg(2, 2) + tz(2)[:1] + tg(1, 1) + dg(2, 3) + tq(3)[:2] + first(x0[:2]) + tq(3)[2:] + tz(2)[1:]
+        pe += second(x0[:2]) + dg(3, 0, 1) + x0[2:] + dg(3, 2, 3) + x1 + tz(3)
+        pe += dg(4, 0, 1) + first(dw(0)[:3]) + second(dw(0)[:3]) + dg(4, 2, 3) + dw(0)[3:] + tz(4)
+        pe += dg(5, 0, 1) + first(dw(1)[:3]) + second(dw(1)[:3]) + dg(5, 2, 3) + tz(5)[:1] + dw(1)[3:] + first(ends[:2]) + tz(5)[1:]
+        pe += second(ends[:2]) + ends[2:4] + first(dw(2)[:3]) + second(dw(2)[:3]) + dw(2)[3:] + ends[4:]
         pe = flat(pe)
 
         pos, count = {}, 0
@@ -364,7 +371,7 @@ def tile_qwen3_5attention_pb_v_kernel(tc, hidden, wq, attn, wo, gate, gout, dx_o
         for s in range(6):
             for a in range(2):
                 k = pos["DG", s, 2 * a]
-                place["WM", s, a], place["SQ", s, a], place["TH", s, a] = k - 2, k - 5, k - 7
+                place["WM", s, a], place["SQ", s, a], place["TH", s, a] = k - 3, k - 5, k - 7
         for n in work:
             if n[0] in ("QG", "QW", "QQ", "QE"):
                 behind(n)
@@ -382,7 +389,7 @@ def tile_qwen3_5attention_pb_v_kernel(tc, hidden, wq, attn, wo, gate, gout, dx_o
         for n in sorted(place, key=lambda n: place[n]):
             if n in copies:
                 i, k = copies.index(n), pos[source[n]]
-                mine = i % 16 == 0 if k in busy else i % 2 == (k > busy[0])
+                mine = i % 16 == 0 and k < pos["DG", 5, 0] if k in busy else i % 2 == (k > busy[0])
                 (ve if mine else sc).append(n)
             else:
                 (sc if n[0] in ("TH", "SQ") else ve).append(n)

@@ -18,12 +18,18 @@ ACT = mybir.ActivationFunctionType
 
 P = 128
 W = 512
-BANKS = 8
+PIN = "all"
+HV = (0, 2, 4)
+ENDING = [(0, 0), (1, 0), (0, 1), (1, 1), (0, 2), (1, 2)]
+LEAD = 2
+VSHARE = 3
+GATES = 5
+OUTS = 4
 
 
 def tile_qwen3_5attention_pb_v_kernel(tc, hidden, wq, attn, wo, gate, gout, dx_out, dw_out):
     nc = tc.nc
-    x_v = hidden.rearrange("b s m -> (b s) m").rearrange("(g p j) m -> g p (j m)", g=2, j=4)
+    x_v = hidden.rearrange("b s m -> (b s) m").rearrange("(g p j) m -> g p j m", g=2, j=4)
     g_v = gout.rearrange("b s m -> (b s) m").rearrange("(g p a i) m -> g a p (i m)", g=2, a=2, i=2)
     wo_v = wo.rearrange("u h m -> (u h) m").rearrange("(c a p i) m -> c a p (i m)", c=3, a=2, i=2)
     wq_v = wq.rearrange("m u h -> m (u h)").rearrange("(r p i) e -> r p (i e)", r=4, i=2)
@@ -32,38 +38,56 @@ def tile_qwen3_5attention_pb_v_kernel(tc, hidden, wq, attn, wo, gate, gout, dx_o
     dx_v = dx_out.rearrange("b s m -> (b s) m").rearrange("(g p j) m -> g j p m", g=2, j=4)
     dw_v = dw_out.rearrange("m u h -> m (u h)").rearrange("(t i q) e -> t q i e", i=2, q=P)
 
+    pairs = [[(0, 2 * a, c), (0, 2 * a + 1, c)] for c in range(3) for a in range(2)]
+    pairs += [[(1, 2 * a, c), (1, 2 * a + 1, c)] for a, c in ENDING]
+    groups = [[0], [1], [2, 3], [4, 5], [6, 7], [8, 9], [10, 11]]
+    group = {k: ks for ks in groups for k in ks}
+    where = {s: (k, i) for k, pr in enumerate(pairs) for i, s in enumerate(pr)}
+
     with ExitStack() as ctx:
         sb = ctx.enter_context(tc.tile_pool(name="sb", bufs=1))
         ps = ctx.enter_context(tc.psum_pool(name="ps", bufs=1))
-        ctx.enter_context(tc.manual_schedule(engines={mybir.EngineType.PE, mybir.EngineType.SP}))
+        if PIN == "all":
+            ctx.enter_context(tc.manual_schedule())
+        else:
+            ctx.enter_context(tc.manual_schedule(engines={mybir.EngineType.PE, mybir.EngineType.SP}))
 
         ident = sb.tile([P, P], F32, name="ident")
         make_identity(nc, ident[:])
 
-        steps = [(c, g) for g in range(2) for c in range(3)]
+        free = {"bank": list(range(8)), "raw": list(range(4)), "big": list(range(3)), "gate": list(range(GATES)), "attn": list(range(3)),
+                "stage": list(range(7)), "es": list(range(3)), "dz": list(range(6)), "out": list(range(OUTS)), "xraw": list(range(2))}
+        held = {}
         tiles = {}
-        work = {}
-        users = {}
-        ring = {}
 
-        def unit(name, needs, uses, fn):
-            work[name] = (needs, uses, fn)
-            for t in uses:
-                users.setdefault(t, []).append(name)
+        def take(key, kind, cols, dtype):
+            slot = free[kind].pop(0)
+            held[key] = (kind, slot)
+            if kind == "bank":
+                tiles[key] = ps.tile([P, cols], dtype, name="bank%d" % slot)
+            else:
+                tiles[key] = sb.tile([P, cols], dtype, name="%s%d" % (kind, slot), align_bytes=64)
+            return tiles[key]
 
-        def decl(key, shape, dtype, kind, depth):
-            ring[key] = (shape, dtype, kind, depth)
+        def give(key):
+            kind, slot = held.pop(key)
+            free[kind].append(slot)
+            pump()
 
         def codes(key, cols):
-            decl((key, "c"), [P, cols], U32, "%s_c" % (key,), 1)
-            decl((key, "s"), [P, cols], U8, "%s_s" % (key,), 1)
-            return [(key, "c"), (key, "s")]
+            tiles[key, "c"] = sb.tile([P, cols], U32, name="c_%s%d" % key, align_bytes=64)
+            tiles[key, "s"] = sb.tile([P, cols], U8, name="s_%s%d" % key, align_bytes=64)
 
-        def copy(eng, out, in_):
-            if eng == "S":
-                nc.scalar.copy(out=out, in_=in_)
-            else:
-                nc.vector.tensor_copy(out=out, in_=in_)
+        for g in range(2):
+            codes(("g", g), 1024)
+            codes(("x", g), 1024)
+            codes(("q", g), 1536)
+        for c in range(3):
+            codes(("w", c), 1024)
+        for k in range(12):
+            codes(("e", k), 256)
+        for k in range(6):
+            codes(("t", k), W)
 
         def quantize(key, c0, fmt, src):
             n = src.shape[1] // 4
@@ -74,365 +98,338 @@ def tile_qwen3_5attention_pb_v_kernel(tc, hidden, wq, attn, wo, gate, gout, dx_o
                                 rhs=tiles[b, "c"][:, b0:b0 + W].bitcast(bfmt), rhs_scale=tiles[b, "s"][:, b0:b0 + W],
                                 start=start, stop=stop)
 
-        def load(name, key, src):
-            unit(name, [], [key], lambda eng: nc.sync.dma_start(out=tiles[key][:], in_=src))
-
-        def turn(name, raw, row, w0, step, drain, dst, d0, pattern, needs):
-            bank = ("bank", name)
-            decl(bank, [P, W], F32, "bank", BANKS)
-
-            def pe(eng):
-                words = tiles[raw][:].bitcast(F32)
-                for i in range(2):
-                    for u in range(2):
-                        if step == 2:
-                            src = words[:, row * i + w0 + u:row * i + w0 + 256:2]
-                        else:
-                            src = words[:, row * i + w0 + P * u:row * i + w0 + P * u + P]
-                        nc.tensor.transpose(tiles[bank][:, 256 * i + P * u:256 * i + P * u + P], src, ident[:])
-
-            def out(eng):
-                to = tiles[dst][:, d0:d0 + 1024].bitcast(F32)
-                if pattern == "i n u":
-                    copy(eng, to.rearrange("p (i n u) -> p i n u", i=2, u=2), tiles[bank][:].rearrange("p (i u n) -> p i n u", i=2, u=2))
-                else:
-                    copy(eng, to.rearrange("p (n i u) -> p n i u", i=2, u=2), tiles[bank][:].rearrange("p (i u n) -> p n i u", i=2, u=2))
-
-            unit(name, needs, [raw, bank], pe)
-            unit(drain, [name], [bank, dst], out)
-
-        def interleave(eng, dst, src):
-            copy(eng, dst.rearrange("p (c i t) -> p c t i", i=4, t=4), src.rearrange("p t (c i) -> p c t i", i=4))
-
-        for g in range(2):
-            gk = "g%d" % g
-            cs = codes(gk, 1024)
-            for a in range(2):
-                raw, stg = ("graw", g, a), ("gstg", g, a)
-                decl(raw, [P, 2048], BF16, "raw", 4)
-                decl(stg, [P, 2048], BF16, "stage", 4)
-                load(("LG", g, a), raw, g_v[g, a])
-                for h in range(2):
-                    turn(("TG", g, a, h), raw, 512, 256 * h, 2, ("CG", g, a, h), stg, 1024 * h, "i n u", [("LG", g, a)])
-                unit(("QG", g, a), [("CG", g, a, 0), ("CG", g, a, 1)], [stg] + cs,
-                     lambda eng, gk=gk, a=a, stg=stg: quantize(gk, W * a, E5M2, tiles[stg][:]))
-        for c in range(3):
-            wk = "w%d" % c
-            cs = codes(wk, 1024)
-            for h in range(2):
-                decl(("wstg", c, h), [P, 2048], BF16, "stage", 4)
-            for a in range(2):
-                raw = ("wraw", c, a)
-                decl(raw, [P, 2048], BF16, "raw", 4)
-                load(("LW", c, a), raw, wo_v[c, a])
-                for h in range(2):
-                    turn(("TW", c, a, h), raw, 512, 256 * h, 2, ("CW", c, a, h), ("wstg", c, h), 1024 * a, "n i u", [("LW", c, a)])
-            for h in range(2):
-                unit(("QW", c, h), [("CW", c, 0, h), ("CW", c, 1, h)], [("wstg", c, h)] + cs,
-                     lambda eng, wk=wk, c=c, h=h: quantize(wk, W * h, E4M3, tiles["wstg", c, h][:]))
-        for n in range(2):
-            qk = "q%d" % n
-            cs = codes(qk, 1536)
-            for c in range(3):
-                decl(("qstg", n, c), [P, 2048], BF16, "qstage", 3)
-            for r in (2 * n, 2 * n + 1):
-                raw = ("qraw", r)
-                decl(raw, [P, 3072], BF16, "big", 3)
-                load(("LQ", r), raw, wq_v[r])
-                for c in range(3):
-                    turn(("TQ", r, c), raw, 768, 256 * c, 2, ("CQ", r, c), ("qstg", n, c), 1024 * (r % 2), "n i u", [("LQ", r)])
-            for c in range(3):
-                unit(("QQ", n, c), [("CQ", 2 * n, c), ("CQ", 2 * n + 1, c)], [("qstg", n, c)] + cs,
-                     lambda eng, qk=qk, n=n, c=c: quantize(qk, W * c, E4M3, tiles["qstg", n, c][:]))
-        for g in range(2):
-            xk = "x%d" % g
-            cs = codes(xk, 1024)
-            raw = ("xraw", g)
-            decl(raw, [P, 4096], BF16, "xraw", 1)
-            load(("LX", g), raw, x_v[g])
-            for i in range(2):
-                stg = ("xstg", g, i)
-                decl(stg, [P, 2048], BF16, "tstage", 2)
-                unit(("IX", g, i), [("LX", g)], [raw, stg],
-                     lambda eng, raw=raw, stg=stg, i=i: interleave(eng, tiles[stg][:], tiles[raw][:].rearrange("p (t m) -> p t m", t=4)[:, :, W * i:W * i + W]))
-                unit(("QX", g, i), [("IX", g, i)], [stg] + cs,
-                     lambda eng, xk=xk, stg=stg, i=i: quantize(xk, W * i, E4M3, tiles[stg][:]))
-
-        def step_units(s):
-            c, g = steps[s]
-            ec = slice(W * c, W * c + W)
-            at, dz, ge, gt = ("attn", s), ("dz", s), ("ge", s), ("gt", s)
-            decl(at, [P, 2048], BF16, "attn", 3)
-            decl(dz, [P, 2048], BF16, "dz", 4)
-            decl(ge, [P, 2048], BF16, "estage", 2)
-            decl(gt, [P, 2048], BF16, "tstage", 2)
-            ek, tk = "e%d" % s, "t%d" % s
-            ecs, tcs = codes(ek, W), codes(tk, W)
-            unit(("LA", s), [], [at], lambda eng: nc.sync.dma_start(out=tiles[at][:].rearrange("p (j e) -> p j e", j=4), in_=at_v[g][:, :, ec]))
-
-            def half(a):
-                ga = ("gate", s, a)
-                decl(ga, [P, 1024], F32, "gate", 2 * 3)
-                unit(("LE", s, a), [], [ga],
-                     lambda eng: nc.sync.dma_start(out=tiles[ga][:].rearrange("p (j e) -> p j e", j=2), in_=ga_v[g][:, 2 * a:2 * a + 2, ec]))
-                unit(("TH", s, a), [("LE", s, a)], [ga],
-                     lambda eng: nc.scalar.activation(out=tiles[ga][:], in_=tiles[ga][:], func=ACT.Tanh, scale=0.5))
-                unit(("SQ", s, a), [("TH", s, a)], [ga],
-                     lambda eng: nc.scalar.activation(out=tiles[ga][:], in_=tiles[ga][:], func=ACT.Square, scale=0.5))
-                unit(("WM", s, a), [("SQ", s, a), ("LA", s)], [ga, at],
-                     lambda eng: nc.vector.scalar_tensor_tensor(out=tiles[ga][:], in0=tiles[ga][:], scalar=0.25, in1=tiles[at][:, 1024 * a:1024 * a + 1024],
-                                                                op0=ALU.subtract, op1=ALU.mult))
-                turn(("TZ", s, a), dz, 256, W * a, 2, ("CZ", s, a), ge, 1024 * a, "i n u", [("DZ", s, 2 * a), ("DZ", s, 2 * a + 1)])
-                unit(("QE", s, a), [("CZ", s, a)], [ge] + ecs, lambda eng: quantize(ek, 256 * a, E5M2, tiles[ge][:, 1024 * a:1024 * a + 1024]))
-
-            def slot(j):
-                bank = ("bank", "DG", s, j)
-                ga = ("gate", s, j // 2)
-                decl(bank, [P, W], F32, "bank", BANKS)
-
-                def pe(eng):
-                    for h in range(2):
-                        mx(tiles[bank][:], "g%d" % g, W * (j // 2) + 256 * h + P * (j % 2), E5M2, "w%d" % c, W * h, E4M3, h == 0, h == 1)
-
-                def out(eng):
-                    nc.vector.scalar_tensor_tensor(out=tiles[dz][:, W * j:W * j + W], in0=tiles[bank][:], scalar=-1.0,
-                                                   in1=tiles[ga][:, W * (j % 2):W * (j % 2) + W], op0=ALU.mult, op1=ALU.mult)
-
-                unit(("DG", s, j), [("QG", g, j // 2), ("QW", c, 0), ("QW", c, 1)], [bank], pe)
-                unit(("DZ", s, j), [("DG", s, j), ("WM", s, j // 2)], [bank, dz, ga], out)
-
-            for a in range(2):
-                half(a)
-            for j in range(4):
-                slot(j)
-            unit(("IZ", s), [("DZ", s, j) for j in range(4)], [dz, gt],
-                 lambda eng: interleave(eng, tiles[gt][:], tiles[dz][:].rearrange("p (t m) -> p t m", t=4)))
-            unit(("QT", s), [("IZ", s)], [gt] + tcs, lambda eng: quantize(tk, 0, E5M2, tiles[gt][:]))
-
-        for s in range(6):
-            step_units(s)
-
-        def dx_units(g, j):
-            o = ("xo", g, j)
-            decl(o, [P, 1024], F32, "out", 4)
-            ss = [steps.index((c, g)) for c in range(3)]
-
-            def half(n):
-                bank = ("bank", "DX", g, j, n)
-                decl(bank, [P, W], F32, "bank", BANKS)
-
-                def passes(cs):
-                    def pe(eng):
-                        for c in cs:
-                            mx(tiles[bank][:], "e%d" % ss[c], P * j, E5M2, "q%d" % n, W * c, E4M3, c == 0, c == 2)
-                    return pe
-
-                unit(("DXa", g, j, n), [("QE", ss[c], j // 2) for c in range(2)] + [("QQ", n, c) for c in range(2)], [bank], passes([0, 1]))
-                unit(("DXb", g, j, n), [("DXa", g, j, n), ("QE", ss[2], j // 2), ("QQ", n, 2)], [bank], passes([2]))
-                unit(("OX", g, j, n), [("DXb", g, j, n)], [bank, o], lambda eng: copy(eng, tiles[o][:, W * n:W * n + W], tiles[bank][:]))
-
-            for n in range(2):
-                half(n)
-            if (g, j) != (1, 3):
-                unit(("SX", g, j), [("OX", g, j, 0), ("OX", g, j, 1)], [o], lambda eng: nc.sync.dma_start(out=dx_v[g, j], in_=tiles[o][:]))
+        def copy(on_vector, out, in_):
+            if on_vector:
+                nc.vector.tensor_copy(out=out, in_=in_)
             else:
-                for n in range(2):
-                    unit(("SY", n), [("OX", g, j, n)], [o],
-                         lambda eng, n=n: nc.sync.dma_start(out=dx_v[g, j][:, W * n:W * n + W], in_=tiles[o][:, W * n:W * n + W]))
+                nc.scalar.copy(out=out, in_=in_)
 
-        def dw_units(c, t):
-            o = ("wo", c, t)
-            decl(o, [P, 1024], F32, "out", 4)
-            ss = [steps.index((c, g)) for g in range(2)]
+        def span(k, view):
+            (g, j0, c0), (g1, j1, c1) = pairs[k]
+            return view[g][:, j0:j1 + 1, W * c0:W * c1 + W]
 
-            def half(i):
-                bank = ("bank", "DW", c, t, i)
-                decl(bank, [P, W], F32, "bank", BANKS)
+        def load_gate(k):
+            src = span(k, ga_v)
+            nc.sync.dma_start(out=take(("gate", k), "gate", 1024, F32)[:].rearrange("p (j e) -> p j e", j=src.shape[1]), in_=src)
 
-                def passes(g):
-                    return lambda eng: mx(tiles[bank][:], "x%d" % g, 256 * t + P * i, E4M3, "t%d" % ss[g], 0, E5M2, g == 0, g == 1)
+        def load_attn(k):
+            (g, j0, c0), (g1, j1, c1) = pairs[k][0], pairs[group[k][-1]][1]
+            src = at_v[g][:, j0:j1 + 1, W * c0:W * c1 + W]
+            nc.sync.dma_start(out=take(("attn", k), "attn", 1024 * len(group[k]), BF16)[:].rearrange("p (j e) -> p j e", j=src.shape[1]), in_=src)
 
-                unit(("DWa", c, t, i), [("QT", ss[0]), ("QX", 0, t // 2)], [bank], passes(0))
-                unit(("DWb", c, t, i), [("DWa", c, t, i), ("QT", ss[1]), ("QX", 1, t // 2)], [bank], passes(1))
-                unit(("OW", c, t, i), [("DWb", c, t, i)], [bank, o],
-                     lambda eng: copy(eng, tiles[o][:, W * i:W * i + W], tiles[bank][:]))
+        def load_x(g, h):
+            nc.sync.dma_start(out=take(("xraw", g, h), "xraw", 2048, BF16)[:].rearrange("p (j m) -> p j m", j=4), in_=x_v[g][:, :, W * h:W * h + W])
 
-            for i in range(2):
-                half(i)
-            unit(("SW", c, t), [("OW", c, t, 0), ("OW", c, t, 1)], [o],
-                 lambda eng: nc.sync.dma_start(out=dw_v[t][:, :, W * c:W * c + W], in_=tiles[o][:].rearrange("p (i e) -> p i e", i=2)))
+        def load_rows(key, kind, src):
+            nc.sync.dma_start(out=take(key, kind, src.shape[1], BF16)[:], in_=src)
 
-        for g in range(2):
-            for j in range(4):
-                dx_units(g, j)
-        for c in range(3):
-            for t in range(4):
-                dw_units(c, t)
+        def ew(k):
+            return [("gate", load_gate, k)] + ([("attn", load_attn, k)] if k % 2 == 0 else [])
 
-        def weave(main, fill):
-            out, k = [], 0
-            for i, f in enumerate(main):
-                out.append(f)
-                want = (i + 1) * len(fill) // len(main)
-                out += fill[k:want]
-                k = want
-            return out
+        def lg(g, a):
+            return ("raw", load_rows, ("graw", g, a), "raw", g_v[g, a])
 
+        def lw(c, a):
+            return ("raw", load_rows, ("wraw", c, a), "raw", wo_v[c, a])
 
-        def tg(g, a):
-            return [("TG", g, a, h) for h in range(2)]
+        def lq(r):
+            return ("big", load_rows, ("qraw", r), "big", wq_v[r])
+
+        def lx(g, h):
+            return ("xraw", load_x, g, h)
+
+        def le(k):
+            return ("gate", load_gate, k)
+
+        def la(k):
+            return ("attn", load_attn, k)
+
+        loads = [lg(0, 0), lw(0, 0), lw(0, 1), le(0), la(0), lg(0, 1), lx(0, 0), le(1), la(1), lw(1, 0), lw(1, 1), le(2), la(2), lx(0, 1), le(3)]
+        loads += [lw(2, 0), lw(2, 1), le(4), la(4), lq(0), lq(1), le(5), lg(1, 0), le(6), la(6), lq(2), lq(3), lg(1, 1), le(7), lx(1, 0), le(8), lx(1, 1)]
+        loads += [la(8), le(9), le(10), la(10), le(11)]
+
+        def pump():
+            while loads and free[loads[0][0]]:
+                job = loads.pop(0)
+                job[1](*job[2:])
+
+        def turn(bank, srcs):
+            b = take(bank, "bank", W, F32)
+            for i, words in enumerate(srcs):
+                for u in range(2):
+                    nc.tensor.transpose(b[:, 256 * i + P * u:256 * i + P * u + P], words[:, u:256:2], ident[:])
+
+        def unturn(bank, to, rows_apart, on_vector):
+            src = tiles[bank][:].rearrange("p (i u n) -> p i n u", i=2, u=2)
+            if rows_apart:
+                copy(on_vector, to.bitcast(F32).rearrange("p (i n u) -> p i n u", i=2, u=2), src)
+            else:
+                copy(on_vector, to.bitcast(F32).rearrange("p (n i u) -> p n i u", i=2, u=2), src.rearrange("p i n u -> p n i u"))
+            give(bank)
+
+        def prep_pe(job):
+            kind, a, b, h = job
+            raw = {"g": ("graw", a, b), "w": ("wraw", a, b), "q": ("qraw", 2 * a + b)}[kind]
+            row = 768 if kind == "q" else 512
+            words = tiles[raw][:].bitcast(F32)
+            turn(job, [words[:, row * i + 256 * h:row * i + 256 * h + 256] for i in range(2)])
+            if h == (2 if kind == "q" else 1):
+                give(raw)
+
+        def prep_out(job, on_vector=False):
+            kind, a, b, h = job
+            stg, half = (("stg", kind, a, b), h) if kind == "g" else (("stg", kind, a, h), b)
+            if half == 0:
+                take(stg, "stage", 2048, BF16)
+            unturn(job, tiles[stg][:, 1024 * half:1024 * half + 1024], kind == "g", on_vector)
+
+        def prep_q(job):
+            kind, a, b, h = job
+            stg, half = (("stg", kind, a, b), h) if kind == "g" else (("stg", kind, a, h), b)
+            if half == 1:
+                quantize((kind, a), W * stg[3], E5M2 if kind == "g" else E4M3, tiles[stg][:])
+                give(stg)
+
+        def interleave(dst, src):
+            nc.vector.tensor_copy(out=dst.rearrange("p (c i t) -> p c t i", i=4, t=4), in_=src.rearrange("p (t c i) -> p c t i", t=4, i=4))
+
+        def weave(src, stg):
+            interleave(take(stg, "stage", 2048, BF16)[:], tiles[src][:])
+
+        def weave_q(stg, key, c0, fmt):
+            quantize(key, c0, fmt, tiles[stg][:])
+            give(stg)
+
+        def ix(g, h):
+            weave(("xraw", g, h), ("xs", g, h))
+            give(("xraw", g, h))
+
+        def qx(g, h):
+            weave_q(("xs", g, h), ("x", g), W * h, E4M3)
+
+        uses = {}
+
+        def used(key, n):
+            uses[key] = uses.get(key, 0) + 1
+            if uses[key] == n:
+                give(key)
+
+        def iz(g, c):
+            weave(("dz", g, c), ("ts", g, c))
+            used(("dz", g, c), 5)
+
+        def qt(g, c):
+            weave_q(("ts", g, c), ("t", 3 * g + c), 0, E5M2)
+
+        def th(k):
+            ga = tiles["gate", k]
+            nc.scalar.activation(out=ga[:], in_=ga[:], func=ACT.Tanh, scale=0.5)
+
+        def sq(k):
+            ga = tiles["gate", k]
+            nc.scalar.activation(out=ga[:], in_=ga[:], func=ACT.Square, scale=0.5)
+
+        def wm(k):
+            (g, j0, c0), (g1, j1, c1), (g2, j, c) = pairs[group[k][0]][0], pairs[group[k][-1]][1], pairs[k][0]
+            ga = tiles["gate", k][:].rearrange("p (j e) -> p j e", j=2)
+            at = tiles["attn", group[k][0]][:].rearrange("p (j e) -> p j e", j=j1 - j0 + 1)[:, j - j0:j - j0 + 2, W * (c - c0):W * (c - c0) + W]
+            nc.vector.scalar_tensor_tensor(out=ga, in0=ga, scalar=0.25, in1=at,
+                                           op0=ALU.subtract, op1=ALU.mult)
+            used(("attn", group[k][0]), len(group[k]))
+
+        def dg(k, i):
+            g, j, c = pairs[k][i]
+            b = take(("dg", k, i), "bank", W, F32)
+            for h in range(2):
+                mx(b[:], ("g", g), W * (j // 2) + 256 * h + P * (j % 2), E5M2, ("w", c), W * h, E4M3, h == 0, h == 1)
+
+        def dz(k, i):
+            g, j, c = pairs[k][i]
+            if j == 0:
+                take(("dz", g, c), "dz", 2048, BF16)
+            nc.vector.scalar_tensor_tensor(out=tiles["dz", g, c][:, W * j:W * j + W], in0=tiles["dg", k, i][:], scalar=-1.0,
+                                           in1=tiles["gate", k][:, W * i:W * i + W], op0=ALU.mult, op1=ALU.mult)
+            give(("dg", k, i))
+            if i == 1:
+                give(("gate", k))
+
+        def tz(k):
+            turn(("tz", k), [tiles["dz", g, c][:, W * j:W * j + W].bitcast(F32) for g, j, c in pairs[k]])
+            for g, j, c in pairs[k]:
+                used(("dz", g, c), 5)
+
+        def cz(k, on_vector=False):
+            unturn(("tz", k), take(("es", k), "es", 1024, BF16)[:], True, on_vector)
+
+        def qe(k):
+            weave_q(("es", k), ("e", k), 0, E5M2)
+
+        def out_pe(job, part):
+            kind, a, b, half = job
+            n = 3 if kind == "dx" else 2
+            if 0 in part:
+                take(job, "bank", W, F32)
+            for s in part:
+                if kind == "dx":
+                    k, i = where[a, b, s]
+                    mx(tiles[job][:], ("e", k), P * i, E5M2, ("q", half), W * s, E4M3, s == 0, s == n - 1)
+                else:
+                    mx(tiles[job][:], ("x", s), 256 * b + P * half, E4M3, ("t", 3 * s + a), 0, E5M2, s == 0, s == n - 1)
+
+        def out_copy(job, on_vector):
+            kind, a, b, half = job
+            o = ("o", kind, a, b)
+            if o not in tiles:
+                take(o, "out", 1024, F32)
+            copy(on_vector, tiles[o][:, W * half:W * half + W], tiles[job][:])
+            give(job)
+            uses[o] = uses.get(o, 0) + 1
+            if uses[o] == 2:
+                if kind == "dx":
+                    nc.sync.dma_start(out=dx_v[a, b], in_=tiles[o][:])
+                else:
+                    nc.sync.dma_start(out=dw_v[b][:, :, W * a:W * a + W], in_=tiles[o][:].rearrange("p (i e) -> p i e", i=2))
+                give(o)
+
+        def tg(g):
+            return [("g", g, a, h) for a in range(2) for h in range(2)]
 
         def tw(c):
-            return [("TW", c, a, h) for a in range(2) for h in range(2)]
+            return [("w", c, a, h) for a in range(2) for h in range(2)]
 
-        def tq(r):
-            return [("TQ", r, c) for c in range(3)]
+        def tq(n):
+            return [("q", n, b, h) for b in range(2) for h in range(3)]
 
-        def dx(g, part="ab"):
-            return [[("DX" + k, g, j, n) for k in part] for j in range(4) for n in range(2)]
+        def dx(g, j):
+            return [("dx", g, j, n) for n in range(2)]
 
-        def dw(c, part="ab"):
-            return [[("DW" + k, c, t, i) for k in part] for t in range(4) for i in range(2)]
+        def dw(c):
+            return [("dw", c, t, i) for t in range(4) for i in range(2)]
 
-        def ew(s):
-            return [(k, s, a) for a in range(2) for k in ("TH", "SQ")]
+        count = [0]
 
-        def flat(ls):
-            return [x for l in ls for x in (l if isinstance(l, list) else [l])]
+        def outs(jobs, share):
+            for job in jobs:
+                out_pe(job, range(3 if job[0] == "dx" else 2))
+                count[0] += 1
+                out_copy(job, count[0] % share == 0)
 
-        drain = {"DG": "DZ", "TG": "CG", "TW": "CW", "TQ": "CQ", "TZ": "CZ", "DXb": "OX", "DWb": "OW"}
+        def preps(jobs, on_vector=()):
+            for n, job in enumerate(jobs):
+                prep_pe(job)
+                prep_out(job, n in on_vector)
+                prep_q(job)
 
-        def drains(q):
-            return [(drain[n[0]],) + n[1:] for n in q if n[0] in drain]
+        pump()
+        def run(todo):
+            for f in todo:
+                f[0](*f[1:])
 
+        def whole(job):
+            return range(3 if job[0] == "dx" else 2)
 
-        def ew_loads(s):
-            return [("LE", s, 0), ("LA", s), ("LE", s, 1)]
+        def zipped(a, b):
+            out = []
+            for i in range(max(len(a), len(b))):
+                out += a[i:i + 1] + b[i:i + 1]
+            return out
 
-        def dxn(g, n):
-            return [[("DXa", g, j, n), ("DXb", g, j, n)] for j in range(4)]
+        g0, g1, w0, w1, w2, q0, q1 = tg(0), tg(1), tw(0), tw(1), tw(2), tq(0), tq(1)
+        for n, job in enumerate(g0[:2] + w0):
+            prep_pe(job)
+            prep_out(job, n in HV)
+            if n == 3:
+                th(0)
+            prep_q(job)
+        sq(0)
+        prep_pe(g0[2])
+        prep_pe(g0[3])
+        dg(0, 0)
+        dg(0, 1)
+        prep_out(g0[2])
+        wm(0)
+        prep_out(g0[3])
+        th(1)
+        sq(1)
+        prep = {-1: g0[2:], 0: w1, 2: w2, 3: q0, 4: g1[:2] + q1[:3], 5: q1[3:] + g1[2:]}
+        acts = {0: [], 1: [(th, 3), (sq, 3)]}
+        for k in range(2, 9):
+            acts[k] = [(th, k + 2), (sq, k + 2)]
+        jobs = {5: dx(0, 0)[:1] + dx(0, 1)[:1], 6: dx(0, 0)[1:] + dx(0, 1)[1:] + dx(0, 2)[:1], 7: dx(0, 3)[:1] + dx(0, 2)[1:] + dx(0, 3)[1:], 8: dw(0)[:6]}
+        share = {3: (1, 3,), 4: (2,), 8: (), 9: (), 10: ()}
+        back = {0: [(ix, 0, 0), (qx, 0, 0)], 1: [(ix, 0, 1), (qx, 0, 1)], 2: [(iz, 0, 0), (qt, 0, 0)], 5: [(ix, 1, 0), (qx, 1, 0)], 6: [(ix, 1, 1), (qx, 1, 1)],
+                7: [(iz, 1, 0), (qt, 1, 0)], 8: [(iz, 0, 1), (qt, 0, 1)], 9: [(iz, 0, 2), (qt, 0, 2)], 10: [(iz, 1, 1), (qt, 1, 1)]}
+        for k in range(9):
+            mine = prep.get(k, [])
+            turns = ([(tz, k - 1)] if k else []) + [(prep_pe, job) for job in mine]
+            drains = ([(cz, k - 1)] if k else []) + [(prep_out, job, n in share.get(k, ())) for n, job in enumerate(mine)]
+            run(turns[:4])
+            quants = [(prep_q, job) for job in prep.get(k - 1, [])]
+            run(quants[-3:])
+            dz(k, 0)
+            run(quants[:-3])
+            dz(k, 1)
+            mix = zipped(drains, acts.get(k, []))
+            run(mix[:4])
+            run(turns[4:])
+            todo = back.get(k, [])
+            run(todo[:1])
+            wm(k + 1)
+            if k > 0:
+                qe(k - 1)
+            dg(k + 1, 0)
+            dg(k + 1, 1)
+            run(mix[4:])
+            if k == 0:
+                th(2)
+                sq(2)
+            run(todo[1:])
+            for n, job in enumerate(jobs.get(k, [])):
+                out_pe(job, whole(job))
+                out_copy(job, n in share.get(k, ()))
 
+        def outs2(jobs, part=None, vec=()):
+            for n, job in enumerate(jobs):
+                out_pe(job, part or whole(job))
+                out_copy(job, n in vec)
 
-        def first(jobs):
-            return [j[:1] for j in jobs]
-
-        def second(jobs):
-            return [j[1:] for j in jobs]
-
-        def tz(s):
-            return [("TZ", s, 0), ("TZ", s, 1)]
-
-        def dg(s, *js):
-            return [("DG", s, j) for j in js]
-
-        loads = [("LG", 0, 0), ("LE", 0, 0), ("LW", 0, 0), ("LW", 0, 1), ("LX", 0), ("LA", 0), ("LG", 0, 1), ("LE", 0, 1)]
-        for s in (1, 2):
-            loads += [("LW", s, 0), ("LW", s, 1), ("LE", s, 0), ("LA", s), ("LQ", s - 1), ("LE", s, 1)]
-        for a in range(2):
-            loads += [("LG", 1, a), ("LQ", 2 + a)]
-        loads += ew_loads(3) + [("LX", 1)] + ew_loads(4) + ew_loads(5)
-        stores = [("SX", 0, j) for j in range(4)] + [("SW", c, t) for c in range(2) for t in range(4)]
-        stores += [("SX", 1, 0), ("SX", 1, 1)] + [("SW", 2, t) for t in range(4)] + [("SX", 1, 2), ("SY", 0), ("SY", 1)]
-        x0, x1, ends = dxn(0, 0), dxn(0, 1), dx(1)
-        pe = tg(0, 0) + tw(0) + tg(0, 1)
-        pe += dg(0, 0, 1) + tw(1)[:2] + dg(0, 2) + tw(1)[2:] + dg(0, 3) + tq(0)
-        pe += dg(1, 0) + tw(2)[:2] + dg(1, 1) + tw(2)[2:] + dg(1, 2) + tz(0) + dg(1, 3) + tq(1)
-        pe += dg(2, 0) + tz(1) + tg(1, 0) + dg(2, 1) + tq(2) + dg(2, 2) + tz(2)[:1] + tg(1, 1) + dg(2, 3) + tq(3)[:2] + first(x0[:2]) + tq(3)[2:] + tz(2)[1:]
-        pe += second(x0[:2]) + dg(3, 0, 1) + x0[2:] + dg(3, 2, 3) + x1 + tz(3)
-        pe += dg(4, 0, 1) + first(dw(0)[:3]) + second(dw(0)[:3]) + dg(4, 2, 3) + dw(0)[3:] + tz(4)
-        pe += dg(5, 0, 1) + first(dw(1)[:3]) + second(dw(1)[:3]) + dg(5, 2, 3) + tz(5)[:1] + dw(1)[3:] + first(ends[:2]) + tz(5)[1:]
-        pe += second(ends[:2]) + ends[2:4] + first(dw(2)[:3]) + second(dw(2)[:3]) + dw(2)[3:] + ends[4:]
-        pe = flat(pe)
-
-        pos, count = {}, 0
-        for n in pe:
-            pos[n] = count
-            if n[0] not in ("DXa", "DWa"):
-                count += 1
-        place, source = {}, {}
-        for n in pe:
-            if n[0] in drain:
-                place[(drain[n[0]],) + n[1:]] = pos[n] + 0.5
-                source[(drain[n[0]],) + n[1:]] = n
-        copies = [n for n in place if n[0] != "DZ"]
-
-        def behind(n):
-            first = max(place[m] for m in work[n][0])
-            due = min([pos[m] for m in pos if n in work[m][0]] + [len(pe)])
-            later = [k for m, k in place.items() if m[0] == "DZ" and k > first]
-            soon = min(later) + 0.01 if later and first > pos["DG", 0, 0] else first + 0.9
-            place[n] = max(first + 0.01, min(soon, due))
-
-        def spread(names, s):
-            first, last = pos["DG", s, 0], pos["DG", s, 3]
-            for i, n in enumerate(names):
-                place[n] = first + (last - first) * i / len(names) + 0.6
-
-        for s in range(6):
-            for a in range(2):
-                k = pos["DG", s, 2 * a]
-                place["WM", s, a], place["SQ", s, a], place["TH", s, a] = k - 3, k - 5, k - 7
-        for n in work:
-            if n[0] in ("QG", "QW", "QQ", "QE"):
-                behind(n)
-        for i in range(2):
-            place["IX", 0, i], place["QX", 0, i] = pos["TG", 0, 1, i] - 0.05, pos["DG", 0, i] + 0.6
-        spread([("IX", 1, 0), ("QX", 1, 0)], 3)
-        place["IX", 1, 1], place["QX", 1, 1] = pos["TZ", 3, 0], pos["DG", 4, 0]
-        for c in range(2):
-            spread([("IZ", c), ("QT", c)], c + 1)
-        place["IZ", 2], place["QT", 2] = pos["TZ", 5, 1] + 1, pos["TZ", 5, 1] + 1.1
-        for c in range(3):
-            place["IZ", c + 3], place["QT", c + 3] = place["DZ", c + 3, 3] + 0.1, place["DZ", c + 3, 3] + 0.2
-        busy = range(pos["DG", 0, 0], pos["TZ", 5, 1] + 1)
-        sc, ve = [], []
-        for n in sorted(place, key=lambda n: place[n]):
-            if n in copies:
-                i, k = copies.index(n), pos[source[n]]
-                mine = i % 16 == 0 and k < pos["DG", 5, 0] if k in busy else i % 2 == (k > busy[0])
-                (ve if mine else sc).append(n)
-            else:
-                (sc if n[0] in ("TH", "SQ") else ve).append(n)
-        queues = {"D": loads + stores, "P": pe, "S": sc, "V": ve}
-
-        done = {}
-        last = {}
-        heads = {eng: 0 for eng in queues}
-
-        def free_slot(kind, depth):
-            free = []
-            for k in range(depth):
-                held = users[last[kind, k]] if (kind, k) in last else []
-                if all(u in done for u in held):
-                    free.append((max([done[u] for u in held] + [-1]), k))
-            return min(free)[1] if free else None
-
-        def ready(name):
-            needs, uses, fn = work[name]
-            return all(n in done for n in needs) and all(t in tiles or free_slot(*ring[t][2:]) is not None for t in uses)
-
-        place.update(pos)
-
-        def emit(finished):
-            while not finished():
-                free = [eng for eng, q in queues.items() if heads[eng] < len(q) and ready(q[heads[eng]])]
-                assert free, [q[heads[e]] for e, q in queues.items() if heads[e] < len(q)]
-                eng = min(free, key=lambda e: place.get(queues[e][heads[e]], -9))
-                name = queues[eng][heads[eng]]
-                needs, uses, fn = work[name]
-                for t in uses:
-                    if t not in tiles:
-                        shape, dtype, kind, depth = ring[t]
-                        k = free_slot(kind, depth)
-                        last[kind, k] = t
-                        if kind == "bank":
-                            tiles[t] = ps.tile(shape, dtype, name="bank%d" % k)
-                        else:
-                            tiles[t] = sb.tile(shape, dtype, name="%s%d" % (kind, k), align_bytes=64)
-                fn(eng)
-                done[name] = len(done)
-                heads[eng] += 1
-
-        with tc.manual_schedule(engines={mybir.EngineType.DVE}):
-            emit(lambda: ("DZ", 0, 1) in done)
-        emit(lambda: len(done) == len(work))
+        tz(8)
+        dz(9, 0)
+        dz(9, 1)
+        cz(8)
+        outs2(dw(0)[6:])
+        dg(10, 0)
+        dg(10, 1)
+        iz(1, 1)
+        th(11)
+        wm(10)
+        qt(1, 1)
+        tz(9)
+        for job in dw(1)[:3]:
+            out_pe(job, [0])
+        cz(9)
+        sq(11)
+        dz(10, 0)
+        dz(10, 1)
+        outs2(dw(1)[:3], [1])
+        dg(11, 0)
+        dg(11, 1)
+        wm(11)
+        qe(8)
+        outs2(dw(1)[3:5])
+        tz(10)
+        dz(11, 0)
+        cz(10)
+        dz(11, 1)
+        outs2(dw(1)[5:])
+        tz(11)
+        iz(0, 2)
+        qe(9)
+        qe(10)
+        cz(11)
+        iz(1, 2)
+        qt(0, 2)
+        outs2(dx(1, 0))
+        qt(1, 2)
+        qe(11)
+        outs2(dx(1, 1) + dx(1, 2) + dw(2) + dx(1, 3), None, range(1, 14, 2))

@@ -20,6 +20,8 @@ P = 128
 W = 512
 PIN = "all"
 HV = (0, 2, 4)
+SHARE = {3: (1, 3)}
+E1 = ()
 ENDING = [(0, 0), (1, 0), (0, 1), (1, 1), (0, 2), (1, 2)]
 LEAD = 2
 VSHARE = 3
@@ -56,7 +58,7 @@ def tile_qwen3_5attention_pb_v_kernel(tc, hidden, wq, attn, wo, gate, gout, dx_o
         make_identity(nc, ident[:])
 
         free = {"bank": list(range(8)), "raw": list(range(4)), "big": list(range(3)), "gate": list(range(GATES)), "attn": list(range(3)),
-                "stage": list(range(7)), "es": list(range(3)), "dz": list(range(6)), "out": list(range(OUTS)), "xraw": list(range(2))}
+                "stage": list(range(7)), "es": list(range(4)), "dz": list(range(6)), "out": list(range(OUTS)), "xraw": list(range(2))}
         held = {}
         tiles = {}
 
@@ -153,11 +155,12 @@ def tile_qwen3_5attention_pb_v_kernel(tc, hidden, wq, attn, wo, gate, gout, dx_o
                 job = loads.pop(0)
                 job[1](*job[2:])
 
-        def turn(bank, srcs):
+        def turn(bank, srcs, sorted_words=False):
             b = take(bank, "bank", W, F32)
             for i, words in enumerate(srcs):
                 for u in range(2):
-                    nc.tensor.transpose(b[:, 256 * i + P * u:256 * i + P * u + P], words[:, u:256:2], ident[:])
+                    src = words[:, P * u:P * u + P] if sorted_words else words[:, u:256:2]
+                    nc.tensor.transpose(b[:, 256 * i + P * u:256 * i + P * u + P], src, ident[:])
 
         def unturn(bank, to, rows_apart, on_vector):
             src = tiles[bank][:].rearrange("p (i u n) -> p i n u", i=2, u=2)
@@ -247,14 +250,15 @@ def tile_qwen3_5attention_pb_v_kernel(tc, hidden, wq, attn, wo, gate, gout, dx_o
             g, j, c = pairs[k][i]
             if j == 0:
                 take(("dz", g, c), "dz", 2048, BF16)
-            nc.vector.scalar_tensor_tensor(out=tiles["dz", g, c][:, W * j:W * j + W], in0=tiles["dg", k, i][:], scalar=-1.0,
-                                           in1=tiles["gate", k][:, W * i:W * i + W], op0=ALU.mult, op1=ALU.mult)
+            nc.vector.tensor_tensor(out=tiles["dz", g, c][:, W * j:W * j + W].rearrange("p (u m i) -> p u m i", u=2, i=2),
+                                    in0=tiles["dg", k, i][:].rearrange("p (m u i) -> p u m i", u=2, i=2),
+                                    in1=tiles["gate", k][:, W * i:W * i + W].rearrange("p (m u i) -> p u m i", u=2, i=2), op=ALU.mult)
             give(("dg", k, i))
             if i == 1:
                 give(("gate", k))
 
         def tz(k):
-            turn(("tz", k), [tiles["dz", g, c][:, W * j:W * j + W].bitcast(F32) for g, j, c in pairs[k]])
+            turn(("tz", k), [tiles["dz", g, c][:, W * j:W * j + W].bitcast(F32) for g, j, c in pairs[k]], True)
             for g, j, c in pairs[k]:
                 used(("dz", g, c), 5)
 
@@ -281,7 +285,13 @@ def tile_qwen3_5attention_pb_v_kernel(tc, hidden, wq, attn, wo, gate, gout, dx_o
             o = ("o", kind, a, b)
             if o not in tiles:
                 take(o, "out", 1024, F32)
-            copy(on_vector, tiles[o][:, W * half:W * half + W], tiles[job][:])
+            to, src = tiles[o][:, W * half:W * half + W], tiles[job][:]
+            if kind == "dw":
+                to, src = to.rearrange("p (m u i) -> p m u i", u=2, i=2), src.rearrange("p (u m i) -> p m u i", u=2, i=2)
+            if on_vector:
+                nc.vector.tensor_scalar_mul(out=to, in0=src, scalar1=-1.0)
+            else:
+                nc.scalar.activation(out=to, in_=src, func=ACT.Copy, scale=-1.0)
             give(job)
             uses[o] = uses.get(o, 0) + 1
             if uses[o] == 2:
@@ -334,6 +344,15 @@ def tile_qwen3_5attention_pb_v_kernel(tc, hidden, wq, attn, wo, gate, gout, dx_o
                 out += a[i:i + 1] + b[i:i + 1]
             return out
 
+        def outs2(jobs, part=None, vec=()):
+            for n, job in enumerate(jobs):
+                out_pe(job, part or whole(job))
+                out_copy(job, n in vec)
+
+        def opens(jobs, part):
+            for job in jobs:
+                out_pe(job, part)
+
         g0, g1, w0, w1, w2, q0, q1 = tg(0), tg(1), tw(0), tw(1), tw(2), tq(0), tq(1)
         for n, job in enumerate(g0[:2] + w0):
             prep_pe(job)
@@ -348,88 +367,130 @@ def tile_qwen3_5attention_pb_v_kernel(tc, hidden, wq, attn, wo, gate, gout, dx_o
         dg(0, 1)
         prep_out(g0[2])
         wm(0)
-        prep_out(g0[3])
         th(1)
+        prep_out(g0[3])
         sq(1)
-        prep = {-1: g0[2:], 0: w1, 2: w2, 3: q0, 4: g1[:2] + q1[:3], 5: q1[3:] + g1[2:]}
-        acts = {0: [], 1: [(th, 3), (sq, 3)]}
-        for k in range(2, 9):
-            acts[k] = [(th, k + 2), (sq, k + 2)]
-        jobs = {5: dx(0, 0)[:1] + dx(0, 1)[:1], 6: dx(0, 0)[1:] + dx(0, 1)[1:] + dx(0, 2)[:1], 7: dx(0, 3)[:1] + dx(0, 2)[1:] + dx(0, 3)[1:], 8: dw(0)[:6]}
-        share = {3: (1, 3,), 4: (2,), 8: (), 9: (), 10: ()}
-        back = {0: [(ix, 0, 0), (qx, 0, 0)], 1: [(ix, 0, 1), (qx, 0, 1)], 2: [(iz, 0, 0), (qt, 0, 0)], 5: [(ix, 1, 0), (qx, 1, 0)], 6: [(ix, 1, 1), (qx, 1, 1)],
-                7: [(iz, 1, 0), (qt, 1, 0)], 8: [(iz, 0, 1), (qt, 0, 1)], 9: [(iz, 0, 2), (qt, 0, 2)], 10: [(iz, 1, 1), (qt, 1, 1)]}
-        for k in range(9):
+        dz(0, 0)
+        dz(0, 1)
+        prep_q(g0[3])
+        run([(prep_pe, job) for job in w1])
+        ix(0, 0)
+        wm(1)
+        dg(1, 0)
+        dg(1, 1)
+        qx(0, 0)
+        run([(prep_out, job) for job in w1] + [(th, 2)])
+        prep = {0: w1, 2: w2, 3: q0, 4: g1[:2] + q1[:3], 5: g1[2:] + q1[3:]}
+        jobs = {5: dx(0, 0)[:1] + dx(0, 1)[:1]}
+        share = SHARE
+        back = {1: [(ix, 0, 1), (qx, 0, 1)], 2: [(iz, 0, 0), (qt, 0, 0)], 5: [(ix, 1, 0), (qx, 1, 0)]}
+        for k in range(1, 6):
             mine = prep.get(k, [])
-            turns = ([(tz, k - 1)] if k else []) + [(prep_pe, job) for job in mine]
-            drains = ([(cz, k - 1)] if k else []) + [(prep_out, job, n in share.get(k, ())) for n, job in enumerate(mine)]
-            run(turns[:4])
+            turns = [(tz, k - 1)] + [(prep_pe, job) for job in mine]
+            drains = [(cz, k - 1)] + [(prep_out, job, n in share.get(k, ())) for n, job in enumerate(mine)]
+            cut = (len(turns) + 1) // 2
+            run(turns[:cut])
             quants = [(prep_q, job) for job in prep.get(k - 1, [])]
             run(quants[-3:])
             dz(k, 0)
             run(quants[:-3])
             dz(k, 1)
-            mix = zipped(drains, acts.get(k, []))
-            run(mix[:4])
-            run(turns[4:])
+            acts = [(th, k + 2), (sq, k + 2)]
+            mix = drains[:2] + zipped(acts, drains[2:]) if mine else [(sq, 2), (cz, 0)] + acts
+            run(mix[:2])
+            dg(k + 1, 0)
+            run(mix[2:4])
+            run(turns[cut:])
             todo = back.get(k, [])
             run(todo[:1])
             wm(k + 1)
-            if k > 0:
-                qe(k - 1)
-            dg(k + 1, 0)
+            qe(k - 1)
             dg(k + 1, 1)
             run(mix[4:])
-            if k == 0:
-                th(2)
-                sq(2)
             run(todo[1:])
-            for n, job in enumerate(jobs.get(k, [])):
-                out_pe(job, whole(job))
-                out_copy(job, n in share.get(k, ()))
-
-        def outs2(jobs, part=None, vec=()):
-            for n, job in enumerate(jobs):
-                out_pe(job, part or whole(job))
-                out_copy(job, n in vec)
-
-        tz(8)
+            outs2(jobs.get(k, []))
+        tz(5)
+        run([(prep_q, job) for job in g1[2:] + q1[3:4]])
+        dz(6, 0)
+        cz(5)
+        run([(prep_q, job) for job in q1[4:]])
+        dz(6, 1)
+        dg(7, 0)
+        dg(7, 1)
+        th(8)
+        wm(7)
+        qe(5)
+        outs2(dx(0, 0)[1:])
+        sq(8)
+        outs2(dx(0, 1)[1:] + dx(0, 2)[:1])
+        ix(1, 1)
+        dz(7, 0)
+        dz(7, 1)
+        dg(8, 0)
+        dg(8, 1)
+        iz(1, 0)
+        qx(1, 1)
+        qt(1, 0)
+        outs2(dx(0, 3)[:1])
+        th(9)
+        outs2(dx(0, 2)[1:])
+        sq(9)
+        wm(8)
+        outs2(dx(0, 3)[1:])
+        tz(6)
+        opens(dw(0)[:2], [0])
+        dz(8, 0)
+        cz(6)
+        dz(8, 1)
+        outs2(dw(0)[:2], [1])
+        dg(9, 0)
+        dg(9, 1)
+        wm(9)
+        th(10)
+        outs2(dw(0)[2:4])
+        iz(0, 1)
+        sq(10)
         dz(9, 0)
         dz(9, 1)
-        cz(8)
-        outs2(dw(0)[6:])
+        outs2(dw(0)[4:], None, E1)
+        iz(1, 1)
+        qt(0, 1)
         dg(10, 0)
         dg(10, 1)
-        iz(1, 1)
-        th(11)
-        wm(10)
+        tz(7)
+        tz(8)
         qt(1, 1)
-        tz(9)
-        for job in dw(1)[:3]:
-            out_pe(job, [0])
-        cz(9)
+        wm(10)
+        th(11)
+        cz(7)
         sq(11)
+        cz(8)
+        opens(dw(1)[:2], [0])
         dz(10, 0)
         dz(10, 1)
-        outs2(dw(1)[:3], [1])
+        outs2(dw(1)[:2], [1])
         dg(11, 0)
         dg(11, 1)
+        qe(6)
         wm(11)
-        qe(8)
-        outs2(dw(1)[3:5])
+        tz(9)
         tz(10)
-        dz(11, 0)
+        qe(7)
+        qe(8)
+        cz(9)
         cz(10)
+        outs2(dw(1)[2:4])
+        dz(11, 0)
         dz(11, 1)
-        outs2(dw(1)[5:])
-        tz(11)
-        iz(0, 2)
         qe(9)
         qe(10)
-        cz(11)
+        outs2(dw(1)[4:])
+        iz(0, 2)
+        tz(11)
         iz(1, 2)
-        qt(0, 2)
+        cz(11)
         outs2(dx(1, 0))
+        qt(0, 2)
         qt(1, 2)
         qe(11)
         outs2(dx(1, 1) + dx(1, 2) + dw(2) + dx(1, 3), None, range(1, 14, 2))

@@ -18,9 +18,9 @@ ACT = mybir.ActivationFunctionType
 
 P = 128
 W = 512
-PIN = "all"
+PIN = "PS"
 HV = (0, 2, 4)
-SHARE = {3: (1, 3)}
+SHARE = {2: (1,), 3: (1, 3)}
 E1 = ()
 ENDING = [(0, 0), (1, 0), (0, 1), (1, 1), (0, 2), (1, 2)]
 LEAD = 2
@@ -146,8 +146,8 @@ def tile_qwen3_5attention_pb_v_kernel(tc, hidden, wq, attn, wo, gate, gout, dx_o
         def la(k):
             return ("attn", load_attn, k)
 
-        loads = [lg(0, 0), lw(0, 0), lw(0, 1), le(0), la(0), lg(0, 1), lx(0, 0), le(1), la(1), lw(1, 0), lw(1, 1), le(2), la(2), lx(0, 1), le(3)]
-        loads += [lw(2, 0), lw(2, 1), le(4), la(4), lq(0), lq(1), le(5), lg(1, 0), le(6), la(6), lq(2), lq(3), lg(1, 1), le(7), lx(1, 0), le(8), lx(1, 1)]
+        loads = [lg(0, 0), lw(0, 0), lw(0, 1), le(0), la(0), lg(0, 1), le(1), la(1), lx(0, 0), lw(1, 0), lw(1, 1), le(2), la(2), le(3)]
+        loads += [lw(2, 0), lw(2, 1), le(4), la(4), lq(0), le(5), lq(1), lx(0, 1), lg(1, 0), le(6), lq(2), la(6), lg(1, 1), le(7), lq(3), lx(1, 0), le(8), lx(1, 1)]
         loads += [la(8), le(9), le(10), la(10), le(11)]
 
         def pump():
@@ -354,36 +354,37 @@ def tile_qwen3_5attention_pb_v_kernel(tc, hidden, wq, attn, wo, gate, gout, dx_o
                 out_pe(job, part)
 
         g0, g1, w0, w1, w2, q0, q1 = tg(0), tg(1), tw(0), tw(1), tw(2), tq(0), tq(1)
-        for n, job in enumerate(g0[:2] + w0):
-            prep_pe(job)
-            prep_out(job, n in HV)
-            if n == 3:
-                th(0)
-            prep_q(job)
-        sq(0)
-        prep_pe(g0[2])
-        prep_pe(g0[3])
-        dg(0, 0)
-        dg(0, 1)
-        prep_out(g0[2])
-        wm(0)
-        th(1)
-        prep_out(g0[3])
-        sq(1)
-        dz(0, 0)
-        dz(0, 1)
-        prep_q(g0[3])
-        run([(prep_pe, job) for job in w1])
-        ix(0, 0)
-        wm(1)
-        dg(1, 0)
-        dg(1, 1)
-        qx(0, 0)
-        run([(prep_out, job) for job in w1] + [(th, 2)])
+        with tc.manual_schedule(engines={mybir.EngineType.DVE, mybir.EngineType.Activation}):
+            for n, job in enumerate(g0[:2] + w0):
+                prep_pe(job)
+                prep_out(job, n in HV)
+                if n == 3:
+                    th(0)
+                prep_q(job)
+            sq(0)
+            prep_pe(g0[2])
+            prep_pe(g0[3])
+            dg(0, 0)
+            dg(0, 1)
+            prep_out(g0[2])
+            wm(0)
+            th(1)
+            prep_out(g0[3])
+            sq(1)
+            dz(0, 0)
+            dz(0, 1)
+            prep_q(g0[3])
+            run([(prep_pe, job) for job in w1])
+            ix(0, 0)
+            wm(1)
+            dg(1, 0)
+            dg(1, 1)
+            qx(0, 0)
+            run([(prep_out, job) for job in w1] + [(th, 2)])
         prep = {0: w1, 2: w2, 3: q0, 4: g1[:2] + q1[:3], 5: g1[2:] + q1[3:]}
         jobs = {5: dx(0, 0)[:1] + dx(0, 1)[:1]}
         share = SHARE
-        back = {1: [(ix, 0, 1), (qx, 0, 1)], 2: [(iz, 0, 0), (qt, 0, 0)], 5: [(ix, 1, 0), (qx, 1, 0)]}
+        back = {1: [(iz, 0, 0), (qt, 0, 0)], 4: [(ix, 0, 1), (qx, 0, 1)], 5: [(ix, 1, 0), (qx, 1, 0)]}
         for k in range(1, 6):
             mine = prep.get(k, [])
             turns = [(tz, k - 1)] + [(prep_pe, job) for job in mine]

@@ -20,10 +20,12 @@ P = 128
 W = 512
 PIN = "PS"
 HV = (0, 2, 4)
-SHARE = {2: (1,), 3: (1, 3)}
+SHARE = {2: (1,), 3: (1, 3), 4: (1,)}
 E1 = ()
+E2 = (0,)
+E3 = 0
 ENDING = [(0, 0), (1, 0), (0, 1), (1, 1), (0, 2), (1, 2)]
-LEAD = 2
+HALVES = [("dw", 2, 3)]
 VSHARE = 3
 GATES = 5
 OUTS = 4
@@ -42,7 +44,7 @@ def tile_qwen3_5attention_pb_v_kernel(tc, hidden, wq, attn, wo, gate, gout, dx_o
 
     pairs = [[(0, 2 * a, c), (0, 2 * a + 1, c)] for c in range(3) for a in range(2)]
     pairs += [[(1, 2 * a, c), (1, 2 * a + 1, c)] for a, c in ENDING]
-    groups = [[0], [1], [2, 3], [4, 5], [6, 7], [8, 9], [10, 11]]
+    groups = [[0], [1], [2, 4], [3, 5], [6, 7], [8, 10], [9, 11]]
     group = {k: ks for ks in groups for k in ks}
     where = {s: (k, i) for k, pr in enumerate(pairs) for i, s in enumerate(pr)}
 
@@ -58,7 +60,7 @@ def tile_qwen3_5attention_pb_v_kernel(tc, hidden, wq, attn, wo, gate, gout, dx_o
         make_identity(nc, ident[:])
 
         free = {"bank": list(range(8)), "raw": list(range(4)), "big": list(range(3)), "gate": list(range(GATES)), "attn": list(range(3)),
-                "stage": list(range(7)), "es": list(range(4)), "dz": list(range(6)), "out": list(range(OUTS)), "xraw": list(range(2))}
+                "stage": list(range(7)), "es": list(range(4)), "dz": list(range(6)), "out": list(range(OUTS)), "xraw": list(range(1))}
         held = {}
         tiles = {}
 
@@ -119,8 +121,10 @@ def tile_qwen3_5attention_pb_v_kernel(tc, hidden, wq, attn, wo, gate, gout, dx_o
             src = at_v[g][:, j0:j1 + 1, W * c0:W * c1 + W]
             nc.sync.dma_start(out=take(("attn", k), "attn", 1024 * len(group[k]), BF16)[:].rearrange("p (j e) -> p j e", j=src.shape[1]), in_=src)
 
-        def load_x(g, h):
-            nc.sync.dma_start(out=take(("xraw", g, h), "xraw", 2048, BF16)[:].rearrange("p (j m) -> p j m", j=4), in_=x_v[g][:, :, W * h:W * h + W])
+        def load_x(g, hs):
+            src = x_v[g][:, :, W * hs[0]:W * hs[-1] + W]
+            raw = take(("xraw", g, hs[0]), "xraw" if len(hs) == 2 else "raw", 2048 * len(hs), BF16)
+            nc.sync.dma_start(out=raw[:].rearrange("p (j m) -> p j m", j=4), in_=src)
 
         def load_rows(key, kind, src):
             nc.sync.dma_start(out=take(key, kind, src.shape[1], BF16)[:], in_=src)
@@ -137,8 +141,8 @@ def tile_qwen3_5attention_pb_v_kernel(tc, hidden, wq, attn, wo, gate, gout, dx_o
         def lq(r):
             return ("big", load_rows, ("qraw", r), "big", wq_v[r])
 
-        def lx(g, h):
-            return ("xraw", load_x, g, h)
+        def lx(g, *hs):
+            return ("xraw" if len(hs) == 2 else "raw", load_x, g, hs)
 
         def le(k):
             return ("gate", load_gate, k)
@@ -146,9 +150,9 @@ def tile_qwen3_5attention_pb_v_kernel(tc, hidden, wq, attn, wo, gate, gout, dx_o
         def la(k):
             return ("attn", load_attn, k)
 
-        loads = [lg(0, 0), lw(0, 0), lw(0, 1), le(0), la(0), lg(0, 1), le(1), la(1), lx(0, 0), lw(1, 0), lw(1, 1), le(2), la(2), le(3)]
-        loads += [lw(2, 0), lw(2, 1), le(4), la(4), lq(0), le(5), lq(1), lx(0, 1), lg(1, 0), le(6), lq(2), la(6), lg(1, 1), le(7), lq(3), lx(1, 0), le(8), lx(1, 1)]
-        loads += [la(8), le(9), le(10), la(10), le(11)]
+        loads = [lg(0, 0), lw(0, 0), lw(0, 1), le(0), la(0), lg(0, 1), le(1), la(1), lw(1, 0), lx(0, 0), le(2), lw(1, 1), la(2), le(3), la(3)]
+        loads += [lw(2, 0), lw(2, 1), le(4), lq(0), le(5), lq(1), lx(0, 1), lg(1, 0), le(6), lq(2), la(6), lg(1, 1), le(7), lq(3), lx(1, 0, 1), le(8)]
+        loads += [la(8), le(9), la(9), le(10), le(11)]
 
         def pump():
             while loads and free[loads[0][0]]:
@@ -194,18 +198,21 @@ def tile_qwen3_5attention_pb_v_kernel(tc, hidden, wq, attn, wo, gate, gout, dx_o
                 give(stg)
 
         def interleave(dst, src):
-            nc.vector.tensor_copy(out=dst.rearrange("p (c i t) -> p c t i", i=4, t=4), in_=src.rearrange("p (t c i) -> p c t i", t=4, i=4))
+            nc.vector.tensor_copy(out=dst.rearrange("p (c i t) -> p c t i", i=4, t=4), in_=src.rearrange("p t (c i) -> p c t i", i=4))
 
-        def weave(src, stg):
-            interleave(take(stg, "stage", 2048, BF16)[:], tiles[src][:])
+        def weave(src, c0, stg):
+            interleave(take(stg, "stage", 2048, BF16)[:], tiles[src][:].rearrange("p (t m) -> p t m", t=4)[:, :, c0:c0 + W])
 
         def weave_q(stg, key, c0, fmt):
             quantize(key, c0, fmt, tiles[stg][:])
             give(stg)
 
         def ix(g, h):
-            weave(("xraw", g, h), ("xs", g, h))
-            give(("xraw", g, h))
+            if g == 0:
+                weave(("xraw", g, h), 0, ("xs", g, h))
+                give(("xraw", g, h))
+            else:
+                weave(("xraw", g, 0), W * h, ("xs", g, h))
 
         def qx(g, h):
             weave_q(("xs", g, h), ("x", g), W * h, E4M3)
@@ -218,7 +225,7 @@ def tile_qwen3_5attention_pb_v_kernel(tc, hidden, wq, attn, wo, gate, gout, dx_o
                 give(key)
 
         def iz(g, c):
-            weave(("dz", g, c), ("ts", g, c))
+            weave(("dz", g, c), 0, ("ts", g, c))
             used(("dz", g, c), 5)
 
         def qt(g, c):
@@ -294,7 +301,9 @@ def tile_qwen3_5attention_pb_v_kernel(tc, hidden, wq, attn, wo, gate, gout, dx_o
                 nc.scalar.activation(out=to, in_=src, func=ACT.Copy, scale=-1.0)
             give(job)
             uses[o] = uses.get(o, 0) + 1
-            if uses[o] == 2:
+            if (kind, a, b) in HALVES:
+                nc.sync.dma_start(out=dw_v[b][:, half, W * a:W * a + W], in_=tiles[o][:, W * half:W * half + W])
+            elif uses[o] == 2:
                 if kind == "dx":
                     nc.sync.dma_start(out=dx_v[a, b], in_=tiles[o][:])
                 else:
@@ -374,13 +383,14 @@ def tile_qwen3_5attention_pb_v_kernel(tc, hidden, wq, attn, wo, gate, gout, dx_o
             dz(0, 0)
             dz(0, 1)
             prep_q(g0[3])
-            run([(prep_pe, job) for job in w1])
+            run([(prep_pe, job) for job in w1[:2]])
             ix(0, 0)
             wm(1)
             dg(1, 0)
             dg(1, 1)
+            run([(prep_pe, job) for job in w1[2:]])
             qx(0, 0)
-            run([(prep_out, job) for job in w1] + [(th, 2)])
+            run([(prep_out, job) for job in w1[:2]] + [(th, 2)] + [(prep_out, job) for job in w1[2:]])
         prep = {0: w1, 2: w2, 3: q0, 4: g1[:2] + q1[:3], 5: g1[2:] + q1[3:]}
         jobs = {5: dx(0, 0)[:1] + dx(0, 1)[:1]}
         share = SHARE
@@ -451,47 +461,51 @@ def tile_qwen3_5attention_pb_v_kernel(tc, hidden, wq, attn, wo, gate, gout, dx_o
         outs2(dw(0)[2:4])
         iz(0, 1)
         sq(10)
-        dz(9, 0)
-        dz(9, 1)
-        outs2(dw(0)[4:], None, E1)
-        iz(1, 1)
-        qt(0, 1)
-        dg(10, 0)
-        dg(10, 1)
-        tz(7)
-        tz(8)
-        qt(1, 1)
-        wm(10)
-        th(11)
-        cz(7)
-        sq(11)
-        cz(8)
-        opens(dw(1)[:2], [0])
-        dz(10, 0)
-        dz(10, 1)
-        outs2(dw(1)[:2], [1])
-        dg(11, 0)
-        dg(11, 1)
-        qe(6)
-        wm(11)
-        tz(9)
-        tz(10)
-        qe(7)
-        qe(8)
-        cz(9)
-        cz(10)
-        outs2(dw(1)[2:4])
-        dz(11, 0)
-        dz(11, 1)
-        qe(9)
-        qe(10)
-        outs2(dw(1)[4:])
-        iz(0, 2)
-        tz(11)
-        iz(1, 2)
-        cz(11)
-        outs2(dx(1, 0))
-        qt(0, 2)
-        qt(1, 2)
-        qe(11)
-        outs2(dx(1, 1) + dx(1, 2) + dw(2) + dx(1, 3), None, range(1, 14, 2))
+        with tc.manual_schedule(engines={mybir.EngineType.DVE}):
+            dz(9, 0)
+            dz(9, 1)
+            outs2(dw(0)[4:], None, E1)
+            qe(6)
+            iz(1, 1)
+            qt(0, 1)
+            dg(10, 0)
+            dg(10, 1)
+            qt(1, 1)
+            wm(10)
+            tz(7)
+            tz(8)
+            opens(dw(1)[:2], [0])
+            th(11)
+            cz(7)
+            dz(10, 0)
+            dz(10, 1)
+            cz(8)
+            sq(11)
+            outs2(dw(1)[:2], [1], E2)
+            dg(11, 0)
+            dg(11, 1)
+            tz(9)
+            tz(10)
+            qe(7)
+            qe(8)
+            cz(9)
+            cz(10)
+            wm(11)
+            outs2(dw(1)[2:4])
+            qe(9)
+            dz(11, 0)
+            dz(11, 1)
+            qe(10)
+            outs2(dw(1)[4:6])
+            iz(0, 2)
+            opens(dw(1)[6:], [0, 1])
+            tz(11)
+            out_copy(dw(1)[6], False)
+            cz(11)
+            out_copy(dw(1)[7], False)
+            iz(1, 2)
+            qe(11)
+            outs2(dx(1, 0) + dx(1, 1))
+            qt(0, 2)
+            qt(1, 2)
+            outs2(dx(1, 2) + dx(1, 3) + dw(2), None, range(E3, 14, 2))

@@ -29,6 +29,7 @@ HALVES = [("dw", 2, 3)]
 VSHARE = 3
 GATES = 5
 OUTS = 4
+SPARE = ("out", "raw", "big", "xraw", "attn", "gate", "dz")
 
 
 def tile_qwen3_5attention_pb_v_kernel(tc, hidden, wq, attn, wo, gate, gout, dx_out, dw_out):
@@ -213,6 +214,7 @@ def tile_qwen3_5attention_pb_v_kernel(tc, hidden, wq, attn, wo, gate, gout, dx_o
                 give(("xraw", g, h))
             else:
                 weave(("xraw", g, 0), W * h, ("xs", g, h))
+                used(("xraw", g, 0), 2)
 
         def qx(g, h):
             weave_q(("xs", g, h), ("x", g), W * h, E4M3)
@@ -291,7 +293,7 @@ def tile_qwen3_5attention_pb_v_kernel(tc, hidden, wq, attn, wo, gate, gout, dx_o
             kind, a, b, half = job
             o = ("o", kind, a, b)
             if o not in tiles:
-                take(o, "out", 1024, F32)
+                take(o, [s for s in SPARE if free[s] and all(job[0] != s for job in loads)][0], 1024, F32)
             to, src = tiles[o][:, W * half:W * half + W], tiles[job][:]
             if kind == "dw":
                 to, src = to.rearrange("p (m u i) -> p m u i", u=2, i=2), src.rearrange("p (u m i) -> p m u i", u=2, i=2)
@@ -308,7 +310,6 @@ def tile_qwen3_5attention_pb_v_kernel(tc, hidden, wq, attn, wo, gate, gout, dx_o
                     nc.sync.dma_start(out=dx_v[a, b], in_=tiles[o][:])
                 else:
                     nc.sync.dma_start(out=dw_v[b][:, :, W * a:W * a + W], in_=tiles[o][:].rearrange("p (i e) -> p i e", i=2))
-                give(o)
 
         def tg(g):
             return [("g", g, a, h) for a in range(2) for h in range(2)]
@@ -508,4 +509,4 @@ def tile_qwen3_5attention_pb_v_kernel(tc, hidden, wq, attn, wo, gate, gout, dx_o
             outs2(dx(1, 0) + dx(1, 1))
             qt(0, 2)
             qt(1, 2)
-            outs2(dx(1, 2) + dx(1, 3) + dw(2), None, range(E3, 14, 2))
+            outs2(dx(1, 2) + dw(2)[:6] + dx(1, 3) + dw(2)[6:], None, range(E3, 14, 2))

@@ -20,15 +20,21 @@ P = 128
 W = 512
 PIN = "PS"
 HV = (0, 2, 4)
-SHARE = {2: (1,), 3: (1, 3), 4: (1,)}
+SHARE = {5: (1,)}
 E1 = ()
-E2 = (0,)
+E2 = ()
 E3 = 0
+E4 = ()
+E5 = ()
+E6 = False
+E7 = ()
 ENDING = [(0, 0), (1, 0), (0, 1), (1, 1), (0, 2), (1, 2)]
 HALVES = [("dw", 2, 3)]
 VSHARE = 3
 GATES = 5
 OUTS = 4
+NEWEST = [("ts", 0, 1), ("xs", 0, 0), ("xs", 0, 1)]
+HW = (1, 2, 3)
 SPARE = ("out", "raw", "big", "xraw", "attn", "gate", "dz")
 
 
@@ -43,9 +49,10 @@ def tile_qwen3_5attention_pb_v_kernel(tc, hidden, wq, attn, wo, gate, gout, dx_o
     dx_v = dx_out.rearrange("b s m -> (b s) m").rearrange("(g p j) m -> g j p m", g=2, j=4)
     dw_v = dw_out.rearrange("m u h -> m (u h)").rearrange("(t i q) e -> t q i e", i=2, q=P)
 
-    pairs = [[(0, 2 * a, c), (0, 2 * a + 1, c)] for c in range(3) for a in range(2)]
+    pairs = [[(0, 2 * a, 0), (0, 2 * a + 1, 0)] for a in range(2)]
+    pairs += [[(0, j, 1), (0, j, 2)] for j in range(4)]
     pairs += [[(1, 2 * a, c), (1, 2 * a + 1, c)] for a, c in ENDING]
-    groups = [[0], [1], [2, 4], [3, 5], [6, 7], [8, 10], [9, 11]]
+    groups = [[0], [1], [2, 3], [4, 5], [6, 7], [8, 10], [9, 11]]
     group = {k: ks for ks in groups for k in ks}
     where = {s: (k, i) for k, pr in enumerate(pairs) for i, s in enumerate(pr)}
 
@@ -66,7 +73,7 @@ def tile_qwen3_5attention_pb_v_kernel(tc, hidden, wq, attn, wo, gate, gout, dx_o
         tiles = {}
 
         def take(key, kind, cols, dtype):
-            slot = free[kind].pop(0)
+            slot = free[kind].pop(-1 if key in NEWEST else 0)
             held[key] = (kind, slot)
             if kind == "bank":
                 tiles[key] = ps.tile([P, cols], dtype, name="bank%d" % slot)
@@ -151,9 +158,8 @@ def tile_qwen3_5attention_pb_v_kernel(tc, hidden, wq, attn, wo, gate, gout, dx_o
         def la(k):
             return ("attn", load_attn, k)
 
-        loads = [lg(0, 0), lw(0, 0), lw(0, 1), le(0), la(0), lg(0, 1), le(1), la(1), lw(1, 0), lx(0, 0), le(2), lw(1, 1), la(2), le(3), la(3)]
-        loads += [lw(2, 0), lw(2, 1), le(4), lq(0), le(5), lq(1), lx(0, 1), lg(1, 0), le(6), lq(2), la(6), lg(1, 1), le(7), lq(3), lx(1, 0, 1), le(8)]
-        loads += [la(8), le(9), la(9), le(10), le(11)]
+        loads = [lg(0, 0), lw(0, 0), lw(0, 1), le(0), la(0), lg(0, 1), le(1), la(1), lw(1, 0), lw(1, 1), le(2), lw(2, 0), lw(2, 1), la(2), le(3)]
+        loads += [lx(0, 0, 1), lq(0), le(4), la(4), lq(1), le(5), lg(1, 0), lg(1, 1), le(6), lq(2), la(6), lq(3), le(7), lx(1, 0, 1), le(8), la(8), le(9), la(9), le(10), le(11)]
 
         def pump():
             while loads and free[loads[0][0]]:
@@ -209,7 +215,7 @@ def tile_qwen3_5attention_pb_v_kernel(tc, hidden, wq, attn, wo, gate, gout, dx_o
             give(stg)
 
         def ix(g, h):
-            if g == 0:
+            if ("xraw", g, 1) in tiles or (h == 0 and tiles["xraw", g, 0].shape[1] == 2048):
                 weave(("xraw", g, h), 0, ("xs", g, h))
                 give(("xraw", g, h))
             else:
@@ -243,8 +249,9 @@ def tile_qwen3_5attention_pb_v_kernel(tc, hidden, wq, attn, wo, gate, gout, dx_o
 
         def wm(k):
             (g, j0, c0), (g1, j1, c1), (g2, j, c) = pairs[group[k][0]][0], pairs[group[k][-1]][1], pairs[k][0]
-            ga = tiles["gate", k][:].rearrange("p (j e) -> p j e", j=2)
-            at = tiles["attn", group[k][0]][:].rearrange("p (j e) -> p j e", j=j1 - j0 + 1)[:, j - j0:j - j0 + 2, W * (c - c0):W * (c - c0) + W]
+            rows = pairs[k][1][1] - j + 1
+            ga = tiles["gate", k][:].rearrange("p (j e) -> p j e", j=rows)
+            at = tiles["attn", group[k][0]][:].rearrange("p (j e) -> p j e", j=j1 - j0 + 1)[:, j - j0:j - j0 + rows, W * (c - c0):W * (c - c0) + 1024 // rows]
             nc.vector.scalar_tensor_tensor(out=ga, in0=ga, scalar=0.25, in1=at,
                                            op0=ALU.subtract, op1=ALU.mult)
             used(("attn", group[k][0]), len(group[k]))
@@ -372,35 +379,48 @@ def tile_qwen3_5attention_pb_v_kernel(tc, hidden, wq, attn, wo, gate, gout, dx_o
                     th(0)
                 prep_q(job)
             sq(0)
-            prep_pe(g0[2])
-            prep_pe(g0[3])
             dg(0, 0)
             dg(0, 1)
-            prep_out(g0[2])
+            run([(prep_pe, job) for job in g0[2:] + w1])
             wm(0)
             th(1)
-            prep_out(g0[3])
-            sq(1)
             dz(0, 0)
+            sq(1)
             dz(0, 1)
-            prep_q(g0[3])
-            run([(prep_pe, job) for job in w1[:2]])
-            ix(0, 0)
+            prep_out(g0[2])
+            prep_out(g0[3])
             wm(1)
+            prep_q(g0[3])
             dg(1, 0)
             dg(1, 1)
-            run([(prep_pe, job) for job in w1[2:]])
-            qx(0, 0)
-            run([(prep_out, job) for job in w1[:2]] + [(th, 2)] + [(prep_out, job) for job in w1[2:]])
-        prep = {0: w1, 2: w2, 3: q0, 4: g1[:2] + q1[:3], 5: g1[2:] + q1[3:]}
+            run([(prep_out, job, n in HW) for n, job in enumerate(w1)])
+            run([(prep_pe, job) for job in w2[:2]])
+            tz(0)
+            th(2)
+            run([(prep_q, job) for job in w1])
+            sq(2)
+            dz(1, 0)
+            dz(1, 1)
+            run([(prep_out, job) for job in w2[:2]] + [(cz, 0)])
+            dg(2, 0)
+            run([(prep_pe, job) for job in w2[2:]] + [(prep_out, job) for job in w2[2:]])
+            wm(2)
+            iz(0, 0)
+            run([(prep_q, job) for job in w2])
+            dg(2, 1)
+            qe(0)
+            qt(0, 0)
+            th(3)
+            sq(3)
+        prep = {2: q0[:3], 3: q0[3:], 4: g1, 5: q1}
         jobs = {5: dx(0, 0)[:1] + dx(0, 1)[:1]}
         share = SHARE
-        back = {1: [(iz, 0, 0), (qt, 0, 0)], 4: [(ix, 0, 1), (qx, 0, 1)], 5: [(ix, 1, 0), (qx, 1, 0)]}
-        for k in range(1, 6):
+        back = {2: [(ix, 0, 0), (qx, 0, 0)], 3: [(ix, 0, 1), (qx, 0, 1)], 5: [(ix, 1, 0), (qx, 1, 0)]}
+        for k in range(2, 6):
             mine = prep.get(k, [])
             turns = [(tz, k - 1)] + [(prep_pe, job) for job in mine]
             drains = [(cz, k - 1)] + [(prep_out, job, n in share.get(k, ())) for n, job in enumerate(mine)]
-            cut = (len(turns) + 1) // 2
+            cut = max(3, (len(turns) + 1) // 2)
             run(turns[:cut])
             quants = [(prep_q, job) for job in prep.get(k - 1, [])]
             run(quants[-3:])
@@ -408,7 +428,7 @@ def tile_qwen3_5attention_pb_v_kernel(tc, hidden, wq, attn, wo, gate, gout, dx_o
             run(quants[:-3])
             dz(k, 1)
             acts = [(th, k + 2), (sq, k + 2)]
-            mix = drains[:2] + zipped(acts, drains[2:]) if mine else [(sq, 2), (cz, 0)] + acts
+            mix = drains[:2] + zipped(acts, drains[2:]) if mine else zipped(acts, drains)
             run(mix[:2])
             dg(k + 1, 0)
             run(mix[2:4])
@@ -422,7 +442,7 @@ def tile_qwen3_5attention_pb_v_kernel(tc, hidden, wq, attn, wo, gate, gout, dx_o
             run(todo[1:])
             outs2(jobs.get(k, []))
         tz(5)
-        run([(prep_q, job) for job in g1[2:] + q1[3:4]])
+        run([(prep_q, job) for job in q1[3:4]])
         dz(6, 0)
         cz(5)
         run([(prep_q, job) for job in q1[4:]])
@@ -480,33 +500,37 @@ def tile_qwen3_5attention_pb_v_kernel(tc, hidden, wq, attn, wo, gate, gout, dx_o
             cz(7)
             dz(10, 0)
             dz(10, 1)
-            cz(8)
+            outs2(dw(1)[:2], [1])
             sq(11)
-            outs2(dw(1)[:2], [1], E2)
+            cz(8)
             dg(11, 0)
             dg(11, 1)
+            opens(dw(1)[2:4], [0, 1])
+            out_copy(dw(1)[2], True)
+            qe(7)
+            out_copy(dw(1)[3], True)
             tz(9)
             tz(10)
-            qe(7)
+            wm(11)
             qe(8)
             cz(9)
             cz(10)
-            wm(11)
-            outs2(dw(1)[2:4])
             qe(9)
             dz(11, 0)
-            dz(11, 1)
             qe(10)
-            outs2(dw(1)[4:6])
-            iz(0, 2)
+            dz(11, 1)
+            outs2(dw(1)[4:6], None, E5)
             opens(dw(1)[6:], [0, 1])
-            tz(11)
-            out_copy(dw(1)[6], False)
-            cz(11)
+            out_copy(dw(1)[6], E6)
             out_copy(dw(1)[7], False)
-            iz(1, 2)
+            opens(dx(1, 0)[:1], [0, 1, 2])
+            tz(11)
+            iz(0, 2)
+            out_copy(dx(1, 0)[0], False)
+            cz(11)
             qe(11)
-            outs2(dx(1, 0) + dx(1, 1))
+            iz(1, 2)
+            outs2(dx(1, 0)[1:] + dx(1, 1), None, E7)
             qt(0, 2)
             qt(1, 2)
             outs2(dx(1, 2) + dw(2)[:6] + dx(1, 3) + dw(2)[6:], None, range(E3, 14, 2))

@@ -15,27 +15,14 @@ E4M3 = mybir.dt.float8_e4m3fn_x4
 E5M2 = mybir.dt.float8_e5m2_x4
 ALU = mybir.AluOpType
 ACT = mybir.ActivationFunctionType
+PE, SP, VECTOR, SCALAR = mybir.EngineType.PE, mybir.EngineType.SP, mybir.EngineType.DVE, mybir.EngineType.Activation
 
 P = 128
 W = 512
-PIN = "PS"
-HV = (0, 2, 4)
-SHARE = {5: (1,)}
-E1 = ()
-E2 = ()
-E3 = 0
-E4 = ()
-E5 = ()
-E6 = False
-E7 = ()
-ENDING = [(0, 0), (1, 0), (0, 1), (1, 1), (0, 2), (1, 2)]
-HALVES = [("dw", 2, 3)]
-VSHARE = 3
-GATES = 5
-OUTS = 4
-NEWEST = [("ts", 0, 1), ("xs", 0, 0), ("xs", 0, 1)]
-HW = (1, 2, 3)
-SPARE = ("out", "raw", "big", "xraw", "attn", "gate", "dz")
+
+SLOTS = {"bank": 8, "raw": 4, "big": 3, "gate": 5, "attn": 3, "stage": 7, "es": 4, "dz": 6, "out": 4, "xraw": 1}
+SPENT = ("out", "raw", "big", "xraw", "attn", "gate", "dz")
+FREED_LAST = [("ts", 0, 1), ("xs", 0, 0), ("xs", 0, 1)]
 
 
 def tile_qwen3_5attention_pb_v_kernel(tc, hidden, wq, attn, wo, gate, gout, dx_out, dw_out):
@@ -51,29 +38,23 @@ def tile_qwen3_5attention_pb_v_kernel(tc, hidden, wq, attn, wo, gate, gout, dx_o
 
     pairs = [[(0, 2 * a, 0), (0, 2 * a + 1, 0)] for a in range(2)]
     pairs += [[(0, j, 1), (0, j, 2)] for j in range(4)]
-    pairs += [[(1, 2 * a, c), (1, 2 * a + 1, c)] for a, c in ENDING]
-    groups = [[0], [1], [2, 3], [4, 5], [6, 7], [8, 10], [9, 11]]
-    group = {k: ks for ks in groups for k in ks}
-    where = {s: (k, i) for k, pr in enumerate(pairs) for i, s in enumerate(pr)}
+    pairs += [[(1, 2 * a, c), (1, 2 * a + 1, c)] for c in range(3) for a in range(2)]
+    where = {slot: (k, i) for k, pair in enumerate(pairs) for i, slot in enumerate(pair)}
+    shared = {k: ks for ks in [[0], [1], [2, 3], [4, 5], [6, 7], [8, 10], [9, 11]] for k in ks}
 
     with ExitStack() as ctx:
         sb = ctx.enter_context(tc.tile_pool(name="sb", bufs=1))
         ps = ctx.enter_context(tc.psum_pool(name="ps", bufs=1))
-        if PIN == "all":
-            ctx.enter_context(tc.manual_schedule())
-        else:
-            ctx.enter_context(tc.manual_schedule(engines={mybir.EngineType.PE, mybir.EngineType.SP}))
+        ctx.enter_context(tc.manual_schedule(engines={PE, SP}))
 
         ident = sb.tile([P, P], F32, name="ident")
         make_identity(nc, ident[:])
 
-        free = {"bank": list(range(8)), "raw": list(range(4)), "big": list(range(3)), "gate": list(range(GATES)), "attn": list(range(3)),
-                "stage": list(range(7)), "es": list(range(4)), "dz": list(range(6)), "out": list(range(OUTS)), "xraw": list(range(1))}
-        held = {}
-        tiles = {}
+        free = {kind: list(range(n)) for kind, n in SLOTS.items()}
+        held, tiles, reads = {}, {}, {}
 
         def take(key, kind, cols, dtype):
-            slot = free[kind].pop(-1 if key in NEWEST else 0)
+            slot = free[kind].pop(-1 if key in FREED_LAST else 0)
             held[key] = (kind, slot)
             if kind == "bank":
                 tiles[key] = ps.tile([P, cols], dtype, name="bank%d" % slot)
@@ -84,7 +65,12 @@ def tile_qwen3_5attention_pb_v_kernel(tc, hidden, wq, attn, wo, gate, gout, dx_o
         def give(key):
             kind, slot = held.pop(key)
             free[kind].append(slot)
-            pump()
+            issue_loads()
+
+        def read(key, readers):
+            reads[key] = reads.get(key, 0) + 1
+            if reads[key] == readers:
+                give(key)
 
         def codes(key, cols):
             tiles[key, "c"] = sb.tile([P, cols], U32, name="c_%s%d" % key, align_bytes=64)
@@ -101,160 +87,130 @@ def tile_qwen3_5attention_pb_v_kernel(tc, hidden, wq, attn, wo, gate, gout, dx_o
         for k in range(6):
             codes(("t", k), W)
 
-        def quantize(key, c0, fmt, src):
-            n = src.shape[1] // 4
-            nc.vector.quantize_mx(out=tiles[key, "c"][:, c0:c0 + n].bitcast(fmt), scales=tiles[key, "s"][:, c0:c0 + n], in_=src)
+        def quantize(key, c0, fmt, stage):
+            n = tiles[stage].shape[1] // 4
+            nc.vector.quantize_mx(out=tiles[key, "c"][:, c0:c0 + n].bitcast(fmt), scales=tiles[key, "s"][:, c0:c0 + n],
+                                  in_=tiles[stage][:])
+            give(stage)
 
         def mx(acc, a, a0, afmt, b, b0, bfmt, start, stop):
             nc.tensor.matmul_mx(out=acc, lhsT=tiles[a, "c"][:, a0:a0 + P].bitcast(afmt), lhsT_scale=tiles[a, "s"][:, a0:a0 + P],
                                 rhs=tiles[b, "c"][:, b0:b0 + W].bitcast(bfmt), rhs_scale=tiles[b, "s"][:, b0:b0 + W],
                                 start=start, stop=stop)
 
-        def copy(on_vector, out, in_):
-            if on_vector:
-                nc.vector.tensor_copy(out=out, in_=in_)
-            else:
-                nc.scalar.copy(out=out, in_=in_)
-
-        def span(k, view):
-            (g, j0, c0), (g1, j1, c1) = pairs[k]
+        def span(view, first, last):
+            (g, j0, c0), (g, j1, c1) = first, last
             return view[g][:, j0:j1 + 1, W * c0:W * c1 + W]
 
-        def load_gate(k):
-            src = span(k, ga_v)
-            nc.sync.dma_start(out=take(("gate", k), "gate", 1024, F32)[:].rearrange("p (j e) -> p j e", j=src.shape[1]), in_=src)
+        def go(g, a):
+            return ("raw", ("graw", g, a), g_v[g, a])
 
-        def load_attn(k):
-            (g, j0, c0), (g1, j1, c1) = pairs[k][0], pairs[group[k][-1]][1]
-            src = at_v[g][:, j0:j1 + 1, W * c0:W * c1 + W]
-            nc.sync.dma_start(out=take(("attn", k), "attn", 1024 * len(group[k]), BF16)[:].rearrange("p (j e) -> p j e", j=src.shape[1]), in_=src)
+        def wo_rows(c, a):
+            return ("raw", ("wraw", c, a), wo_v[c, a])
 
-        def load_x(g, hs):
-            src = x_v[g][:, :, W * hs[0]:W * hs[-1] + W]
-            raw = take(("xraw", g, hs[0]), "xraw" if len(hs) == 2 else "raw", 2048 * len(hs), BF16)
-            nc.sync.dma_start(out=raw[:].rearrange("p (j m) -> p j m", j=4), in_=src)
+        def wq_rows(r):
+            return ("big", ("qraw", r), wq_v[r])
 
-        def load_rows(key, kind, src):
-            nc.sync.dma_start(out=take(key, kind, src.shape[1], BF16)[:], in_=src)
+        def hid(g):
+            return ("xraw", ("xraw", g), x_v[g])
 
-        def ew(k):
-            return [("gate", load_gate, k)] + ([("attn", load_attn, k)] if k % 2 == 0 else [])
+        def ga(k):
+            return ("gate", ("gate", k), span(ga_v, *pairs[k]))
 
-        def lg(g, a):
-            return ("raw", load_rows, ("graw", g, a), "raw", g_v[g, a])
+        def at(k):
+            return ("attn", ("attn", k), span(at_v, pairs[k][0], pairs[shared[k][-1]][1]))
 
-        def lw(c, a):
-            return ("raw", load_rows, ("wraw", c, a), "raw", wo_v[c, a])
+        loads = [go(0, 0), wo_rows(0, 0), wo_rows(0, 1), ga(0), at(0), go(0, 1), ga(1), at(1)]
+        loads += [wo_rows(1, 0), wo_rows(1, 1), ga(2), wo_rows(2, 0), wo_rows(2, 1), at(2), ga(3)]
+        loads += [hid(0), wq_rows(0), ga(4), at(4), wq_rows(1), ga(5), go(1, 0), go(1, 1), ga(6)]
+        loads += [wq_rows(2), at(6), wq_rows(3), ga(7), hid(1), ga(8), at(8), ga(9), at(9), ga(10), ga(11)]
 
-        def lq(r):
-            return ("big", load_rows, ("qraw", r), "big", wq_v[r])
-
-        def lx(g, *hs):
-            return ("xraw" if len(hs) == 2 else "raw", load_x, g, hs)
-
-        def le(k):
-            return ("gate", load_gate, k)
-
-        def la(k):
-            return ("attn", load_attn, k)
-
-        loads = [lg(0, 0), lw(0, 0), lw(0, 1), le(0), la(0), lg(0, 1), le(1), la(1), lw(1, 0), lw(1, 1), le(2), lw(2, 0), lw(2, 1), la(2), le(3)]
-        loads += [lx(0, 0, 1), lq(0), le(4), la(4), lq(1), le(5), lg(1, 0), lg(1, 1), le(6), lq(2), la(6), lq(3), le(7), lx(1, 0, 1), le(8), la(8), le(9), la(9), le(10), le(11)]
-
-        def pump():
+        def issue_loads():
             while loads and free[loads[0][0]]:
-                job = loads.pop(0)
-                job[1](*job[2:])
+                kind, key, src = loads.pop(0)
+                dtype = F32 if kind == "gate" else BF16
+                if len(src.shape) == 2:
+                    nc.sync.dma_start(out=take(key, kind, src.shape[1], dtype)[:], in_=src)
+                else:
+                    to = take(key, kind, src.shape[1] * src.shape[2], dtype)
+                    nc.sync.dma_start(out=to[:].rearrange("p (j e) -> p j e", j=src.shape[1]), in_=src)
 
-        def turn(bank, srcs, sorted_words=False):
+        def turn(bank, halves):
             b = take(bank, "bank", W, F32)
-            for i, words in enumerate(srcs):
-                for u in range(2):
-                    src = words[:, P * u:P * u + P] if sorted_words else words[:, u:256:2]
-                    nc.tensor.transpose(b[:, 256 * i + P * u:256 * i + P * u + P], src, ident[:])
+            for n, words in enumerate(halves):
+                nc.tensor.transpose(b[:, P * n:P * n + P], words, ident[:])
 
         def unturn(bank, to, rows_apart, on_vector):
             src = tiles[bank][:].rearrange("p (i u n) -> p i n u", i=2, u=2)
             if rows_apart:
-                copy(on_vector, to.bitcast(F32).rearrange("p (i n u) -> p i n u", i=2, u=2), src)
+                to = to.bitcast(F32).rearrange("p (i n u) -> p i n u", i=2, u=2)
             else:
-                copy(on_vector, to.bitcast(F32).rearrange("p (n i u) -> p n i u", i=2, u=2), src.rearrange("p i n u -> p n i u"))
+                to, src = to.bitcast(F32).rearrange("p (n i u) -> p n i u", i=2, u=2), src.rearrange("p i n u -> p n i u")
+            if on_vector:
+                nc.vector.tensor_copy(out=to, in_=src)
+            else:
+                nc.scalar.copy(out=to, in_=src)
             give(bank)
 
-        def prep_pe(job):
+        def turn_in(job):
             kind, a, b, h = job
             raw = {"g": ("graw", a, b), "w": ("wraw", a, b), "q": ("qraw", 2 * a + b)}[kind]
-            row = 768 if kind == "q" else 512
+            passes = 3 if kind == "q" else 2
             words = tiles[raw][:].bitcast(F32)
-            turn(job, [words[:, row * i + 256 * h:row * i + 256 * h + 256] for i in range(2)])
-            if h == (2 if kind == "q" else 1):
+            rows = [words[:, 256 * (passes * i + h):256 * (passes * i + h) + 256] for i in range(2)]
+            turn(job, [row[:, u:256:2] for row in rows for u in range(2)])
+            if h == passes - 1:
                 give(raw)
 
-        def prep_out(job, on_vector=False):
+        def staged(job):
             kind, a, b, h = job
-            stg, half = (("stg", kind, a, b), h) if kind == "g" else (("stg", kind, a, h), b)
+            return (("stg", kind, a, b), h) if kind == "g" else (("stg", kind, a, h), b)
+
+        def copy_in(job, on_vector=False):
+            stage, half = staged(job)
             if half == 0:
-                take(stg, "stage", 2048, BF16)
-            unturn(job, tiles[stg][:, 1024 * half:1024 * half + 1024], kind == "g", on_vector)
+                take(stage, "stage", 2048, BF16)
+            unturn(job, tiles[stage][:, 1024 * half:1024 * half + 1024], job[0] == "g", on_vector)
 
-        def prep_q(job):
-            kind, a, b, h = job
-            stg, half = (("stg", kind, a, b), h) if kind == "g" else (("stg", kind, a, h), b)
+        def quant_in(job):
+            stage, half = staged(job)
             if half == 1:
-                quantize((kind, a), W * stg[3], E5M2 if kind == "g" else E4M3, tiles[stg][:])
-                give(stg)
+                quantize(job[:2], W * stage[3], E5M2 if job[0] == "g" else E4M3, stage)
 
-        def interleave(dst, src):
-            nc.vector.tensor_copy(out=dst.rearrange("p (c i t) -> p c t i", i=4, t=4), in_=src.rearrange("p t (c i) -> p c t i", i=4))
+        def weave(src, c0, stage):
+            rows = tiles[src][:].rearrange("p (t m) -> p t m", t=4)[:, :, c0:c0 + W]
+            nc.vector.tensor_copy(out=take(stage, "stage", 2048, BF16)[:].rearrange("p (c i t) -> p c t i", i=8, t=4),
+                                  in_=rows.rearrange("p t (c i) -> p c t i", i=8))
 
-        def weave(src, c0, stg):
-            interleave(take(stg, "stage", 2048, BF16)[:], tiles[src][:].rearrange("p (t m) -> p t m", t=4)[:, :, c0:c0 + W])
+        def weave_x(g, h):
+            weave(("xraw", g), W * h, ("xs", g, h))
+            read(("xraw", g), 2)
 
-        def weave_q(stg, key, c0, fmt):
-            quantize(key, c0, fmt, tiles[stg][:])
-            give(stg)
+        def quant_x(g, h):
+            quantize(("x", g), W * h, E4M3, ("xs", g, h))
 
-        def ix(g, h):
-            if ("xraw", g, 1) in tiles or (h == 0 and tiles["xraw", g, 0].shape[1] == 2048):
-                weave(("xraw", g, h), 0, ("xs", g, h))
-                give(("xraw", g, h))
-            else:
-                weave(("xraw", g, 0), W * h, ("xs", g, h))
-                used(("xraw", g, 0), 2)
-
-        def qx(g, h):
-            weave_q(("xs", g, h), ("x", g), W * h, E4M3)
-
-        uses = {}
-
-        def used(key, n):
-            uses[key] = uses.get(key, 0) + 1
-            if uses[key] == n:
-                give(key)
-
-        def iz(g, c):
+        def weave_dz(g, c):
             weave(("dz", g, c), 0, ("ts", g, c))
-            used(("dz", g, c), 5)
+            read(("dz", g, c), 5)
 
-        def qt(g, c):
-            weave_q(("ts", g, c), ("t", 3 * g + c), 0, E5M2)
+        def quant_tokens(g, c):
+            quantize(("t", 3 * g + c), 0, E5M2, ("ts", g, c))
 
-        def th(k):
-            ga = tiles["gate", k]
-            nc.scalar.activation(out=ga[:], in_=ga[:], func=ACT.Tanh, scale=0.5)
+        def tanh(k):
+            nc.scalar.activation(out=tiles["gate", k][:], in_=tiles["gate", k][:], func=ACT.Tanh, scale=0.5)
 
-        def sq(k):
-            ga = tiles["gate", k]
-            nc.scalar.activation(out=ga[:], in_=ga[:], func=ACT.Square, scale=0.5)
+        def square(k):
+            nc.scalar.activation(out=tiles["gate", k][:], in_=tiles["gate", k][:], func=ACT.Square, scale=0.5)
 
-        def wm(k):
-            (g, j0, c0), (g1, j1, c1), (g2, j, c) = pairs[group[k][0]][0], pairs[group[k][-1]][1], pairs[k][0]
+        def factor(k):
+            first, last = shared[k][0], shared[k][-1]
+            (g, j0, c0), j1, (g, j, c) = pairs[first][0], pairs[last][1][1], pairs[k][0]
             rows = pairs[k][1][1] - j + 1
-            ga = tiles["gate", k][:].rearrange("p (j e) -> p j e", j=rows)
-            at = tiles["attn", group[k][0]][:].rearrange("p (j e) -> p j e", j=j1 - j0 + 1)[:, j - j0:j - j0 + rows, W * (c - c0):W * (c - c0) + 1024 // rows]
-            nc.vector.scalar_tensor_tensor(out=ga, in0=ga, scalar=0.25, in1=at,
-                                           op0=ALU.subtract, op1=ALU.mult)
-            used(("attn", group[k][0]), len(group[k]))
+            q = tiles["gate", k][:].rearrange("p (j e) -> p j e", j=rows)
+            a = tiles["attn", first][:].rearrange("p (j e) -> p j e", j=j1 - j0 + 1)
+            nc.vector.scalar_tensor_tensor(out=q, in0=q, scalar=0.25, op0=ALU.subtract, op1=ALU.mult,
+                                           in1=a[:, j - j0:j - j0 + rows, W * (c - c0):W * (c - c0) + 1024 // rows])
+            read(("attn", first), len(shared[k]))
 
         def dg(k, i):
             g, j, c = pairs[k][i]
@@ -268,39 +224,41 @@ def tile_qwen3_5attention_pb_v_kernel(tc, hidden, wq, attn, wo, gate, gout, dx_o
                 take(("dz", g, c), "dz", 2048, BF16)
             nc.vector.tensor_tensor(out=tiles["dz", g, c][:, W * j:W * j + W].rearrange("p (u m i) -> p u m i", u=2, i=2),
                                     in0=tiles["dg", k, i][:].rearrange("p (m u i) -> p u m i", u=2, i=2),
-                                    in1=tiles["gate", k][:, W * i:W * i + W].rearrange("p (m u i) -> p u m i", u=2, i=2), op=ALU.mult)
+                                    in1=tiles["gate", k][:, W * i:W * i + W].rearrange("p (m u i) -> p u m i", u=2, i=2),
+                                    op=ALU.mult)
             give(("dg", k, i))
             if i == 1:
                 give(("gate", k))
 
-        def tz(k):
-            turn(("tz", k), [tiles["dz", g, c][:, W * j:W * j + W].bitcast(F32) for g, j, c in pairs[k]], True)
+        def turn_dz(k):
+            rows = [tiles["dz", g, c][:, W * j:W * j + W].bitcast(F32) for g, j, c in pairs[k]]
+            turn(("tz", k), [row[:, P * u:P * u + P] for row in rows for u in range(2)])
             for g, j, c in pairs[k]:
-                used(("dz", g, c), 5)
+                read(("dz", g, c), 5)
 
-        def cz(k, on_vector=False):
-            unturn(("tz", k), take(("es", k), "es", 1024, BF16)[:], True, on_vector)
+        def copy_dz(k):
+            unturn(("tz", k), take(("es", k), "es", 1024, BF16)[:], True, False)
 
-        def qe(k):
-            weave_q(("es", k), ("e", k), 0, E5M2)
+        def quant_features(k):
+            quantize(("e", k), 0, E5M2, ("es", k))
 
-        def out_pe(job, part):
+        def product(job, passes=None):
             kind, a, b, half = job
             n = 3 if kind == "dx" else 2
-            if 0 in part:
-                take(job, "bank", W, F32)
-            for s in part:
+            for s in passes or range(n):
+                if s == 0:
+                    take(job, "bank", W, F32)
                 if kind == "dx":
                     k, i = where[a, b, s]
                     mx(tiles[job][:], ("e", k), P * i, E5M2, ("q", half), W * s, E4M3, s == 0, s == n - 1)
                 else:
                     mx(tiles[job][:], ("x", s), 256 * b + P * half, E4M3, ("t", 3 * s + a), 0, E5M2, s == 0, s == n - 1)
 
-        def out_copy(job, on_vector):
+        def copy_out(job, on_vector=False):
             kind, a, b, half = job
             o = ("o", kind, a, b)
             if o not in tiles:
-                take(o, [s for s in SPARE if free[s] and all(job[0] != s for job in loads)][0], 1024, F32)
+                take(o, [s for s in SPENT if free[s] and all(load[0] != s for load in loads)][0], 1024, F32)
             to, src = tiles[o][:, W * half:W * half + W], tiles[job][:]
             if kind == "dw":
                 to, src = to.rearrange("p (m u i) -> p m u i", u=2, i=2), src.rearrange("p (u m i) -> p m u i", u=2, i=2)
@@ -309,228 +267,182 @@ def tile_qwen3_5attention_pb_v_kernel(tc, hidden, wq, attn, wo, gate, gout, dx_o
             else:
                 nc.scalar.activation(out=to, in_=src, func=ACT.Copy, scale=-1.0)
             give(job)
-            uses[o] = uses.get(o, 0) + 1
-            if (kind, a, b) in HALVES:
+            if o == ("o", "dw", 2, 3):
                 nc.sync.dma_start(out=dw_v[b][:, half, W * a:W * a + W], in_=tiles[o][:, W * half:W * half + W])
-            elif uses[o] == 2:
-                if kind == "dx":
-                    nc.sync.dma_start(out=dx_v[a, b], in_=tiles[o][:])
-                else:
-                    nc.sync.dma_start(out=dw_v[b][:, :, W * a:W * a + W], in_=tiles[o][:].rearrange("p (i e) -> p i e", i=2))
+            elif half == 1 and kind == "dx":
+                nc.sync.dma_start(out=dx_v[a, b], in_=tiles[o][:])
+            elif half == 1:
+                nc.sync.dma_start(out=dw_v[b][:, :, W * a:W * a + W], in_=tiles[o][:].rearrange("p (i e) -> p i e", i=2))
 
-        def tg(g):
-            return [("g", g, a, h) for a in range(2) for h in range(2)]
-
-        def tw(c):
-            return [("w", c, a, h) for a in range(2) for h in range(2)]
-
-        def tq(n):
-            return [("q", n, b, h) for b in range(2) for h in range(3)]
-
-        def dx(g, j):
-            return [("dx", g, j, n) for n in range(2)]
-
-        def dw(c):
-            return [("dw", c, t, i) for t in range(4) for i in range(2)]
-
-        count = [0]
-
-        def outs(jobs, share):
+        def each(f, jobs, *args):
             for job in jobs:
-                out_pe(job, range(3 if job[0] == "dx" else 2))
-                count[0] += 1
-                out_copy(job, count[0] % share == 0)
+                f(job, *args)
 
-        def preps(jobs, on_vector=()):
+        def outputs(jobs, passes=None, alternate=False):
             for n, job in enumerate(jobs):
-                prep_pe(job)
-                prep_out(job, n in on_vector)
-                prep_q(job)
+                product(job, passes)
+                copy_out(job, alternate and n % 2 == 0)
 
-        pump()
-        def run(todo):
-            for f in todo:
-                f[0](*f[1:])
+        def both(f, k):
+            f(k, 0)
+            f(k, 1)
 
-        def whole(job):
-            return range(3 if job[0] == "dx" else 2)
+        def run(calls):
+            for call in calls:
+                call[0](*call[1:])
 
-        def zipped(a, b):
-            out = []
-            for i in range(max(len(a), len(b))):
-                out += a[i:i + 1] + b[i:i + 1]
-            return out
+        g0, g1 = [[("g", g, a, h) for a in range(2) for h in range(2)] for g in range(2)]
+        w0, w1, w2 = [[("w", c, a, h) for a in range(2) for h in range(2)] for c in range(3)]
+        q0, q1 = [[("q", n, b, h) for b in range(2) for h in range(3)] for n in range(2)]
+        dx0, dx1 = [[("dx", g, j, n) for j in range(4) for n in range(2)] for g in range(2)]
+        dw0, dw1, dw2 = [[("dw", c, t, i) for t in range(4) for i in range(2)] for c in range(3)]
 
-        def outs2(jobs, part=None, vec=()):
-            for n, job in enumerate(jobs):
-                out_pe(job, part or whole(job))
-                out_copy(job, n in vec)
+        issue_loads()
 
-        def opens(jobs, part):
-            for job in jobs:
-                out_pe(job, part)
-
-        g0, g1, w0, w1, w2, q0, q1 = tg(0), tg(1), tw(0), tw(1), tw(2), tq(0), tq(1)
-        with tc.manual_schedule(engines={mybir.EngineType.DVE, mybir.EngineType.Activation}):
+        with tc.manual_schedule(engines={VECTOR, SCALAR}):
             for n, job in enumerate(g0[:2] + w0):
-                prep_pe(job)
-                prep_out(job, n in HV)
+                turn_in(job)
+                copy_in(job, n % 2 == 0)
                 if n == 3:
-                    th(0)
-                prep_q(job)
-            sq(0)
-            dg(0, 0)
-            dg(0, 1)
-            run([(prep_pe, job) for job in g0[2:] + w1])
-            wm(0)
-            th(1)
+                    tanh(0)
+                quant_in(job)
+            square(0)
+            both(dg, 0)
+            each(turn_in, g0[2:] + w1)
+            factor(0)
+            tanh(1)
             dz(0, 0)
-            sq(1)
+            square(1)
             dz(0, 1)
-            prep_out(g0[2])
-            prep_out(g0[3])
-            wm(1)
-            prep_q(g0[3])
-            dg(1, 0)
-            dg(1, 1)
-            run([(prep_out, job, n in HW) for n, job in enumerate(w1)])
-            run([(prep_pe, job) for job in w2[:2]])
-            tz(0)
-            th(2)
-            run([(prep_q, job) for job in w1])
-            sq(2)
-            dz(1, 0)
-            dz(1, 1)
-            run([(prep_out, job) for job in w2[:2]] + [(cz, 0)])
+            each(copy_in, g0[2:])
+            factor(1)
+            quant_in(g0[3])
+            both(dg, 1)
+            copy_in(w1[0])
+            each(copy_in, w1[1:], True)
+            each(turn_in, w2[:2])
+            turn_dz(0)
+            tanh(2)
+            each(quant_in, w1)
+            square(2)
+            both(dz, 1)
+            each(copy_in, w2[:2])
+            copy_dz(0)
             dg(2, 0)
-            run([(prep_pe, job) for job in w2[2:]] + [(prep_out, job) for job in w2[2:]])
-            wm(2)
-            iz(0, 0)
-            run([(prep_q, job) for job in w2])
+            each(turn_in, w2[2:])
+            each(copy_in, w2[2:])
+            factor(2)
+            weave_dz(0, 0)
+            each(quant_in, w2)
             dg(2, 1)
-            qe(0)
-            qt(0, 0)
-            th(3)
-            sq(3)
-        prep = {2: q0[:3], 3: q0[3:], 4: g1, 5: q1}
-        jobs = {5: dx(0, 0)[:1] + dx(0, 1)[:1]}
-        share = SHARE
-        back = {2: [(ix, 0, 0), (qx, 0, 0)], 3: [(ix, 0, 1), (qx, 0, 1)], 5: [(ix, 1, 0), (qx, 1, 0)]}
+            quant_features(0)
+            quant_tokens(0, 0)
+            tanh(3)
+            square(3)
+
+        turned = {1: [], 2: q0[:3], 3: q0[3:], 4: g1, 5: q1}
+        woven = {2: (0, 0), 3: (0, 1), 5: (1, 0)}
         for k in range(2, 6):
-            mine = prep.get(k, [])
-            turns = [(tz, k - 1)] + [(prep_pe, job) for job in mine]
-            drains = [(cz, k - 1)] + [(prep_out, job, n in share.get(k, ())) for n, job in enumerate(mine)]
+            turns = [(turn_dz, k - 1)] + [(turn_in, job) for job in turned[k]]
+            drains = [(copy_dz, k - 1)] + [(copy_in, job, job == q1[1]) for job in turned[k]]
+            scalar = drains[:2] + [(tanh, k + 2), drains[2], (square, k + 2)] + drains[3:]
             cut = max(3, (len(turns) + 1) // 2)
             run(turns[:cut])
-            quants = [(prep_q, job) for job in prep.get(k - 1, [])]
-            run(quants[-3:])
-            dz(k, 0)
-            run(quants[:-3])
-            dz(k, 1)
-            acts = [(th, k + 2), (sq, k + 2)]
-            mix = drains[:2] + zipped(acts, drains[2:]) if mine else zipped(acts, drains)
-            run(mix[:2])
+            each(quant_in, turned[k - 1][-3:])
+            both(dz, k)
+            run(scalar[:2])
             dg(k + 1, 0)
-            run(mix[2:4])
+            run(scalar[2:4])
             run(turns[cut:])
-            todo = back.get(k, [])
-            run(todo[:1])
-            wm(k + 1)
-            qe(k - 1)
+            if k in woven:
+                weave_x(*woven[k])
+            factor(k + 1)
+            quant_features(k - 1)
             dg(k + 1, 1)
-            run(mix[4:])
-            run(todo[1:])
-            outs2(jobs.get(k, []))
-        tz(5)
-        run([(prep_q, job) for job in q1[3:4]])
+            run(scalar[4:])
+            if k in woven:
+                quant_x(*woven[k])
+
+        outputs([dx0[0], dx0[2]])
+        turn_dz(5)
+        quant_in(q1[3])
         dz(6, 0)
-        cz(5)
-        run([(prep_q, job) for job in q1[4:]])
+        copy_dz(5)
+        each(quant_in, q1[4:])
         dz(6, 1)
-        dg(7, 0)
-        dg(7, 1)
-        th(8)
-        wm(7)
-        qe(5)
-        outs2(dx(0, 0)[1:])
-        sq(8)
-        outs2(dx(0, 1)[1:] + dx(0, 2)[:1])
-        ix(1, 1)
-        dz(7, 0)
-        dz(7, 1)
-        dg(8, 0)
-        dg(8, 1)
-        iz(1, 0)
-        qx(1, 1)
-        qt(1, 0)
-        outs2(dx(0, 3)[:1])
-        th(9)
-        outs2(dx(0, 2)[1:])
-        sq(9)
-        wm(8)
-        outs2(dx(0, 3)[1:])
-        tz(6)
-        opens(dw(0)[:2], [0])
+        both(dg, 7)
+        tanh(8)
+        factor(7)
+        quant_features(5)
+        outputs([dx0[1]])
+        square(8)
+        outputs(dx0[3:5])
+        weave_x(1, 1)
+        both(dz, 7)
+        both(dg, 8)
+        weave_dz(1, 0)
+        quant_x(1, 1)
+        quant_tokens(1, 0)
+        outputs([dx0[6]])
+        tanh(9)
+        outputs([dx0[5]])
+        square(9)
+        factor(8)
+        outputs([dx0[7]])
+        turn_dz(6)
+        each(product, dw0[:2], [0])
         dz(8, 0)
-        cz(6)
+        copy_dz(6)
         dz(8, 1)
-        outs2(dw(0)[:2], [1])
-        dg(9, 0)
-        dg(9, 1)
-        wm(9)
-        th(10)
-        outs2(dw(0)[2:4])
-        iz(0, 1)
-        sq(10)
-        with tc.manual_schedule(engines={mybir.EngineType.DVE}):
-            dz(9, 0)
-            dz(9, 1)
-            outs2(dw(0)[4:], None, E1)
-            qe(6)
-            iz(1, 1)
-            qt(0, 1)
-            dg(10, 0)
-            dg(10, 1)
-            qt(1, 1)
-            wm(10)
-            tz(7)
-            tz(8)
-            opens(dw(1)[:2], [0])
-            th(11)
-            cz(7)
-            dz(10, 0)
-            dz(10, 1)
-            outs2(dw(1)[:2], [1])
-            sq(11)
-            cz(8)
-            dg(11, 0)
-            dg(11, 1)
-            opens(dw(1)[2:4], [0, 1])
-            out_copy(dw(1)[2], True)
-            qe(7)
-            out_copy(dw(1)[3], True)
-            tz(9)
-            tz(10)
-            wm(11)
-            qe(8)
-            cz(9)
-            cz(10)
-            qe(9)
+        outputs(dw0[:2], [1])
+        both(dg, 9)
+        factor(9)
+        tanh(10)
+        outputs(dw0[2:4])
+        weave_dz(0, 1)
+        square(10)
+
+        with tc.manual_schedule(engines={VECTOR}):
+            both(dz, 9)
+            outputs(dw0[4:])
+            quant_features(6)
+            weave_dz(1, 1)
+            quant_tokens(0, 1)
+            both(dg, 10)
+            quant_tokens(1, 1)
+            factor(10)
+            each(turn_dz, [7, 8])
+            each(product, dw1[:2], [0])
+            tanh(11)
+            copy_dz(7)
+            both(dz, 10)
+            outputs(dw1[:2], [1])
+            square(11)
+            copy_dz(8)
+            both(dg, 11)
+            each(product, dw1[2:4])
+            copy_out(dw1[2], True)
+            quant_features(7)
+            copy_out(dw1[3], True)
+            each(turn_dz, [9, 10])
+            factor(11)
+            quant_features(8)
+            each(copy_dz, [9, 10])
+            quant_features(9)
             dz(11, 0)
-            qe(10)
+            quant_features(10)
             dz(11, 1)
-            outs2(dw(1)[4:6], None, E5)
-            opens(dw(1)[6:], [0, 1])
-            out_copy(dw(1)[6], E6)
-            out_copy(dw(1)[7], False)
-            opens(dx(1, 0)[:1], [0, 1, 2])
-            tz(11)
-            iz(0, 2)
-            out_copy(dx(1, 0)[0], False)
-            cz(11)
-            qe(11)
-            iz(1, 2)
-            outs2(dx(1, 0)[1:] + dx(1, 1), None, E7)
-            qt(0, 2)
-            qt(1, 2)
-            outs2(dx(1, 2) + dw(2)[:6] + dx(1, 3) + dw(2)[6:], None, range(E3, 14, 2))
+            outputs(dw1[4:6])
+            each(product, dw1[6:])
+            each(copy_out, dw1[6:])
+            product(dx1[0])
+            turn_dz(11)
+            weave_dz(0, 2)
+            copy_out(dx1[0])
+            copy_dz(11)
+            quant_features(11)
+            weave_dz(1, 2)
+            outputs(dx1[1:4])
+            quant_tokens(0, 2)
+            quant_tokens(1, 2)
+            outputs(dx1[4:6] + dw2[:6] + dx1[6:] + dw2[6:], alternate=True)

@@ -15,14 +15,17 @@ E4M3 = mybir.dt.float8_e4m3fn_x4
 E5M2 = mybir.dt.float8_e5m2_x4
 ALU = mybir.AluOpType
 ACT = mybir.ActivationFunctionType
-PE, SP, VECTOR, SCALAR = mybir.EngineType.PE, mybir.EngineType.SP, mybir.EngineType.DVE, mybir.EngineType.Activation
+ENG = mybir.EngineType
 
 P = 128
 W = 512
 
-SLOTS = {"bank": 8, "raw": 4, "big": 3, "gate": 5, "attn": 3, "stage": 7, "es": 4, "dz": 6, "out": 4, "xraw": 1}
-SPENT = ("out", "raw", "big", "xraw", "attn", "gate", "dz")
-FREED_LAST = [("ts", 0, 1), ("xs", 0, 0), ("xs", 0, 1)]
+SLOTS = {"raw": 8, "six": 5, "eight": 4, "stage": 6, "es": 4, "dz": 5, "out": 4, "sq": 1}
+BANKS_V = 4
+ON_GPSIMD = (10,)
+APART = (8, 10)
+SHARE = 384
+SPENT = ("raw", "six", "eight", "out")
 
 
 def tile_qwen3_5attention_pb_v_kernel(tc, hidden, wq, attn, wo, gate, gout, dx_out, dw_out):
@@ -31,31 +34,32 @@ def tile_qwen3_5attention_pb_v_kernel(tc, hidden, wq, attn, wo, gate, gout, dx_o
     g_v = gout.rearrange("b s m -> (b s) m").rearrange("(g p a i) m -> g a p (i m)", g=2, a=2, i=2)
     wo_v = wo.rearrange("u h m -> (u h) m").rearrange("(c a p i) m -> c a p (i m)", c=3, a=2, i=2)
     wq_v = wq.rearrange("m u h -> m (u h)").rearrange("(r p i) e -> r p (i e)", r=4, i=2)
-    at_v = attn.rearrange("b s u h -> (b s) (u h)").rearrange("(g p j) e -> g p j e", g=2, j=4)
-    ga_v = gate.rearrange("b s u h -> (b s) (u h)").rearrange("(g p j) e -> g p j e", g=2, j=4)
+    at_v = attn.rearrange("b s u h -> (b s) (u h)").rearrange("(g p a i) e -> g a p i e", g=2, a=2, i=2)
+    ga_v = gate.rearrange("b s u h -> (b s) (u h)").rearrange("(g p a i) e -> g a p i e", g=2, a=2, i=2)
     dx_v = dx_out.rearrange("b s m -> (b s) m").rearrange("(g p j) m -> g j p m", g=2, j=4)
     dw_v = dw_out.rearrange("m u h -> m (u h)").rearrange("(t i q) e -> t q i e", i=2, q=P)
 
-    pairs = [[(0, 2 * a, 0), (0, 2 * a + 1, 0)] for a in range(2)]
-    pairs += [[(0, j, 1), (0, j, 2)] for j in range(4)]
-    pairs += [[(1, 2 * a, c), (1, 2 * a + 1, c)] for c in range(3) for a in range(2)]
-    where = {slot: (k, i) for k, pair in enumerate(pairs) for i, slot in enumerate(pair)}
-    shared = {k: ks for ks in [[0], [1], [2, 3], [4, 5], [6, 7], [8, 10], [9, 11]] for k in ks}
+    steps = [(0, 0, 0), (0, 1, 0)] + [(0, a, c) for a in range(2) for c in (1, 2)] + [(1, a, c) for c in range(3) for a in range(2)]
 
     with ExitStack() as ctx:
         sb = ctx.enter_context(tc.tile_pool(name="sb", bufs=1))
         ps = ctx.enter_context(tc.psum_pool(name="ps", bufs=1))
-        ctx.enter_context(tc.manual_schedule(engines={PE, SP}))
+        ctx.enter_context(tc.manual_schedule())
 
         ident = sb.tile([P, P], F32, name="ident")
         make_identity(nc, ident[:])
 
         free = {kind: list(range(n)) for kind, n in SLOTS.items()}
+        free["V"], free["S"] = list(range(BANKS_V)), list(range(BANKS_V, 8))
         held, tiles, reads = {}, {}, {}
 
         def take(key, kind, cols, dtype):
-            slot = free[kind].pop(-1 if key in FREED_LAST else 0)
-            held[key] = (kind, slot)
+            if kind == "bank":
+                slot = free[lender(key)].pop(0)
+                held[key] = (drainer[key], slot)
+            else:
+                slot = free[kind].pop(0)
+                held[key] = (kind, slot)
             if kind == "bank":
                 tiles[key] = ps.tile([P, cols], dtype, name="bank%d" % slot)
             else:
@@ -65,7 +69,6 @@ def tile_qwen3_5attention_pb_v_kernel(tc, hidden, wq, attn, wo, gate, gout, dx_o
         def give(key):
             kind, slot = held.pop(key)
             free[kind].append(slot)
-            issue_loads()
 
         def read(key, readers):
             reads[key] = reads.get(key, 0) + 1
@@ -98,10 +101,6 @@ def tile_qwen3_5attention_pb_v_kernel(tc, hidden, wq, attn, wo, gate, gout, dx_o
                                 rhs=tiles[b, "c"][:, b0:b0 + W].bitcast(bfmt), rhs_scale=tiles[b, "s"][:, b0:b0 + W],
                                 start=start, stop=stop)
 
-        def span(view, first, last):
-            (g, j0, c0), (g, j1, c1) = first, last
-            return view[g][:, j0:j1 + 1, W * c0:W * c1 + W]
-
         def go(g, a):
             return ("raw", ("graw", g, a), g_v[g, a])
 
@@ -109,31 +108,39 @@ def tile_qwen3_5attention_pb_v_kernel(tc, hidden, wq, attn, wo, gate, gout, dx_o
             return ("raw", ("wraw", c, a), wo_v[c, a])
 
         def wq_rows(r):
-            return ("big", ("qraw", r), wq_v[r])
+            return ("six", ("qraw", r), wq_v[r])
 
         def hid(g):
-            return ("xraw", ("xraw", g), x_v[g])
+            return ("eight", ("xraw", g), x_v[g])
 
-        def ga(k):
-            return ("gate", ("gate", k), span(ga_v, *pairs[k]))
+        piece = {}
 
-        def at(k):
-            return ("attn", ("attn", k), span(at_v, pairs[k][0], pairs[shared[k][-1]][1]))
+        def rect(name, view, kind, g, a, c0, c1):
+            for c in range(c0, c1):
+                piece[name, g, a, c] = ((name, g, a, c0), c0, c1 - c0)
+            return (kind, (name, g, a, c0), view[g, a][:, :, W * c0:W * c1])
 
-        loads = [go(0, 0), wo_rows(0, 0), wo_rows(0, 1), ga(0), at(0), go(0, 1), ga(1), at(1)]
-        loads += [wo_rows(1, 0), wo_rows(1, 1), ga(2), wo_rows(2, 0), wo_rows(2, 1), at(2), ga(3)]
-        loads += [hid(0), wq_rows(0), ga(4), at(4), wq_rows(1), ga(5), go(1, 0), go(1, 1), ga(6)]
-        loads += [wq_rows(2), at(6), wq_rows(3), ga(7), hid(1), ga(8), at(8), ga(9), at(9), ga(10), ga(11)]
+        def ga(g, a, c0, c1):
+            return rect("gate", ga_v, "raw" if c1 - c0 == 1 else "eight", g, a, c0, c1)
 
-        def issue_loads():
-            while loads and free[loads[0][0]]:
-                kind, key, src = loads.pop(0)
-                dtype = F32 if kind == "gate" else BF16
-                if len(src.shape) == 2:
-                    nc.sync.dma_start(out=take(key, kind, src.shape[1], dtype)[:], in_=src)
-                else:
-                    to = take(key, kind, src.shape[1] * src.shape[2], dtype)
-                    nc.sync.dma_start(out=to[:].rearrange("p (j e) -> p j e", j=src.shape[1]), in_=src)
+        def at(g, a, c0, c1):
+            return rect("attn", at_v, "six" if c1 - c0 == 3 else "raw", g, a, c0, c1)
+
+        loads = [go(0, 0), wo_rows(0, 0), wo_rows(0, 1), ga(0, 0, 0, 1), at(0, 0, 0, 1), go(0, 1), ga(0, 1, 0, 1), at(0, 1, 0, 1)]
+        loads += [wo_rows(1, 0), wo_rows(1, 1), ga(0, 0, 1, 3), wo_rows(2, 0), wo_rows(2, 1), at(0, 0, 1, 3)]
+        loads += [wq_rows(0), hid(0), ga(0, 1, 1, 3), at(0, 1, 1, 3), wq_rows(1), go(1, 0), ga(1, 0, 0, 1), go(1, 1), wq_rows(2)]
+        loads += [ga(1, 1, 0, 1), wq_rows(3), at(1, 0, 0, 3), hid(1), at(1, 1, 0, 3), ga(1, 0, 1, 3), ga(1, 1, 1, 3)]
+
+        sources = {key: (kind, src) for kind, key, src in loads}
+
+        def load(key):
+            kind, src = sources.pop(key)
+            dtype = F32 if key[0] == "gate" else BF16
+            if len(src.shape) == 2:
+                nc.sync.dma_start(out=take(key, kind, src.shape[1], dtype)[:], in_=src)
+            else:
+                to = take(key, kind, src.shape[1] * src.shape[2], dtype)
+                nc.sync.dma_start(out=to[:].rearrange("p (j e) -> p j e", j=src.shape[1]), in_=src)
 
         def turn(bank, halves):
             b = take(bank, "bank", W, F32)
@@ -152,30 +159,31 @@ def tile_qwen3_5attention_pb_v_kernel(tc, hidden, wq, attn, wo, gate, gout, dx_o
                 nc.scalar.copy(out=to, in_=src)
             give(bank)
 
+        def raw_of(job):
+            kind, a, b, h = job
+            return {"g": ("graw", a, b), "w": ("wraw", a, b), "q": ("qraw", 2 * a + b)}[kind]
+
         def turn_in(job):
             kind, a, b, h = job
-            raw = {"g": ("graw", a, b), "w": ("wraw", a, b), "q": ("qraw", 2 * a + b)}[kind]
+            raw = raw_of(job)
             passes = 3 if kind == "q" else 2
             words = tiles[raw][:].bitcast(F32)
             rows = [words[:, 256 * (passes * i + h):256 * (passes * i + h) + 256] for i in range(2)]
             turn(job, [row[:, u:256:2] for row in rows for u in range(2)])
-            if h == passes - 1:
-                give(raw)
+            read(raw, passes)
 
         def staged(job):
             kind, a, b, h = job
             return (("stg", kind, a, b), h) if kind == "g" else (("stg", kind, a, h), b)
 
-        def copy_in(job, on_vector=False):
+        def copy_in(job):
             stage, half = staged(job)
-            if half == 0:
+            if stage not in tiles:
                 take(stage, "stage", 2048, BF16)
-            unturn(job, tiles[stage][:, 1024 * half:1024 * half + 1024], job[0] == "g", on_vector)
+            unturn(job, tiles[stage][:, 1024 * half:1024 * half + 1024], job[0] == "g", drainer[job] == "V")
 
-        def quant_in(job):
-            stage, half = staged(job)
-            if half == 1:
-                quantize(job[:2], W * stage[3], E5M2 if job[0] == "g" else E4M3, stage)
+        def quant_in(kind, a, n):
+            quantize((kind, a), W * n, E5M2 if kind == "g" else E4M3, ("stg", kind, a, n))
 
         def weave(src, c0, stage):
             rows = tiles[src][:].rearrange("p (t m) -> p t m", t=4)[:, :, c0:c0 + W]
@@ -183,113 +191,203 @@ def tile_qwen3_5attention_pb_v_kernel(tc, hidden, wq, attn, wo, gate, gout, dx_o
                                   in_=rows.rearrange("p t (c i) -> p c t i", i=8))
 
         def weave_x(g, h):
-            weave(("xraw", g), W * h, ("xs", g, h))
-            read(("xraw", g), 2)
+            c0 = SHARE if (g, h) in gate_of else 0
+            if c0 == 0:
+                take(("xs", g, h), "stage", 2048, BF16)
+            rows = tiles["xraw", g][:].rearrange("p (t m) -> p t m", t=4)[:, :, W * h + c0:W * h + W]
+            nc.vector.tensor_copy(out=tiles["xs", g, h][:, 4 * c0:].rearrange("p (c i t) -> p c t i", i=8, t=4),
+                                  in_=rows.rearrange("p t (c i) -> p c t i", i=8))
+            read(("xraw", g), 2 + len([1 for half in gate_of if half[0] == g]))
+
+        def weave_aside(g, h):
+            free["stage"].insert(0, free["stage"].pop())
+            rows = tiles["xraw", g][:].rearrange("p (t m) -> p m t", t=4)[:, W * h:W * h + SHARE, :]
+            to = take(("xs", g, h), "stage", 2048, BF16)[:, :4 * SHARE].rearrange("p (c t) -> p c t", t=4)
+            nc.gpsimd.tensor_scalar(out=to, in0=rows, scalar1=1.0, scalar2=0.0, op0=ALU.mult, op1=ALU.add)
+            read(("xraw", g), 2 + len([1 for half in gate_of if half[0] == g]))
 
         def quant_x(g, h):
             quantize(("x", g), W * h, E4M3, ("xs", g, h))
 
         def weave_dz(g, c):
             weave(("dz", g, c), 0, ("ts", g, c))
-            read(("dz", g, c), 5)
+            read(("dz", g, c), 3)
 
         def quant_tokens(g, c):
             quantize(("t", 3 * g + c), 0, E5M2, ("ts", g, c))
 
+        def part(name, k):
+            g, a, c = steps[k]
+            key, c0, chunks = piece[name, g, a, c]
+            return tiles[key][:].rearrange("p (i e) -> p i e", i=2)[:, :, W * (c - c0):W * (c - c0) + W]
+
+        def done_with(name, k, readers):
+            key, c0, chunks = piece[(name,) + steps[k]]
+            read(key, readers * chunks)
+
         def tanh(k):
-            nc.scalar.activation(out=tiles["gate", k][:], in_=tiles["gate", k][:], func=ACT.Tanh, scale=0.5)
+            nc.scalar.activation(out=part("gate", k), in_=part("gate", k), func=ACT.Tanh, scale=0.5)
+
+        def squared(k):
+            return tiles["sq", k][:].rearrange("p (i e) -> p i e", i=2) if k in APART else part("gate", k)
 
         def square(k):
-            nc.scalar.activation(out=tiles["gate", k][:], in_=tiles["gate", k][:], func=ACT.Square, scale=0.5)
+            if k in APART:
+                take(("sq", k), "sq", 1024, F32)
+            if k in ON_GPSIMD:
+                nc.gpsimd.tensor_tensor(out=squared(k), in0=part("gate", k), in1=part("gate", k), op=ALU.mult)
+            else:
+                nc.scalar.activation(out=squared(k), in_=part("gate", k), func=ACT.Square)
 
         def factor(k):
-            first, last = shared[k][0], shared[k][-1]
-            (g, j0, c0), j1, (g, j, c) = pairs[first][0], pairs[last][1][1], pairs[k][0]
-            rows = pairs[k][1][1] - j + 1
-            q = tiles["gate", k][:].rearrange("p (j e) -> p j e", j=rows)
-            a = tiles["attn", first][:].rearrange("p (j e) -> p j e", j=j1 - j0 + 1)
-            nc.vector.scalar_tensor_tensor(out=q, in0=q, scalar=0.25, op0=ALU.subtract, op1=ALU.mult,
-                                           in1=a[:, j - j0:j - j0 + rows, W * (c - c0):W * (c - c0) + 1024 // rows])
-            read(("attn", first), len(shared[k]))
+            nc.vector.scalar_tensor_tensor(out=part("gate", k), in0=squared(k), scalar=1.0, op0=ALU.subtract,
+                                           op1=ALU.mult, in1=part("attn", k))
+            done_with("attn", k, 1)
+            if k in APART:
+                give(("sq", k))
 
         def dg(k, i):
-            g, j, c = pairs[k][i]
+            g, a, c = steps[k]
             b = take(("dg", k, i), "bank", W, F32)
             for h in range(2):
-                mx(b[:], ("g", g), W * (j // 2) + 256 * h + P * (j % 2), E5M2, ("w", c), W * h, E4M3, h == 0, h == 1)
+                mx(b[:], ("g", g), W * a + 256 * h + P * i, E5M2, ("w", c), W * h, E4M3, h == 0, h == 1)
 
         def dz(k, i):
-            g, j, c = pairs[k][i]
-            if j == 0:
+            g, a, c = steps[k]
+            j = 2 * a + i
+            if ("dz", g, c) not in tiles:
                 take(("dz", g, c), "dz", 2048, BF16)
             nc.vector.tensor_tensor(out=tiles["dz", g, c][:, W * j:W * j + W].rearrange("p (u m i) -> p u m i", u=2, i=2),
                                     in0=tiles["dg", k, i][:].rearrange("p (m u i) -> p u m i", u=2, i=2),
-                                    in1=tiles["gate", k][:, W * i:W * i + W].rearrange("p (m u i) -> p u m i", u=2, i=2),
+                                    in1=part("gate", k)[:, i, :].rearrange("p (m u i) -> p u m i", u=2, i=2),
                                     op=ALU.mult)
             give(("dg", k, i))
-            if i == 1:
-                give(("gate", k))
+            done_with("gate", k, 2)
 
         def turn_dz(k):
-            rows = [tiles["dz", g, c][:, W * j:W * j + W].bitcast(F32) for g, j, c in pairs[k]]
+            g, a, c = steps[k]
+            rows = [tiles["dz", g, c][:, W * j:W * j + W].bitcast(F32) for j in (2 * a, 2 * a + 1)]
             turn(("tz", k), [row[:, P * u:P * u + P] for row in rows for u in range(2)])
-            for g, j, c in pairs[k]:
-                read(("dz", g, c), 5)
+            read(("dz", g, c), 3)
 
         def copy_dz(k):
-            unturn(("tz", k), take(("es", k), "es", 1024, BF16)[:], True, False)
+            unturn(("tz", k), take(("es", k), "es", 1024, BF16)[:], True, drainer["tz", k] == "V")
 
         def quant_features(k):
             quantize(("e", k), 0, E5M2, ("es", k))
 
-        def product(job, passes=None):
+        def product(job, s0, s1):
             kind, a, b, half = job
             n = 3 if kind == "dx" else 2
-            for s in passes or range(n):
+            for s in range(s0, s1):
                 if s == 0:
                     take(job, "bank", W, F32)
                 if kind == "dx":
-                    k, i = where[a, b, s]
-                    mx(tiles[job][:], ("e", k), P * i, E5M2, ("q", half), W * s, E4M3, s == 0, s == n - 1)
+                    mx(tiles[job][:], ("e", steps.index((a, b // 2, s))), P * (b % 2), E5M2, ("q", half), W * s, E4M3, s == 0, s == n - 1)
                 else:
                     mx(tiles[job][:], ("x", s), 256 * b + P * half, E4M3, ("t", 3 * s + a), 0, E5M2, s == 0, s == n - 1)
 
-        def copy_out(job, on_vector=False):
+        def spare():
+            return [s for s in SPENT if free[s] and all(kind != s for kind, src in sources.values())]
+
+        def copy_out(job):
             kind, a, b, half = job
             o = ("o", kind, a, b)
             if o not in tiles:
-                take(o, [s for s in SPENT if free[s] and all(load[0] != s for load in loads)][0], 1024, F32)
+                take(o, spare()[0], 1024, F32)
             to, src = tiles[o][:, W * half:W * half + W], tiles[job][:]
             if kind == "dw":
                 to, src = to.rearrange("p (m u i) -> p m u i", u=2, i=2), src.rearrange("p (u m i) -> p m u i", u=2, i=2)
-            if on_vector:
-                nc.vector.tensor_scalar_mul(out=to, in0=src, scalar1=-1.0)
+            if drainer[job] == "V":
+                nc.vector.tensor_scalar_mul(out=to, in0=src, scalar1=-0.25)
             else:
-                nc.scalar.activation(out=to, in_=src, func=ACT.Copy, scale=-1.0)
+                nc.scalar.activation(out=to, in_=src, func=ACT.Copy, scale=-0.25)
             give(job)
-            if o == ("o", "dw", 2, 3):
-                nc.sync.dma_start(out=dw_v[b][:, half, W * a:W * a + W], in_=tiles[o][:, W * half:W * half + W])
-            elif half == 1 and kind == "dx":
+
+        def store(job):
+            kind, a, b, half = job
+            o = ("o", kind, a, b)
+            if kind == "dx":
                 nc.sync.dma_start(out=dx_v[a, b], in_=tiles[o][:])
-            elif half == 1:
+            else:
                 nc.sync.dma_start(out=dw_v[b][:, :, W * a:W * a + W], in_=tiles[o][:].rearrange("p (i e) -> p i e", i=2))
+            give(o)
 
-        def each(f, jobs, *args):
-            for job in jobs:
-                f(job, *args)
+        def store_bank(job):
+            kind, a, b, half = job
+            nc.sync.dma_start(out=dw_v[b][:, half, W * a:W * a + W], in_=tiles["o", kind, a, b][:, W * half:W * half + W])
 
-        def outputs(jobs, passes=None, alternate=False):
-            for n, job in enumerate(jobs):
-                product(job, passes)
-                copy_out(job, alternate and n % 2 == 0)
+        def warm(n):
+            b = take(("warm", n), "bank", W, F32)
+            nc.tensor.matmul(out=b[:, 0:P], lhsT=ident[:], rhs=ident[:], start=True, stop=True)
+            give(("warm", n))
+
+        def needs(call):
+            f, args = call[0], call[1:]
+            if f == load:
+                return [], [sources[args[0]][0]]
+            if f == warm:
+                return [], [lender(("warm",) + args)]
+            if f == turn_in:
+                return [(load, raw_of(args[0]))], [lender(args[0])]
+            if f == copy_in:
+                return [(turn_in,) + args], ([] if staged(args[0])[0] in tiles else ["stage"])
+            if f == quant_in:
+                kind, a, n = args
+                return [(copy_in, (kind, a, n, i) if kind == "g" else (kind, a, i, n)) for i in range(2)], []
+            if f == tanh:
+                return [(load, piece[("gate",) + steps[args[0]]][0])], []
+            if f == square:
+                return [(tanh,) + args], (["sq"] if args[0] in APART else [])
+            if f == factor:
+                return [(square,) + args, (load, piece[("attn",) + steps[args[0]]][0])], []
+            if f == dg:
+                g, a, c = steps[args[0]]
+                return [(quant_in, "g", g, a), (quant_in, "w", c, 0), (quant_in, "w", c, 1)], [lender(("dg",) + args)]
+            if f == dz:
+                g, a, c = steps[args[0]]
+                return [(dg,) + args, (factor, args[0])], ([] if ("dz", g, c) in tiles else ["dz"])
+            if f == turn_dz:
+                return [(dz, args[0], 0), (dz, args[0], 1)], [lender(("tz", args[0]))]
+            if f == copy_dz:
+                return [(turn_dz,) + args], ["es"]
+            if f == quant_features:
+                return [(copy_dz,) + args], []
+            if f == weave_aside:
+                return [(load, ("xraw", args[0])), gate_of[args]], ["stage"]
+            if f == weave_x:
+                return ([(weave_aside,) + args], []) if args in gate_of else ([(load, ("xraw", args[0]))], ["stage"])
+            if f == weave_dz:
+                return [(dz, steps.index((args[0], a, args[1])), i) for a in range(2) for i in range(2)], ["stage"]
+            if f == quant_x:
+                return [(weave_x,) + args], []
+            if f == quant_tokens:
+                return [(weave_dz,) + args], []
+            if f == product:
+                (kind, a, b, half), s0, s1 = args
+                if kind == "dx":
+                    before = [(quant_features, steps.index((a, b // 2, s))) for s in range(s0, s1)]
+                    before += [(quant_in, "q", half, s) for s in range(s0, s1)]
+                else:
+                    before = [(quant_x, s, b // 2) for s in range(s0, s1)] + [(quant_tokens, s, a) for s in range(s0, s1)]
+                return before, ([lender(args[0])] if s0 == 0 else [])
+            if f == copy_out:
+                return [last[args[0]]], ([] if ("o",) + args[0][:3] in tiles else spare()[:1] or ["none"])
+            if f == store:
+                return [(copy_out, args[0][:3] + (half,)) for half in range(2)], []
+            return [(copy_out,) + args], []
+
+        def each(f, jobs):
+            return [(f, job) for job in jobs]
 
         def both(f, k):
-            f(k, 0)
-            f(k, 1)
+            return [(f, k, 0), (f, k, 1)]
 
-        def run(calls):
-            for call in calls:
-                call[0](*call[1:])
+        def passes(jobs, s0=0, s1=None):
+            return [(product, job, s0, s1 or (3 if job[0] == "dx" else 2)) for job in jobs]
+
+        def quants(kind, a, ns):
+            return [(quant_in, kind, a, n) for n in ns]
 
         g0, g1 = [[("g", g, a, h) for a in range(2) for h in range(2)] for g in range(2)]
         w0, w1, w2 = [[("w", c, a, h) for a in range(2) for h in range(2)] for c in range(3)]
@@ -297,152 +395,69 @@ def tile_qwen3_5attention_pb_v_kernel(tc, hidden, wq, attn, wo, gate, gout, dx_o
         dx0, dx1 = [[("dx", g, j, n) for j in range(4) for n in range(2)] for g in range(2)]
         dw0, dw1, dw2 = [[("dw", c, t, i) for t in range(4) for i in range(2)] for c in range(3)]
 
-        issue_loads()
+        tensor = each(turn_in, g0[:2] + w0) + both(dg, 0) + each(turn_in, g0[2:] + w1) + both(dg, 1) + each(turn_in, w2[:2]) + [(turn_dz, 0)]
+        tensor += both(dg, 2) + each(turn_in, w2[2:]) + [(turn_dz, 1)] + each(turn_in, q0[:2]) + both(dg, 3) + each(turn_in, q0[2:3]) + both(dg, 4)
+        tensor += each(turn_dz, [2, 3]) + each(turn_in, q0[3:]) + both(dg, 5) + each(turn_in, g1) + passes([dx0[0]]) + each(turn_in, q1[:3]) + passes([dx0[2]])
+        tensor += each(turn_dz, [4, 5]) + each(turn_in, q1[3:]) + both(dg, 6) + both(dg, 7) + passes([dx0[4], dx0[6], dx0[1], dx0[3], dx0[5], dx0[7]])
+        tensor += both(dg, 8) + both(dg, 9) + passes(dw0[:2], 0, 1) + passes(dw0[:2], 1) + each(turn_dz, [6, 7]) + passes(dw0[2:])
+        tensor += both(dg, 10) + both(dg, 11) + each(turn_dz, [8, 9]) + passes(dw1[:2], 0, 1) + passes(dw1[:2], 1) + passes(dw1[2:6]) + [(turn_dz, 10)]
+        tensor += passes(dw1[6:]) + passes(dx1[:2]) + [(turn_dz, 11)] + passes(dx1[2:4])
+        tail = dx1[4:6] + dw2[:6] + dx1[6:] + dw2[6:]
+        tensor += passes(tail)
 
-        with tc.manual_schedule(engines={VECTOR, SCALAR}):
-            for n, job in enumerate(g0[:2] + w0):
-                turn_in(job)
-                copy_in(job, n % 2 == 0)
-                if n == 3:
-                    tanh(0)
-                quant_in(job)
-            square(0)
-            both(dg, 0)
-            each(turn_in, g0[2:] + w1)
-            factor(0)
-            tanh(1)
-            dz(0, 0)
-            square(1)
-            dz(0, 1)
-            each(copy_in, g0[2:])
-            factor(1)
-            quant_in(g0[3])
-            both(dg, 1)
-            copy_in(w1[0])
-            each(copy_in, w1[1:], True)
-            each(turn_in, w2[:2])
-            turn_dz(0)
-            tanh(2)
-            each(quant_in, w1)
-            square(2)
-            both(dz, 1)
-            each(copy_in, w2[:2])
-            copy_dz(0)
-            dg(2, 0)
-            each(turn_in, w2[2:])
-            each(copy_in, w2[2:])
-            factor(2)
-            weave_dz(0, 0)
-            each(quant_in, w2)
-            dg(2, 1)
-            quant_features(0)
-            quant_tokens(0, 0)
-            tanh(3)
-            square(3)
+        scalar = [(copy_in, g0[1]), (copy_in, w0[1]), (tanh, 0), (copy_in, w0[3]), (square, 0), (tanh, 1), (square, 1)] + each(copy_in, g0[2:] + w1[:1])
+        scalar += [(tanh, 2), (tanh, 3), (square, 2)] + each(copy_in, w2[:2]) + [(square, 3)] + each(copy_in, w2[2:]) + each(copy_dz, [0, 1])
+        scalar += each(copy_in, q0[:3]) + [(tanh, 4), (tanh, 5)] + each(copy_dz, [2, 3]) + [(square, 4), (copy_in, q0[5]), (square, 5), (tanh, 6)] + each(copy_in, g1[:2]) + [(square, 6)]
+        scalar += each(copy_in, g1[2:]) + [(copy_out, dx0[0])] + each(copy_in, q1[:3]) + [(copy_out, dx0[2])] + each(copy_dz, [4, 5]) + [(tanh, 7)] + each(copy_in, q1[3:])
+        scalar += [(square, 7), (tanh, 8), (copy_out, dx0[4]), (copy_out, dx0[6]), (tanh, 9)] + each(copy_out, [dx0[1], dx0[3]]) + [(square, 9)] + each(copy_out, [dx0[5], dx0[7]])
+        scalar += [(square, 8), (copy_out, dw0[0]), (tanh, 10)] + each(copy_dz, [6, 7]) + each(copy_out, dw0[2:4]) + [(tanh, 11)] + each(copy_out, dw0[4:6]) + [(square, 11)] + each(copy_out, dw0[7:]) + each(copy_dz, [8, 9])
+        scalar += each(copy_out, dw1[:5]) + [(copy_dz, 10)] + each(copy_out, dw1[6:] + dx1[:1]) + [(copy_dz, 11)] + each(copy_out, dx1[1:4] + tail[1::2])
 
-        turned = {1: [], 2: q0[:3], 3: q0[3:], 4: g1, 5: q1}
-        woven = {2: (0, 0), 3: (0, 1), 5: (1, 0)}
-        for k in range(2, 6):
-            turns = [(turn_dz, k - 1)] + [(turn_in, job) for job in turned[k]]
-            drains = [(copy_dz, k - 1)] + [(copy_in, job, job == q1[1]) for job in turned[k]]
-            scalar = drains[:2] + [(tanh, k + 2), drains[2], (square, k + 2)] + drains[3:]
-            cut = max(3, (len(turns) + 1) // 2)
-            run(turns[:cut])
-            each(quant_in, turned[k - 1][-3:])
-            both(dz, k)
-            run(scalar[:2])
-            dg(k + 1, 0)
-            run(scalar[2:4])
-            run(turns[cut:])
-            if k in woven:
-                weave_x(*woven[k])
-            factor(k + 1)
-            quant_features(k - 1)
-            dg(k + 1, 1)
-            run(scalar[4:])
-            if k in woven:
-                quant_x(*woven[k])
+        vector = [(copy_in, g0[0]), (quant_in, "g", 0, 0)] + each(copy_in, w0[0::2]) + quants("w", 0, [0, 1]) + [(factor, 0)] + both(dz, 0)
+        vector += [(factor, 1)] + quants("g", 0, [1]) + each(copy_in, w1[1:]) + quants("w", 1, [0, 1]) + both(dz, 1)
+        vector += [(factor, 2), (weave_dz, 0, 0)] + quants("w", 2, [0, 1]) + [(quant_features, 0), (quant_tokens, 0, 0), (factor, 3)]
+        vector += both(dz, 2) + both(dz, 3) + [(weave_x, 0, 0), (quant_features, 1), (quant_x, 0, 0)] + each(copy_in, q0[3:5]) + each(quant_features, [2, 3]) + quants("q", 0, [0, 1])
+        vector += [(factor, 4)] + quants("q", 0, [2]) + [(factor, 5)]
+        vector += both(dz, 4) + both(dz, 5) + [(weave_x, 0, 1)] + quants("g", 1, [0, 1]) + [(quant_x, 0, 1), (factor, 6)]
+        vector += [(weave_x, 1, 0)] + each(quant_features, [4, 5]) + quants("q", 1, [0, 1, 2]) + [(quant_x, 1, 0), (factor, 7)]
+        vector += both(dz, 6) + both(dz, 7) + [(weave_x, 1, 1), (weave_dz, 1, 0), (quant_x, 1, 1), (quant_tokens, 1, 0), (weave_dz, 0, 1), (copy_out, dw0[1]), (factor, 9), (factor, 8), (quant_tokens, 0, 1)]
+        vector += both(dz, 8) + both(dz, 9) + [(copy_out, dw0[6]), (quant_features, 6), (weave_dz, 1, 1), (quant_features, 7), (quant_tokens, 1, 1), (factor, 10), (factor, 11)]
+        vector += both(dz, 10) + both(dz, 11) + [(quant_features, 8), (copy_out, dw1[5]), (quant_features, 10), (weave_dz, 0, 2), (weave_dz, 1, 2), (quant_tokens, 0, 2)]
+        vector += each(quant_features, [9, 11]) + [(quant_tokens, 1, 2)] + each(copy_out, tail[0::2])
 
-        outputs([dx0[0], dx0[2]])
-        turn_dz(5)
-        quant_in(q1[3])
-        dz(6, 0)
-        copy_dz(5)
-        each(quant_in, q1[4:])
-        dz(6, 1)
-        both(dg, 7)
-        tanh(8)
-        factor(7)
-        quant_features(5)
-        outputs([dx0[1]])
-        square(8)
-        outputs(dx0[3:5])
-        weave_x(1, 1)
-        both(dz, 7)
-        both(dg, 8)
-        weave_dz(1, 0)
-        quant_x(1, 1)
-        quant_tokens(1, 0)
-        outputs([dx0[6]])
-        tanh(9)
-        outputs([dx0[5]])
-        square(9)
-        factor(8)
-        outputs([dx0[7]])
-        turn_dz(6)
-        each(product, dw0[:2], [0])
-        dz(8, 0)
-        copy_dz(6)
-        dz(8, 1)
-        outputs(dw0[:2], [1])
-        both(dg, 9)
-        factor(9)
-        tanh(10)
-        outputs(dw0[2:4])
-        weave_dz(0, 1)
-        square(10)
+        dma = each(load, [key for kind, key, src in loads]) + each(store, (dx0 + dw0 + dw1 + dx1[:4] + tail[:-2])[1::2]) + each(store_bank, tail[-2:])
+        lent = {dw0[1]: "S", dw0[3]: "V", dw0[6]: "S", dw1[0]: "V"}
+        gate_of = {(0, 0): (quant_tokens, 0, 0), (0, 1): (quant_in, "q", 0, 2), (1, 1): (quant_x, 1, 0)}
+        extra = [[(weave_aside, 0, 0), (weave_aside, 0, 1), (weave_aside, 1, 1), (square, 10)]]
 
-        with tc.manual_schedule(engines={VECTOR}):
-            both(dz, 9)
-            outputs(dw0[4:])
-            quant_features(6)
-            weave_dz(1, 1)
-            quant_tokens(0, 1)
-            both(dg, 10)
-            quant_tokens(1, 1)
-            factor(10)
-            each(turn_dz, [7, 8])
-            each(product, dw1[:2], [0])
-            tanh(11)
-            copy_dz(7)
-            both(dz, 10)
-            outputs(dw1[:2], [1])
-            square(11)
-            copy_dz(8)
-            both(dg, 11)
-            each(product, dw1[2:4])
-            copy_out(dw1[2], True)
-            quant_features(7)
-            copy_out(dw1[3], True)
-            each(turn_dz, [9, 10])
-            factor(11)
-            quant_features(8)
-            each(copy_dz, [9, 10])
-            quant_features(9)
-            dz(11, 0)
-            quant_features(10)
-            dz(11, 1)
-            outputs(dw1[4:6])
-            each(product, dw1[6:])
-            each(copy_out, dw1[6:])
-            product(dx1[0])
-            turn_dz(11)
-            weave_dz(0, 2)
-            copy_out(dx1[0])
-            copy_dz(11)
-            quant_features(11)
-            weave_dz(1, 2)
-            outputs(dx1[1:4])
-            quant_tokens(0, 2)
-            quant_tokens(1, 2)
-            outputs(dx1[4:6] + dw2[:6] + dx1[6:] + dw2[6:], alternate=True)
+
+        drainer = {("warm", call[1]): "S" for call in tensor if call[0] == warm}
+        for name, queue in (("V", vector), ("S", scalar)):
+            for call in queue:
+                if call[0] in (copy_in, copy_out):
+                    drainer[call[1]] = name
+                elif call[0] == copy_dz:
+                    drainer["tz", call[1]] = name
+                elif call[0] == dz:
+                    drainer[("dg",) + call[1:]] = name
+        last = {call[1]: call for call in tensor if call[0] == product}
+        free["none"] = []
+
+
+        def lender(key):
+            return lent.get(key, drainer[key])
+
+
+        made = set()
+        queues = [dma, tensor, scalar, vector] + extra
+        while any(queues):
+            moved = False
+            for queue in queues:
+                if queue:
+                    before, kinds = needs(queue[0])
+                    if all(call in made for call in before) and all(free[kind] for kind in kinds):
+                        call = queue.pop(0)
+                        call[0](*call[1:])
+                        made.add(call)
+                        moved = True
+            assert moved, [(queue[0][0], queue[0][1:], needs(queue[0])[1]) for queue in queues if queue]

@@ -128,8 +128,8 @@ def tile_qwen3_5attention_pb_v_kernel(tc, hidden, wq, attn, wo, gate, gout, dx_o
 
         loads = [go(0, 0), wo_rows(0, 0), wo_rows(0, 1), ga(0, 0, 0, 1), at(0, 0, 0, 1), go(0, 1), ga(0, 1, 0, 1), at(0, 1, 0, 1)]
         loads += [wo_rows(1, 0), wo_rows(1, 1), ga(0, 0, 1, 3), wo_rows(2, 0), wo_rows(2, 1), at(0, 0, 1, 3)]
-        loads += [wq_rows(0), hid(0), ga(0, 1, 1, 3), at(0, 1, 1, 3), wq_rows(1), go(1, 0), ga(1, 0, 0, 1), go(1, 1), wq_rows(2)]
-        loads += [ga(1, 1, 0, 1), wq_rows(3), at(1, 0, 0, 3), hid(1), at(1, 1, 0, 3), ga(1, 0, 1, 3), ga(1, 1, 1, 3)]
+        loads += [wq_rows(0), hid(0), wq_rows(1), ga(0, 1, 1, 3), at(0, 1, 1, 3), go(1, 0), ga(1, 0, 0, 1), go(1, 1), wq_rows(2)]
+        loads += [wq_rows(3), at(1, 0, 0, 3), hid(1), ga(1, 1, 0, 1), at(1, 1, 0, 3), ga(1, 0, 1, 3), ga(1, 1, 1, 3)]
 
         sources = {key: (kind, src) for kind, key, src in loads}
 
@@ -395,10 +395,12 @@ def tile_qwen3_5attention_pb_v_kernel(tc, hidden, wq, attn, wo, gate, gout, dx_o
         dx0, dx1 = [[("dx", g, j, n) for j in range(4) for n in range(2)] for g in range(2)]
         dw0, dw1, dw2 = [[("dw", c, t, i) for t in range(4) for i in range(2)] for c in range(3)]
 
-        tensor = each(turn_in, g0[:2] + w0) + both(dg, 0) + each(turn_in, g0[2:] + w1) + both(dg, 1) + each(turn_in, w2[:2]) + [(turn_dz, 0)]
-        tensor += both(dg, 2) + each(turn_in, w2[2:]) + [(turn_dz, 1)] + each(turn_in, q0[:2]) + both(dg, 3) + each(turn_in, q0[2:3]) + both(dg, 4)
-        tensor += each(turn_dz, [2, 3]) + each(turn_in, q0[3:]) + both(dg, 5) + each(turn_in, g1) + passes([dx0[0]]) + each(turn_in, q1[:3]) + passes([dx0[2]])
-        tensor += each(turn_dz, [4, 5]) + each(turn_in, q1[3:]) + both(dg, 6) + both(dg, 7) + passes([dx0[4], dx0[6], dx0[1], dx0[3], dx0[5], dx0[7]])
+        tensor = each(turn_in, g0[:2] + w0) + both(dg, 0) + each(turn_in, g0[2:] + w1) + both(dg, 1) + each(turn_in, w2[:2]) + [(turn_dz, 0), (dg, 2, 0)]
+        tensor += each(turn_in, w2[2:]) + [(dg, 2, 1), (turn_dz, 1)] + each(turn_in, q0[:2]) + [(dg, 3, 0)] + each(turn_in, q0[2:3]) + [(dg, 3, 1)]
+        tensor += each(turn_in, q0[3:5]) + [(dg, 4, 0)] + each(turn_in, q0[5:]) + [(turn_dz, 2), (dg, 4, 1), (turn_dz, 3), (dg, 5, 0)] + each(turn_in, g1[:2]) + [(dg, 5, 1)] + each(turn_in, g1[2:])
+        tensor += passes(dx0[:1]) + each(turn_in, q1[:2]) + passes(dx0[2:3]) + each(turn_in, q1[2:4]) + [(dg, 6, 0)] + each(turn_in, q1[4:]) + [(dg, 6, 1)]
+        tensor += each(turn_dz, [4, 5]) + both(dg, 7)
+        tensor += passes([dx0[4], dx0[6], dx0[1], dx0[3], dx0[5], dx0[7]])
         tensor += both(dg, 8) + both(dg, 9) + passes(dw0[:2], 0, 1) + passes(dw0[:2], 1) + each(turn_dz, [6, 7]) + passes(dw0[2:])
         tensor += both(dg, 10) + both(dg, 11) + each(turn_dz, [8, 9]) + passes(dw1[:2], 0, 1) + passes(dw1[:2], 1) + passes(dw1[2:6]) + [(turn_dz, 10)]
         tensor += passes(dw1[6:]) + passes(dx1[:2]) + [(turn_dz, 11)] + passes(dx1[2:4])
@@ -407,27 +409,27 @@ def tile_qwen3_5attention_pb_v_kernel(tc, hidden, wq, attn, wo, gate, gout, dx_o
 
         scalar = [(copy_in, g0[1]), (copy_in, w0[1]), (tanh, 0), (copy_in, w0[3]), (square, 0), (tanh, 1), (square, 1)] + each(copy_in, g0[2:] + w1[:1])
         scalar += [(tanh, 2), (tanh, 3), (square, 2)] + each(copy_in, w2[:2]) + [(square, 3)] + each(copy_in, w2[2:]) + each(copy_dz, [0, 1])
-        scalar += each(copy_in, q0[:3]) + [(tanh, 4), (tanh, 5)] + each(copy_dz, [2, 3]) + [(square, 4), (copy_in, q0[5]), (square, 5), (tanh, 6)] + each(copy_in, g1[:2]) + [(square, 6)]
-        scalar += each(copy_in, g1[2:]) + [(copy_out, dx0[0])] + each(copy_in, q1[:3]) + [(copy_out, dx0[2])] + each(copy_dz, [4, 5]) + [(tanh, 7)] + each(copy_in, q1[3:])
+        scalar += each(copy_in, q0[:5]) + [(tanh, 4), (copy_dz, 2), (tanh, 5), (square, 4), (copy_dz, 3)] + each(copy_in, g1[1:2]) + [(square, 5)]
+        scalar += each(copy_in, g1[2:]) + [(copy_out, dx0[0]), (tanh, 6)] + each(copy_in, q1[:2]) + [(copy_out, dx0[2]), (square, 6)] + each(copy_in, q1[2:]) + [(tanh, 7)] + each(copy_dz, [4, 5])
         scalar += [(square, 7), (tanh, 8), (copy_out, dx0[4]), (copy_out, dx0[6]), (tanh, 9)] + each(copy_out, [dx0[1], dx0[3]]) + [(square, 9)] + each(copy_out, [dx0[5], dx0[7]])
-        scalar += [(square, 8), (copy_out, dw0[0]), (tanh, 10)] + each(copy_dz, [6, 7]) + each(copy_out, dw0[2:4]) + [(tanh, 11)] + each(copy_out, dw0[4:6]) + [(square, 11)] + each(copy_out, dw0[7:]) + each(copy_dz, [8, 9])
+        scalar += [(square, 8), (copy_out, dw0[0]), (tanh, 10), (copy_out, dw0[1])] + each(copy_dz, [6, 7]) + each(copy_out, dw0[2:4]) + [(tanh, 11)] + each(copy_out, dw0[4:6]) + [(square, 11)] + each(copy_out, dw0[7:]) + each(copy_dz, [8, 9])
         scalar += each(copy_out, dw1[:5]) + [(copy_dz, 10)] + each(copy_out, dw1[6:] + dx1[:1]) + [(copy_dz, 11)] + each(copy_out, dx1[1:4] + tail[1::2])
 
         vector = [(copy_in, g0[0]), (quant_in, "g", 0, 0)] + each(copy_in, w0[0::2]) + quants("w", 0, [0, 1]) + [(factor, 0)] + both(dz, 0)
         vector += [(factor, 1)] + quants("g", 0, [1]) + each(copy_in, w1[1:]) + quants("w", 1, [0, 1]) + both(dz, 1)
         vector += [(factor, 2), (weave_dz, 0, 0)] + quants("w", 2, [0, 1]) + [(quant_features, 0), (quant_tokens, 0, 0), (factor, 3)]
-        vector += both(dz, 2) + both(dz, 3) + [(weave_x, 0, 0), (quant_features, 1), (quant_x, 0, 0)] + each(copy_in, q0[3:5]) + each(quant_features, [2, 3]) + quants("q", 0, [0, 1])
-        vector += [(factor, 4)] + quants("q", 0, [2]) + [(factor, 5)]
-        vector += both(dz, 4) + both(dz, 5) + [(weave_x, 0, 1)] + quants("g", 1, [0, 1]) + [(quant_x, 0, 1), (factor, 6)]
-        vector += [(weave_x, 1, 0)] + each(quant_features, [4, 5]) + quants("q", 1, [0, 1, 2]) + [(quant_x, 1, 0), (factor, 7)]
-        vector += both(dz, 6) + both(dz, 7) + [(weave_x, 1, 1), (weave_dz, 1, 0), (quant_x, 1, 1), (quant_tokens, 1, 0), (weave_dz, 0, 1), (copy_out, dw0[1]), (factor, 9), (factor, 8), (quant_tokens, 0, 1)]
+        vector += both(dz, 2) + both(dz, 3) + [(weave_x, 0, 0), (quant_features, 1), (copy_in, q0[5]), (quant_x, 0, 0)] + quants("q", 0, range(3)) + [(quant_features, 2), (copy_in, g1[0])]
+        vector += [(factor, 4), (quant_features, 3)] + quants("g", 1, [0]) + [(factor, 5)]
+        vector += both(dz, 4) + both(dz, 5) + [(weave_x, 0, 1)] + quants("g", 1, [1]) + [(quant_x, 0, 1), (factor, 6)]
+        vector += [(weave_x, 1, 0)] + quants("q", 1, [0, 1, 2]) + each(quant_features, [4, 5]) + [(quant_x, 1, 0), (factor, 7)]
+        vector += both(dz, 6) + both(dz, 7) + [(weave_x, 1, 1), (weave_dz, 1, 0), (quant_x, 1, 1), (quant_tokens, 1, 0), (weave_dz, 0, 1), (factor, 9), (factor, 8), (quant_tokens, 0, 1)]
         vector += both(dz, 8) + both(dz, 9) + [(copy_out, dw0[6]), (quant_features, 6), (weave_dz, 1, 1), (quant_features, 7), (quant_tokens, 1, 1), (factor, 10), (factor, 11)]
         vector += both(dz, 10) + both(dz, 11) + [(quant_features, 8), (copy_out, dw1[5]), (quant_features, 10), (weave_dz, 0, 2), (weave_dz, 1, 2), (quant_tokens, 0, 2)]
         vector += each(quant_features, [9, 11]) + [(quant_tokens, 1, 2)] + each(copy_out, tail[0::2])
 
         dma = each(load, [key for kind, key, src in loads]) + each(store, (dx0 + dw0 + dw1 + dx1[:4] + tail[:-2])[1::2]) + each(store_bank, tail[-2:])
-        lent = {dw0[1]: "S", dw0[3]: "V", dw0[6]: "S", dw1[0]: "V"}
-        gate_of = {(0, 0): (quant_tokens, 0, 0), (0, 1): (quant_in, "q", 0, 2), (1, 1): (quant_x, 1, 0)}
+        lent = {q0[5]: "S", q1[0]: "V", dw0[6]: "S", dw1[0]: "V"}
+        gate_of = {(0, 0): (quant_tokens, 0, 0), (0, 1): (quant_in, "g", 1, 0), (1, 1): (quant_x, 1, 0)}
         extra = [[(weave_aside, 0, 0), (weave_aside, 0, 1), (weave_aside, 1, 1), (square, 10)]]
 
 

@@ -24,8 +24,8 @@ SLOTS = {"raw": 8, "six": 5, "eight": 4, "stage": 6, "es": 4, "dz": 5, "out": 4,
 BANKS_V = 4
 ON_GPSIMD = (10,)
 APART = (8, 10)
-SHARE = 384
-SPENT = ("raw", "six", "eight", "out")
+SHARE = 512
+SPENT = ["out", "raw", "six", "eight"]
 
 
 def tile_qwen3_5attention_pb_v_kernel(tc, hidden, wq, attn, wo, gate, gout, dx_out, dw_out):
@@ -127,9 +127,9 @@ def tile_qwen3_5attention_pb_v_kernel(tc, hidden, wq, attn, wo, gate, gout, dx_o
             return rect("attn", at_v, "six" if c1 - c0 == 3 else "raw", g, a, c0, c1)
 
         loads = [go(0, 0), wo_rows(0, 0), wo_rows(0, 1), ga(0, 0, 0, 1), at(0, 0, 0, 1), go(0, 1), ga(0, 1, 0, 1), at(0, 1, 0, 1)]
-        loads += [wo_rows(1, 0), wo_rows(1, 1), ga(0, 0, 1, 3), wo_rows(2, 0), wo_rows(2, 1), at(0, 0, 1, 3)]
-        loads += [wq_rows(0), hid(0), wq_rows(1), ga(0, 1, 1, 3), at(0, 1, 1, 3), go(1, 0), ga(1, 0, 0, 1), go(1, 1), wq_rows(2)]
-        loads += [wq_rows(3), at(1, 0, 0, 3), hid(1), ga(1, 1, 0, 1), at(1, 1, 0, 3), ga(1, 0, 1, 3), ga(1, 1, 1, 3)]
+        loads += [wo_rows(1, 0), wo_rows(1, 1), ga(0, 0, 1, 3), wo_rows(2, 0), at(0, 0, 1, 3), wo_rows(2, 1)]
+        loads += [wq_rows(0), hid(0), wq_rows(1), ga(0, 1, 1, 3), go(1, 0), at(0, 1, 1, 3), go(1, 1), ga(1, 0, 0, 1), wq_rows(2)]
+        loads += [wq_rows(3), at(1, 0, 0, 1), ga(1, 1, 0, 1), hid(1), at(1, 1, 0, 1), ga(1, 0, 1, 3), ga(1, 1, 1, 3), at(1, 0, 1, 3), at(1, 1, 1, 3)]
 
         sources = {key: (kind, src) for kind, key, src in loads}
 
@@ -197,14 +197,14 @@ def tile_qwen3_5attention_pb_v_kernel(tc, hidden, wq, attn, wo, gate, gout, dx_o
             rows = tiles["xraw", g][:].rearrange("p (t m) -> p t m", t=4)[:, :, W * h + c0:W * h + W]
             nc.vector.tensor_copy(out=tiles["xs", g, h][:, 4 * c0:].rearrange("p (c i t) -> p c t i", i=8, t=4),
                                   in_=rows.rearrange("p t (c i) -> p c t i", i=8))
-            read(("xraw", g), 2 + len([1 for half in gate_of if half[0] == g]))
+            read(("xraw", g), 2)
 
         def weave_aside(g, h):
             free["stage"].insert(0, free["stage"].pop())
             rows = tiles["xraw", g][:].rearrange("p (t m) -> p m t", t=4)[:, W * h:W * h + SHARE, :]
             to = take(("xs", g, h), "stage", 2048, BF16)[:, :4 * SHARE].rearrange("p (c t) -> p c t", t=4)
             nc.gpsimd.tensor_scalar(out=to, in0=rows, scalar1=1.0, scalar2=0.0, op0=ALU.mult, op1=ALU.add)
-            read(("xraw", g), 2 + len([1 for half in gate_of if half[0] == g]))
+            read(("xraw", g), 2)
 
         def quant_x(g, h):
             quantize(("x", g), W * h, E4M3, ("xs", g, h))
@@ -288,7 +288,7 @@ def tile_qwen3_5attention_pb_v_kernel(tc, hidden, wq, attn, wo, gate, gout, dx_o
                     mx(tiles[job][:], ("x", s), 256 * b + P * half, E4M3, ("t", 3 * s + a), 0, E5M2, s == 0, s == n - 1)
 
         def spare():
-            return [s for s in SPENT if free[s] and all(kind != s for kind, src in sources.values())]
+            return [s for s in (SPENT[1:] if not sources else []) + SPENT[:1] if free[s]]
 
         def copy_out(job):
             kind, a, b, half = job
@@ -360,7 +360,7 @@ def tile_qwen3_5attention_pb_v_kernel(tc, hidden, wq, attn, wo, gate, gout, dx_o
             if f == weave_dz:
                 return [(dz, steps.index((args[0], a, args[1])), i) for a in range(2) for i in range(2)], ["stage"]
             if f == quant_x:
-                return [(weave_x,) + args], []
+                return [(weave_aside if args in gate_of else weave_x,) + args], []
             if f == quant_tokens:
                 return [(weave_dz,) + args], []
             if f == product:
@@ -400,35 +400,35 @@ def tile_qwen3_5attention_pb_v_kernel(tc, hidden, wq, attn, wo, gate, gout, dx_o
         tensor += each(turn_in, q0[3:5]) + [(dg, 4, 0)] + each(turn_in, q0[5:]) + [(turn_dz, 2), (dg, 4, 1), (turn_dz, 3), (dg, 5, 0)] + each(turn_in, g1[:2]) + [(dg, 5, 1)] + each(turn_in, g1[2:])
         tensor += passes(dx0[:1]) + each(turn_in, q1[:2]) + passes(dx0[2:3]) + each(turn_in, q1[2:4]) + [(dg, 6, 0)] + each(turn_in, q1[4:]) + [(dg, 6, 1)]
         tensor += each(turn_dz, [4, 5]) + both(dg, 7)
-        tensor += passes([dx0[4], dx0[6], dx0[1], dx0[3], dx0[5], dx0[7]])
-        tensor += both(dg, 8) + both(dg, 9) + passes(dw0[:2], 0, 1) + passes(dw0[:2], 1) + each(turn_dz, [6, 7]) + passes(dw0[2:])
+        tensor += passes([dx0[1], dx0[3], dx0[4], dx0[6], dx0[5], dx0[7]])
+        tensor += both(dg, 8) + each(turn_dz, [6, 7]) + both(dg, 9) + passes(dw0[:2], 0, 1) + passes(dw0[:2], 1) + passes(dw0[2:])
         tensor += both(dg, 10) + both(dg, 11) + each(turn_dz, [8, 9]) + passes(dw1[:2], 0, 1) + passes(dw1[:2], 1) + passes(dw1[2:6]) + [(turn_dz, 10)]
         tensor += passes(dw1[6:]) + passes(dx1[:2]) + [(turn_dz, 11)] + passes(dx1[2:4])
         tail = dx1[4:6] + dw2[:6] + dx1[6:] + dw2[6:]
         tensor += passes(tail)
 
         scalar = [(copy_in, g0[1]), (copy_in, w0[1]), (tanh, 0), (copy_in, w0[3]), (square, 0), (tanh, 1), (square, 1)] + each(copy_in, g0[2:] + w1[:1])
-        scalar += [(tanh, 2), (tanh, 3), (square, 2)] + each(copy_in, w2[:2]) + [(square, 3)] + each(copy_in, w2[2:]) + each(copy_dz, [0, 1])
-        scalar += each(copy_in, q0[:5]) + [(tanh, 4), (copy_dz, 2), (tanh, 5), (square, 4), (copy_dz, 3)] + each(copy_in, g1[1:2]) + [(square, 5)]
-        scalar += each(copy_in, g1[2:]) + [(copy_out, dx0[0]), (tanh, 6)] + each(copy_in, q1[:2]) + [(copy_out, dx0[2]), (square, 6)] + each(copy_in, q1[2:]) + [(tanh, 7)] + each(copy_dz, [4, 5])
-        scalar += [(square, 7), (tanh, 8), (copy_out, dx0[4]), (copy_out, dx0[6]), (tanh, 9)] + each(copy_out, [dx0[1], dx0[3]]) + [(square, 9)] + each(copy_out, [dx0[5], dx0[7]])
-        scalar += [(square, 8), (copy_out, dw0[0]), (tanh, 10), (copy_out, dw0[1])] + each(copy_dz, [6, 7]) + each(copy_out, dw0[2:4]) + [(tanh, 11)] + each(copy_out, dw0[4:6]) + [(square, 11)] + each(copy_out, dw0[7:]) + each(copy_dz, [8, 9])
+        scalar += [(tanh, 2), (tanh, 3), (square, 2)] + each(copy_in, w2[:2]) + [(square, 3)] + each(copy_in, w2[2:]) + [(copy_dz, 0)]
+        scalar += each(copy_in, q0[:5]) + [(tanh, 4), (copy_dz, 2), (tanh, 5), (square, 4), (copy_dz, 3), (copy_in, g1[1]), (square, 5)]
+        scalar += each(copy_in, g1[2:]) + [(copy_out, dx0[0]), (tanh, 6)] + each(copy_in, q1[:2]) + [(square, 6)] + each(copy_in, q1[2:]) + [(tanh, 7)] + each(copy_dz, [4, 5])
+        scalar += [(square, 7), (copy_out, dx0[1]), (copy_out, dx0[3]), (tanh, 8), (copy_out, dx0[4]), (tanh, 9), (copy_out, dx0[6]), (square, 9)] + each(copy_out, [dx0[5], dx0[7]])
+        scalar += [(square, 8), (copy_dz, 7), (tanh, 10)] + each(copy_out, dw0[:6]) + [(tanh, 11)] + each(copy_out, dw0[6:]) + [(square, 11)] + each(copy_dz, [8, 9])
         scalar += each(copy_out, dw1[:5]) + [(copy_dz, 10)] + each(copy_out, dw1[6:] + dx1[:1]) + [(copy_dz, 11)] + each(copy_out, dx1[1:4] + tail[1::2])
 
         vector = [(copy_in, g0[0]), (quant_in, "g", 0, 0)] + each(copy_in, w0[0::2]) + quants("w", 0, [0, 1]) + [(factor, 0)] + both(dz, 0)
         vector += [(factor, 1)] + quants("g", 0, [1]) + each(copy_in, w1[1:]) + quants("w", 1, [0, 1]) + both(dz, 1)
         vector += [(factor, 2), (weave_dz, 0, 0)] + quants("w", 2, [0, 1]) + [(quant_features, 0), (quant_tokens, 0, 0), (factor, 3)]
-        vector += both(dz, 2) + both(dz, 3) + [(weave_x, 0, 0), (quant_features, 1), (copy_in, q0[5]), (quant_x, 0, 0)] + quants("q", 0, range(3)) + [(quant_features, 2), (copy_in, g1[0])]
+        vector += [(copy_dz, 1)] + both(dz, 2) + both(dz, 3) + [(quant_features, 1), (copy_in, q0[5]), (quant_x, 0, 0)] + quants("q", 0, range(3)) + [(quant_features, 2), (copy_in, g1[0])]
         vector += [(factor, 4), (quant_features, 3)] + quants("g", 1, [0]) + [(factor, 5)]
-        vector += both(dz, 4) + both(dz, 5) + [(weave_x, 0, 1)] + quants("g", 1, [1]) + [(quant_x, 0, 1), (factor, 6)]
-        vector += [(weave_x, 1, 0)] + quants("q", 1, [0, 1, 2]) + each(quant_features, [4, 5]) + [(quant_x, 1, 0), (factor, 7)]
-        vector += both(dz, 6) + both(dz, 7) + [(weave_x, 1, 1), (weave_dz, 1, 0), (quant_x, 1, 1), (quant_tokens, 1, 0), (weave_dz, 0, 1), (factor, 9), (factor, 8), (quant_tokens, 0, 1)]
-        vector += both(dz, 8) + both(dz, 9) + [(copy_out, dw0[6]), (quant_features, 6), (weave_dz, 1, 1), (quant_features, 7), (quant_tokens, 1, 1), (factor, 10), (factor, 11)]
+        vector += both(dz, 4) + both(dz, 5) + [(copy_out, dx0[2])] + quants("g", 1, [1]) + [(quant_x, 0, 1), (factor, 6)]
+        vector += quants("q", 1, [0, 1, 2]) + [(weave_x, 1, 0), (quant_features, 4), (quant_features, 5), (quant_x, 1, 0), (factor, 7)]
+        vector += both(dz, 6) + both(dz, 7) + [(weave_dz, 1, 0), (quant_x, 1, 1), (quant_tokens, 1, 0), (copy_dz, 6), (weave_dz, 0, 1), (factor, 9), (factor, 8), (quant_tokens, 0, 1)]
+        vector += both(dz, 8) + both(dz, 9) + [(quant_features, 6), (weave_dz, 1, 1), (quant_features, 7), (quant_tokens, 1, 1), (factor, 10), (factor, 11)]
         vector += both(dz, 10) + both(dz, 11) + [(quant_features, 8), (copy_out, dw1[5]), (quant_features, 10), (weave_dz, 0, 2), (weave_dz, 1, 2), (quant_tokens, 0, 2)]
         vector += each(quant_features, [9, 11]) + [(quant_tokens, 1, 2)] + each(copy_out, tail[0::2])
 
         dma = each(load, [key for kind, key, src in loads]) + each(store, (dx0 + dw0 + dw1 + dx1[:4] + tail[:-2])[1::2]) + each(store_bank, tail[-2:])
-        lent = {q0[5]: "S", q1[0]: "V", dw0[6]: "S", dw1[0]: "V"}
+        lent = {("tz", 1): "S", q1[3]: "V", ("tz", 6): "S", dw0[2]: "V"}
         gate_of = {(0, 0): (quant_tokens, 0, 0), (0, 1): (quant_in, "g", 1, 0), (1, 1): (quant_x, 1, 0)}
         extra = [[(weave_aside, 0, 0), (weave_aside, 0, 1), (weave_aside, 1, 1), (square, 10)]]
 

@@ -20,7 +20,7 @@ ENG = mybir.EngineType
 P = 128
 W = 512
 
-SLOTS = {"raw": 8, "six": 5, "eight": 4, "stage": 6, "es": 4, "dz": 5, "out": 4, "sq": 1}
+SLOTS = {"raw": 12, "six": 5, "eight": 2, "stage": 6, "es": 4, "dz": 5, "out": 4, "sq": 1}
 BANKS_V = 4
 ON_GPSIMD = (10,)
 APART = (8, 10)
@@ -123,13 +123,17 @@ def tile_qwen3_5attention_pb_v_kernel(tc, hidden, wq, attn, wo, gate, gout, dx_o
         def ga(g, a, c0, c1):
             return rect("gate", ga_v, "raw" if c1 - c0 == 1 else "eight", g, a, c0, c1)
 
+        def ga_row(g, a, i):
+            piece["gate row", 2 * a + i] = ("gate", g, a, "row", i)
+            return ("raw", ("gate", g, a, "row", i), ga_v[g, a][:, i, W:])
+
         def at(g, a, c0, c1):
             return rect("attn", at_v, "six" if c1 - c0 == 3 else "raw", g, a, c0, c1)
 
-        loads = [go(0, 0), wo_rows(0, 0), wo_rows(0, 1), ga(0, 0, 0, 1), at(0, 0, 0, 1), go(0, 1), ga(0, 1, 0, 1), at(0, 1, 0, 1)]
-        loads += [wo_rows(1, 0), wo_rows(1, 1), ga(0, 0, 1, 3), wo_rows(2, 0), at(0, 0, 1, 3), wo_rows(2, 1)]
-        loads += [wq_rows(0), hid(0), wq_rows(1), ga(0, 1, 1, 3), go(1, 0), at(0, 1, 1, 3), go(1, 1), ga(1, 0, 0, 1), wq_rows(2)]
-        loads += [wq_rows(3), at(1, 0, 0, 1), ga(1, 1, 0, 1), hid(1), at(1, 1, 0, 1), ga(1, 0, 1, 3), ga(1, 1, 1, 3), at(1, 0, 1, 3), at(1, 1, 1, 3)]
+        loads = [go(0, 0), wo_rows(0, 0), wo_rows(0, 1), ga(0, 0, 0, 1), at(0, 0, 0, 1), ga(0, 1, 0, 1), go(0, 1), at(0, 1, 0, 1)]
+        loads += [wo_rows(1, 0), wo_rows(1, 1), ga_row(0, 0, 0), ga_row(0, 0, 1), wo_rows(2, 0), at(0, 0, 1, 3), wo_rows(2, 1)]
+        loads += [wq_rows(0), hid(0), wq_rows(1), ga_row(0, 1, 0), go(1, 0), ga_row(0, 1, 1), at(0, 1, 1, 3), go(1, 1), ga(1, 0, 0, 1), wq_rows(2)]
+        loads += [wq_rows(3), at(1, 0, 0, 1), ga(1, 1, 0, 1), hid(1), at(1, 1, 0, 1), ga(1, 0, 1, 2), ga(1, 1, 1, 2), at(1, 0, 1, 3), at(1, 1, 1, 3), ga(1, 0, 2, 3), ga(1, 1, 2, 3)]
 
         sources = {key: (kind, src) for kind, key, src in loads}
 
@@ -221,15 +225,29 @@ def tile_qwen3_5attention_pb_v_kernel(tc, hidden, wq, attn, wo, gate, gout, dx_o
             key, c0, chunks = piece[name, g, a, c]
             return tiles[key][:].rearrange("p (i e) -> p i e", i=2)[:, :, W * (c - c0):W * (c - c0) + W]
 
+        def whole(name, k):
+            if 2 <= k < 6 and name == "gate":
+                return tiles[piece["gate row", k - 2]][:].rearrange("p (i e) -> p i e", i=2)
+            if 2 <= k < 6:
+                key, c0, chunks = piece[(name,) + steps[k]]
+                first = W * (chunks * (k % 2) + 1 - c0)
+                return tiles[key][:, first:first + 1024].rearrange("p (i e) -> p i e", i=2)
+            return part(name, k)
+
+        def made_for(k, i):
+            if 2 <= k < 6:
+                return whole("gate", k - k % 2 + i)[:, k % 2, :]
+            return part("gate", k)[:, i, :]
+
         def done_with(name, k, readers):
             key, c0, chunks = piece[(name,) + steps[k]]
             read(key, readers * chunks)
 
         def tanh(k):
-            nc.scalar.activation(out=part("gate", k), in_=part("gate", k), func=ACT.Tanh, scale=0.5)
+            nc.scalar.activation(out=whole("gate", k), in_=whole("gate", k), func=ACT.Tanh, scale=0.5)
 
         def squared(k):
-            return tiles["sq", k][:].rearrange("p (i e) -> p i e", i=2) if k in APART else part("gate", k)
+            return tiles["sq", k][:].rearrange("p (i e) -> p i e", i=2) if k in APART else whole("gate", k)
 
         def square(k):
             if k in APART:
@@ -237,11 +255,11 @@ def tile_qwen3_5attention_pb_v_kernel(tc, hidden, wq, attn, wo, gate, gout, dx_o
             if k in ON_GPSIMD:
                 nc.gpsimd.tensor_tensor(out=squared(k), in0=part("gate", k), in1=part("gate", k), op=ALU.mult)
             else:
-                nc.scalar.activation(out=squared(k), in_=part("gate", k), func=ACT.Square)
+                nc.scalar.activation(out=squared(k), in_=whole("gate", k), func=ACT.Square)
 
         def factor(k):
-            nc.vector.scalar_tensor_tensor(out=part("gate", k), in0=squared(k), scalar=1.0, op0=ALU.subtract,
-                                           op1=ALU.mult, in1=part("attn", k))
+            nc.vector.scalar_tensor_tensor(out=whole("gate", k), in0=squared(k), scalar=1.0, op0=ALU.subtract,
+                                           op1=ALU.mult, in1=whole("attn", k))
             done_with("attn", k, 1)
             if k in APART:
                 give(("sq", k))
@@ -259,10 +277,13 @@ def tile_qwen3_5attention_pb_v_kernel(tc, hidden, wq, attn, wo, gate, gout, dx_o
                 take(("dz", g, c), "dz", 2048, BF16)
             nc.vector.tensor_tensor(out=tiles["dz", g, c][:, W * j:W * j + W].rearrange("p (u m i) -> p u m i", u=2, i=2),
                                     in0=tiles["dg", k, i][:].rearrange("p (m u i) -> p u m i", u=2, i=2),
-                                    in1=part("gate", k)[:, i, :].rearrange("p (m u i) -> p u m i", u=2, i=2),
+                                    in1=made_for(k, i).rearrange("p (m u i) -> p u m i", u=2, i=2),
                                     op=ALU.mult)
             give(("dg", k, i))
-            done_with("gate", k, 2)
+            if 2 <= k < 6:
+                read(piece["gate row", 2 * a + i], 2)
+            else:
+                done_with("gate", k, 2)
 
         def turn_dz(k):
             g, a, c = steps[k]
@@ -315,7 +336,8 @@ def tile_qwen3_5attention_pb_v_kernel(tc, hidden, wq, attn, wo, gate, gout, dx_o
 
         def store_bank(job):
             kind, a, b, half = job
-            nc.sync.dma_start(out=dw_v[b][:, half, W * a:W * a + W], in_=tiles["o", kind, a, b][:, W * half:W * half + W])
+            to = dx_v[a, b][:, W * half:W * half + W] if kind == "dx" else dw_v[b][:, half, W * a:W * a + W]
+            nc.sync.dma_start(out=to, in_=tiles["o", kind, a, b][:, W * half:W * half + W])
 
         def warm(n):
             b = take(("warm", n), "bank", W, F32)
@@ -336,7 +358,8 @@ def tile_qwen3_5attention_pb_v_kernel(tc, hidden, wq, attn, wo, gate, gout, dx_o
                 kind, a, n = args
                 return [(copy_in, (kind, a, n, i) if kind == "g" else (kind, a, i, n)) for i in range(2)], []
             if f == tanh:
-                return [(load, piece[("gate",) + steps[args[0]]][0])], []
+                k = args[0]
+                return [(load, piece["gate row", k - 2] if 2 <= k < 6 else piece[("gate",) + steps[k]][0])], []
             if f == square:
                 return [(tanh,) + args], (["sq"] if args[0] in APART else [])
             if f == factor:
@@ -346,7 +369,7 @@ def tile_qwen3_5attention_pb_v_kernel(tc, hidden, wq, attn, wo, gate, gout, dx_o
                 return [(quant_in, "g", g, a), (quant_in, "w", c, 0), (quant_in, "w", c, 1)], [lender(("dg",) + args)]
             if f == dz:
                 g, a, c = steps[args[0]]
-                return [(dg,) + args, (factor, args[0])], ([] if ("dz", g, c) in tiles else ["dz"])
+                return [(dg,) + args, (factor, args[0] - args[0] % 2 + args[1] if 2 <= args[0] < 6 else args[0])], ([] if ("dz", g, c) in tiles else ["dz"])
             if f == turn_dz:
                 return [(dz, args[0], 0), (dz, args[0], 1)], [lender(("tz", args[0]))]
             if f == copy_dz:
@@ -383,6 +406,9 @@ def tile_qwen3_5attention_pb_v_kernel(tc, hidden, wq, attn, wo, gate, gout, dx_o
         def both(f, k):
             return [(f, k, 0), (f, k, 1)]
 
+        def rows(k):
+            return [(dz, k + c, i) for i in range(2) for c in range(2)]
+
         def passes(jobs, s0=0, s1=None):
             return [(product, job, s0, s1 or (3 if job[0] == "dx" else 2)) for job in jobs]
 
@@ -418,9 +444,9 @@ def tile_qwen3_5attention_pb_v_kernel(tc, hidden, wq, attn, wo, gate, gout, dx_o
         vector = [(copy_in, g0[0]), (quant_in, "g", 0, 0)] + each(copy_in, w0[0::2]) + quants("w", 0, [0, 1]) + [(factor, 0)] + both(dz, 0)
         vector += [(factor, 1)] + quants("g", 0, [1]) + each(copy_in, w1[1:]) + quants("w", 1, [0, 1]) + both(dz, 1)
         vector += [(factor, 2), (weave_dz, 0, 0)] + quants("w", 2, [0, 1]) + [(quant_features, 0), (quant_tokens, 0, 0), (factor, 3)]
-        vector += [(copy_dz, 1)] + both(dz, 2) + both(dz, 3) + [(quant_features, 1), (copy_in, q0[5]), (quant_x, 0, 0)] + quants("q", 0, range(3)) + [(quant_features, 2), (copy_in, g1[0])]
+        vector += [(copy_dz, 1)] + rows(2) + [(quant_features, 1), (quant_x, 0, 0)] + quants("q", 0, [0]) + [(copy_in, q0[5])] + quants("q", 0, [1, 2]) + [(quant_features, 2), (copy_in, g1[0])]
         vector += [(factor, 4), (quant_features, 3)] + quants("g", 1, [0]) + [(factor, 5)]
-        vector += both(dz, 4) + both(dz, 5) + [(copy_out, dx0[2])] + quants("g", 1, [1]) + [(quant_x, 0, 1), (factor, 6)]
+        vector += rows(4) + [(copy_out, dx0[2])] + quants("g", 1, [1]) + [(quant_x, 0, 1), (factor, 6)]
         vector += quants("q", 1, [0, 1, 2]) + [(weave_x, 1, 0), (quant_features, 4), (quant_features, 5), (quant_x, 1, 0), (factor, 7)]
         vector += both(dz, 6) + both(dz, 7) + [(weave_dz, 1, 0), (quant_x, 1, 1), (quant_tokens, 1, 0), (copy_dz, 6), (weave_dz, 0, 1), (factor, 9), (factor, 8), (quant_tokens, 0, 1)]
         vector += both(dz, 8) + both(dz, 9) + [(quant_features, 6), (weave_dz, 1, 1), (quant_features, 7), (quant_tokens, 1, 1), (factor, 10), (factor, 11)]

@@ -20,10 +20,8 @@ ENG = mybir.EngineType
 P = 128
 W = 512
 
-SLOTS = {"raw": 12, "six": 5, "eight": 2, "stage": 6, "es": 4, "dz": 5, "out": 4, "sq": 1}
+SLOTS = {"raw": 10, "six": 4, "eight": 2, "stage": 7, "es": 4, "dz": 5, "out": 4}
 BANKS_V = 4
-ON_GPSIMD = (10,)
-APART = (8, 10)
 SHARE = 512
 SPENT = ["out", "raw", "six", "eight"]
 
@@ -199,15 +197,15 @@ def tile_qwen3_5attention_pb_v_kernel(tc, hidden, wq, attn, wo, gate, gout, dx_o
             if c0 == 0:
                 take(("xs", g, h), "stage", 2048, BF16)
             rows = tiles["xraw", g][:].rearrange("p (t m) -> p t m", t=4)[:, :, W * h + c0:W * h + W]
-            nc.vector.tensor_copy(out=tiles["xs", g, h][:, 4 * c0:].rearrange("p (c i t) -> p c t i", i=8, t=4),
-                                  in_=rows.rearrange("p t (c i) -> p c t i", i=8))
+            nc.vector.tensor_scalar_mul(out=tiles["xs", g, h][:, 4 * c0:].rearrange("p (c i t) -> p c t i", i=8, t=4),
+                                        in0=rows.rearrange("p t (c i) -> p c t i", i=8), scalar1=-0.25)
             read(("xraw", g), 2)
 
         def weave_aside(g, h):
             free["stage"].insert(0, free["stage"].pop())
             rows = tiles["xraw", g][:].rearrange("p (t m) -> p m t", t=4)[:, W * h:W * h + SHARE, :]
             to = take(("xs", g, h), "stage", 2048, BF16)[:, :4 * SHARE].rearrange("p (c t) -> p c t", t=4)
-            nc.gpsimd.tensor_scalar(out=to, in0=rows, scalar1=1.0, scalar2=0.0, op0=ALU.mult, op1=ALU.add)
+            nc.gpsimd.tensor_scalar(out=to, in0=rows, scalar1=-0.25, scalar2=0.0, op0=ALU.mult, op1=ALU.add)
             read(("xraw", g), 2)
 
         def quant_x(g, h):
@@ -247,13 +245,13 @@ def tile_qwen3_5attention_pb_v_kernel(tc, hidden, wq, attn, wo, gate, gout, dx_o
             nc.scalar.activation(out=whole("gate", k), in_=whole("gate", k), func=ACT.Tanh, scale=0.5)
 
         def squared(k):
-            return tiles["sq", k][:].rearrange("p (i e) -> p i e", i=2) if k in APART else whole("gate", k)
+            return tiles["sq", k][:].rearrange("p (i e) -> p i e", i=2) if k in gate_of else whole("gate", k)
 
         def square(k):
-            if k in APART:
-                take(("sq", k), "sq", 1024, F32)
-            if k in ON_GPSIMD:
-                nc.gpsimd.tensor_tensor(out=squared(k), in0=part("gate", k), in1=part("gate", k), op=ALU.mult)
+            if k in gate_of:
+                free["stage"].insert(0, free["stage"].pop())
+                take(("sq", k), "stage", 1024, F32)
+                nc.gpsimd.tensor_tensor(out=squared(k), in0=whole("gate", k), in1=whole("gate", k), op=ALU.mult)
             else:
                 nc.scalar.activation(out=squared(k), in_=whole("gate", k), func=ACT.Square)
 
@@ -261,7 +259,7 @@ def tile_qwen3_5attention_pb_v_kernel(tc, hidden, wq, attn, wo, gate, gout, dx_o
             nc.vector.scalar_tensor_tensor(out=whole("gate", k), in0=squared(k), scalar=1.0, op0=ALU.subtract,
                                            op1=ALU.mult, in1=whole("attn", k))
             done_with("attn", k, 1)
-            if k in APART:
+            if k in gate_of:
                 give(("sq", k))
 
         def dg(k, i):
@@ -308,18 +306,22 @@ def tile_qwen3_5attention_pb_v_kernel(tc, hidden, wq, attn, wo, gate, gout, dx_o
                 else:
                     mx(tiles[job][:], ("x", s), 256 * b + P * half, E4M3, ("t", 3 * s + a), 0, E5M2, s == 0, s == n - 1)
 
-        def spare():
-            return [s for s in (SPENT[1:] if not sources else []) + SPENT[:1] if free[s]]
+        def spare(job):
+            return [s for s in (SPENT[:1] if job in dx0 else SPENT[1:]) if free[s]]
 
         def copy_out(job):
             kind, a, b, half = job
             o = ("o", kind, a, b)
             if o not in tiles:
-                take(o, spare()[0], 1024, F32)
+                take(o, spare(job)[0], 1024, F32)
             to, src = tiles[o][:, W * half:W * half + W], tiles[job][:]
             if kind == "dw":
                 to, src = to.rearrange("p (m u i) -> p m u i", u=2, i=2), src.rearrange("p (u m i) -> p m u i", u=2, i=2)
-            if drainer[job] == "V":
+            if kind == "dw" and drainer[job] == "V":
+                nc.vector.tensor_copy(out=to, in_=src)
+            elif kind == "dw":
+                nc.scalar.copy(out=to, in_=src)
+            elif drainer[job] == "V":
                 nc.vector.tensor_scalar_mul(out=to, in0=src, scalar1=-0.25)
             else:
                 nc.scalar.activation(out=to, in_=src, func=ACT.Copy, scale=-0.25)
@@ -361,7 +363,7 @@ def tile_qwen3_5attention_pb_v_kernel(tc, hidden, wq, attn, wo, gate, gout, dx_o
                 k = args[0]
                 return [(load, piece["gate row", k - 2] if 2 <= k < 6 else piece[("gate",) + steps[k]][0])], []
             if f == square:
-                return [(tanh,) + args], (["sq"] if args[0] in APART else [])
+                return ([(tanh,) + args, gate_of[args[0]]], ["stage"]) if args[0] in gate_of else ([(tanh,) + args], [])
             if f == factor:
                 return [(square,) + args, (load, piece[("attn",) + steps[args[0]]][0])], []
             if f == dg:
@@ -395,7 +397,7 @@ def tile_qwen3_5attention_pb_v_kernel(tc, hidden, wq, attn, wo, gate, gout, dx_o
                     before = [(quant_x, s, b // 2) for s in range(s0, s1)] + [(quant_tokens, s, a) for s in range(s0, s1)]
                 return before, ([lender(args[0])] if s0 == 0 else [])
             if f == copy_out:
-                return [last[args[0]]], ([] if ("o",) + args[0][:3] in tiles else spare()[:1] or ["none"])
+                return [last[args[0]]], ([] if ("o",) + args[0][:3] in tiles else spare(args[0])[:1] or ["none"])
             if f == store:
                 return [(copy_out, args[0][:3] + (half,)) for half in range(2)], []
             return [(copy_out,) + args], []
@@ -428,8 +430,8 @@ def tile_qwen3_5attention_pb_v_kernel(tc, hidden, wq, attn, wo, gate, gout, dx_o
         tensor += each(turn_dz, [4, 5]) + both(dg, 7)
         tensor += passes([dx0[1], dx0[3], dx0[4], dx0[6], dx0[5], dx0[7]])
         tensor += both(dg, 8) + each(turn_dz, [6, 7]) + both(dg, 9) + passes(dw0[:2], 0, 1) + passes(dw0[:2], 1) + passes(dw0[2:])
-        tensor += both(dg, 10) + both(dg, 11) + each(turn_dz, [8, 9]) + passes(dw1[:2], 0, 1) + passes(dw1[:2], 1) + passes(dw1[2:6]) + [(turn_dz, 10)]
-        tensor += passes(dw1[6:]) + passes(dx1[:2]) + [(turn_dz, 11)] + passes(dx1[2:4])
+        tensor += both(dg, 10) + both(dg, 11) + each(turn_dz, [8, 9]) + passes(dw1[:2], 0, 1) + passes(dw1[:2], 1) + passes(dw1[2:5]) + [(turn_dz, 10)] + passes(dw1[5:6])
+        tensor += passes(dw1[6:]) + passes(dx1[:2], 0, 2) + passes(dx1[:2], 2) + [(turn_dz, 11)] + passes(dx1[2:4])
         tail = dx1[4:6] + dw2[:6] + dx1[6:] + dw2[6:]
         tensor += passes(tail)
 
@@ -437,9 +439,9 @@ def tile_qwen3_5attention_pb_v_kernel(tc, hidden, wq, attn, wo, gate, gout, dx_o
         scalar += [(tanh, 2), (tanh, 3), (square, 2)] + each(copy_in, w2[:2]) + [(square, 3)] + each(copy_in, w2[2:]) + [(copy_dz, 0)]
         scalar += each(copy_in, q0[:5]) + [(tanh, 4), (copy_dz, 2), (tanh, 5), (square, 4), (copy_dz, 3), (copy_in, g1[1]), (square, 5)]
         scalar += each(copy_in, g1[2:]) + [(copy_out, dx0[0]), (tanh, 6)] + each(copy_in, q1[:2]) + [(square, 6)] + each(copy_in, q1[2:]) + [(tanh, 7)] + each(copy_dz, [4, 5])
-        scalar += [(square, 7), (copy_out, dx0[1]), (copy_out, dx0[3]), (tanh, 8), (copy_out, dx0[4]), (tanh, 9), (copy_out, dx0[6]), (square, 9)] + each(copy_out, [dx0[5], dx0[7]])
-        scalar += [(square, 8), (copy_dz, 7), (tanh, 10)] + each(copy_out, dw0[:6]) + [(tanh, 11)] + each(copy_out, dw0[6:]) + [(square, 11)] + each(copy_dz, [8, 9])
-        scalar += each(copy_out, dw1[:5]) + [(copy_dz, 10)] + each(copy_out, dw1[6:] + dx1[:1]) + [(copy_dz, 11)] + each(copy_out, dx1[1:4] + tail[1::2])
+        scalar += [(square, 7), (copy_out, dx0[1]), (copy_out, dx0[3]), (tanh, 8), (tanh, 9), (copy_out, dx0[6]), (square, 8)] + each(copy_out, [dx0[5], dx0[7]])
+        scalar += [(square, 9), (copy_dz, 6), (tanh, 10), (copy_dz, 7)] + each(copy_out, dw0[:6]) + [(tanh, 11)] + each(copy_out, dw0[6:]) + [(square, 11)] + each(copy_dz, [8, 9])
+        scalar += each(copy_out, dw1[:4]) + [(copy_dz, 10)] + each(copy_out, dw1[4:] + dx1[:1]) + [(copy_dz, 11)] + each(copy_out, dx1[1:4] + tail[1::2])
 
         vector = [(copy_in, g0[0]), (quant_in, "g", 0, 0)] + each(copy_in, w0[0::2]) + quants("w", 0, [0, 1]) + [(factor, 0)] + both(dz, 0)
         vector += [(factor, 1)] + quants("g", 0, [1]) + each(copy_in, w1[1:]) + quants("w", 1, [0, 1]) + both(dz, 1)
@@ -448,14 +450,14 @@ def tile_qwen3_5attention_pb_v_kernel(tc, hidden, wq, attn, wo, gate, gout, dx_o
         vector += [(factor, 4), (quant_features, 3)] + quants("g", 1, [0]) + [(factor, 5)]
         vector += rows(4) + [(copy_out, dx0[2])] + quants("g", 1, [1]) + [(quant_x, 0, 1), (factor, 6)]
         vector += quants("q", 1, [0, 1, 2]) + [(weave_x, 1, 0), (quant_features, 4), (quant_features, 5), (quant_x, 1, 0), (factor, 7)]
-        vector += both(dz, 6) + both(dz, 7) + [(weave_dz, 1, 0), (quant_x, 1, 1), (quant_tokens, 1, 0), (copy_dz, 6), (weave_dz, 0, 1), (factor, 9), (factor, 8), (quant_tokens, 0, 1)]
-        vector += both(dz, 8) + both(dz, 9) + [(quant_features, 6), (weave_dz, 1, 1), (quant_features, 7), (quant_tokens, 1, 1), (factor, 10), (factor, 11)]
-        vector += both(dz, 10) + both(dz, 11) + [(quant_features, 8), (copy_out, dw1[5]), (quant_features, 10), (weave_dz, 0, 2), (weave_dz, 1, 2), (quant_tokens, 0, 2)]
-        vector += each(quant_features, [9, 11]) + [(quant_tokens, 1, 2)] + each(copy_out, tail[0::2])
+        vector += both(dz, 6) + both(dz, 7) + [(copy_out, dx0[4]), (weave_dz, 1, 0), (quant_x, 1, 1), (quant_tokens, 1, 0), (weave_dz, 0, 1), (factor, 8), (quant_tokens, 0, 1), (factor, 9)]
+        vector += both(dz, 8) + both(dz, 9) + [(quant_features, 6), (weave_dz, 1, 1), (quant_features, 7), (quant_tokens, 1, 1), (factor, 10), (quant_features, 8)]
+        vector += both(dz, 10) + [(factor, 11), (quant_features, 9)] + both(dz, 11) + [(quant_features, 10), (weave_dz, 0, 2), (weave_dz, 1, 2), (quant_features, 11), (quant_tokens, 0, 2), (quant_tokens, 1, 2)]
+        vector += [] + each(copy_out, tail[0::2])
 
         dma = each(load, [key for kind, key, src in loads]) + each(store, (dx0 + dw0 + dw1 + dx1[:4] + tail[:-2])[1::2]) + each(store_bank, tail[-2:])
-        lent = {("tz", 1): "S", q1[3]: "V", ("tz", 6): "S", dw0[2]: "V"}
-        gate_of = {(0, 0): (quant_tokens, 0, 0), (0, 1): (quant_in, "g", 1, 0), (1, 1): (quant_x, 1, 0)}
+        lent = {("tz", 1): "S", q1[3]: "V", dx0[4]: "S", ("tz", 6): "V", dw1[5]: "V"}
+        gate_of = {(0, 0): (quant_tokens, 0, 0), (0, 1): (quant_in, "g", 1, 0), (1, 1): (quant_x, 1, 0), 10: (quant_tokens, 0, 1)}
         extra = [[(weave_aside, 0, 0), (weave_aside, 0, 1), (weave_aside, 1, 1), (square, 10)]]
 
 

from contextlib import ExitStack

import concourse.mybir as mybir
from concourse.masks import make_identity

T, M, E = 1024, 1024, 1536
FLOPS = 3 * 2 * T * M * E
BYTES = 2 * (T * M + M * E + T * E + E * M + T * M) + 4 * T * E + 4 * (T * M + M * E)

F32 = mybir.dt.float32
BF16 = mybir.dt.bfloat16
U32 = mybir.dt.uint32
U8 = mybir.dt.uint8
E4M3 = mybir.dt.float8_e4m3fn_x4
E5M2 = mybir.dt.float8_e5m2_x4
ALU = mybir.AluOpType
ACT = mybir.ActivationFunctionType
ENG = mybir.EngineType

P = 128
W = 512

SLOTS = {"raw": 10, "six": 4, "eight": 2, "stage": 7, "es": 4, "dz": 5, "out": 4}
BANKS_V = 4
SHARE = 512
SPENT = ["out", "raw", "six", "eight"]


def tile_qwen3_5attention_pb_v_kernel(tc, hidden, wq, attn, wo, gate, gout, dx_out, dw_out):
    nc = tc.nc
    x_v = hidden.rearrange("b s m -> (b s) m").rearrange("(g p j) m -> g p j m", g=2, j=4)
    g_v = gout.rearrange("b s m -> (b s) m").rearrange("(g p a i) m -> g a p (i m)", g=2, a=2, i=2)
    wo_v = wo.rearrange("u h m -> (u h) m").rearrange("(c a p i) m -> c a p (i m)", c=3, a=2, i=2)
    wq_v = wq.rearrange("m u h -> m (u h)").rearrange("(r p i) e -> r p (i e)", r=4, i=2)
    at_v = attn.rearrange("b s u h -> (b s) (u h)").rearrange("(g p a i) e -> g a p i e", g=2, a=2, i=2)
    ga_v = gate.rearrange("b s u h -> (b s) (u h)").rearrange("(g p a i) e -> g a p i e", g=2, a=2, i=2)
    dx_v = dx_out.rearrange("b s m -> (b s) m").rearrange("(g p j) m -> g j p m", g=2, j=4)
    dw_v = dw_out.rearrange("m u h -> m (u h)").rearrange("(t i q) e -> t q i e", i=2, q=P)

    steps = [(0, 0, 0), (0, 1, 0)] + [(0, a, c) for a in range(2) for c in (1, 2)] + [(1, a, c) for c in range(3) for a in range(2)]

    with ExitStack() as ctx:
        sb = ctx.enter_context(tc.tile_pool(name="sb", bufs=1))
        ps = ctx.enter_context(tc.psum_pool(name="ps", bufs=1))
        ctx.enter_context(tc.manual_schedule())

        ident = sb.tile([P, P], F32, name="ident")
        make_identity(nc, ident[:])

        free = {kind: list(range(n)) for kind, n in SLOTS.items()}
        free["V"], free["S"] = list(range(BANKS_V)), list(range(BANKS_V, 8))
        held, tiles, reads = {}, {}, {}

        def take(key, kind, cols, dtype):
            if kind == "bank":
                slot = free[lender(key)].pop(0)
                held[key] = (drainer[key], slot)
            else:
                slot = free[kind].pop(0)
                held[key] = (kind, slot)
            if kind == "bank":
                tiles[key] = ps.tile([P, cols], dtype, name="bank%d" % slot)
            else:
                tiles[key] = sb.tile([P, cols], dtype, name="%s%d" % (kind, slot), align_bytes=64)
            return tiles[key]

        def give(key):
            kind, slot = held.pop(key)
            free[kind].append(slot)

        def read(key, readers):
            reads[key] = reads.get(key, 0) + 1
            if reads[key] == readers:
                give(key)

        def codes(key, cols):
            tiles[key, "c"] = sb.tile([P, cols], U32, name="c_%s%d" % key, align_bytes=64)
            tiles[key, "s"] = sb.tile([P, cols], U8, name="s_%s%d" % key, align_bytes=64)

        for g in range(2):
            codes(("g", g), 1024)
            codes(("x", g), 1024)
            codes(("q", g), 1536)
        for c in range(3):
            codes(("w", c), 1024)
        for k in range(12):
            codes(("e", k), 256)
        for k in range(6):
            codes(("t", k), W)

        def quantize(key, c0, fmt, stage):
            n = tiles[stage].shape[1] // 4
            nc.vector.quantize_mx(out=tiles[key, "c"][:, c0:c0 + n].bitcast(fmt), scales=tiles[key, "s"][:, c0:c0 + n],
                                  in_=tiles[stage][:])
            give(stage)

        def mx(acc, a, a0, afmt, b, b0, bfmt, start, stop):
            nc.tensor.matmul_mx(out=acc, lhsT=tiles[a, "c"][:, a0:a0 + P].bitcast(afmt), lhsT_scale=tiles[a, "s"][:, a0:a0 + P],
                                rhs=tiles[b, "c"][:, b0:b0 + W].bitcast(bfmt), rhs_scale=tiles[b, "s"][:, b0:b0 + W],
                                start=start, stop=stop)

        def go(g, a):
            return ("raw", ("graw", g, a), g_v[g, a])

        def wo_rows(c, a):
            return ("raw", ("wraw", c, a), wo_v[c, a])

        def wq_rows(r):
            return ("six", ("qraw", r), wq_v[r])

        def hid(g):
            return ("eight", ("xraw", g), x_v[g])

        piece = {}

        def rect(name, view, kind, g, a, c0, c1):
            for c in range(c0, c1):
                piece[name, g, a, c] = ((name, g, a, c0), c0, c1 - c0)
            return (kind, (name, g, a, c0), view[g, a][:, :, W * c0:W * c1])

        def ga(g, a, c0, c1):
            return rect("gate", ga_v, "raw" if c1 - c0 == 1 else "eight", g, a, c0, c1)

        def ga_row(g, a, i):
            piece["gate row", 2 * a + i] = ("gate", g, a, "row", i)
            return ("raw", ("gate", g, a, "row", i), ga_v[g, a][:, i, W:])

        def at(g, a, c0, c1):
            return rect("attn", at_v, "six" if c1 - c0 == 3 else "raw", g, a, c0, c1)

        loads = [go(0, 0), wo_rows(0, 0), wo_rows(0, 1), ga(0, 0, 0, 1), at(0, 0, 0, 1), ga(0, 1, 0, 1), go(0, 1), at(0, 1, 0, 1)]
        loads += [wo_rows(1, 0), wo_rows(1, 1), ga_row(0, 0, 0), ga_row(0, 0, 1), wo_rows(2, 0), at(0, 0, 1, 3), wo_rows(2, 1)]
        loads += [wq_rows(0), hid(0), wq_rows(1), ga_row(0, 1, 0), go(1, 0), ga_row(0, 1, 1), at(0, 1, 1, 3), go(1, 1), ga(1, 0, 0, 1), wq_rows(2)]
        loads += [wq_rows(3), at(1, 0, 0, 1), ga(1, 1, 0, 1), hid(1), at(1, 1, 0, 1), ga(1, 0, 1, 2), ga(1, 1, 1, 2), at(1, 0, 1, 3), at(1, 1, 1, 3), ga(1, 0, 2, 3), ga(1, 1, 2, 3)]

        sources = {key: (kind, src) for kind, key, src in loads}

        def load(key):
            kind, src = sources.pop(key)
            dtype = F32 if key[0] == "gate" else BF16
            if len(src.shape) == 2:
                nc.sync.dma_start(out=take(key, kind, src.shape[1], dtype)[:], in_=src)
            else:
                to = take(key, kind, src.shape[1] * src.shape[2], dtype)
                nc.sync.dma_start(out=to[:].rearrange("p (j e) -> p j e", j=src.shape[1]), in_=src)

        def turn(bank, halves):
            b = take(bank, "bank", W, F32)
            for n, words in enumerate(halves):
                nc.tensor.transpose(b[:, P * n:P * n + P], words, ident[:])

        def unturn(bank, to, rows_apart, on_vector):
            src = tiles[bank][:].rearrange("p (i u n) -> p i n u", i=2, u=2)
            if rows_apart:
                to = to.bitcast(F32).rearrange("p (i n u) -> p i n u", i=2, u=2)
            else:
                to, src = to.bitcast(F32).rearrange("p (n i u) -> p n i u", i=2, u=2), src.rearrange("p i n u -> p n i u")
            if on_vector:
                nc.vector.tensor_copy(out=to, in_=src)
            else:
                nc.scalar.copy(out=to, in_=src)
            give(bank)

        def raw_of(job):
            kind, a, b, h = job
            return {"g": ("graw", a, b), "w": ("wraw", a, b), "q": ("qraw", 2 * a + b)}[kind]

        def turn_in(job):
            kind, a, b, h = job
            raw = raw_of(job)
            passes = 3 if kind == "q" else 2
            words = tiles[raw][:].bitcast(F32)
            rows = [words[:, 256 * (passes * i + h):256 * (passes * i + h) + 256] for i in range(2)]
            turn(job, [row[:, u:256:2] for row in rows for u in range(2)])
            read(raw, passes)

        def staged(job):
            kind, a, b, h = job
            return (("stg", kind, a, b), h) if kind == "g" else (("stg", kind, a, h), b)

        def copy_in(job):
            stage, half = staged(job)
            if stage not in tiles:
                take(stage, "stage", 2048, BF16)
            unturn(job, tiles[stage][:, 1024 * half:1024 * half + 1024], job[0] == "g", drainer[job] == "V")

        def quant_in(kind, a, n):
            quantize((kind, a), W * n, E5M2 if kind == "g" else E4M3, ("stg", kind, a, n))

        def weave(src, c0, stage):
            rows = tiles[src][:].rearrange("p (t m) -> p t m", t=4)[:, :, c0:c0 + W]
            nc.vector.tensor_copy(out=take(stage, "stage", 2048, BF16)[:].rearrange("p (c i t) -> p c t i", i=8, t=4),
                                  in_=rows.rearrange("p t (c i) -> p c t i", i=8))

        def weave_x(g, h):
            c0 = SHARE if (g, h) in gate_of else 0
            if c0 == 0:
                take(("xs", g, h), "stage", 2048, BF16)
            rows = tiles["xraw", g][:].rearrange("p (t m) -> p t m", t=4)[:, :, W * h + c0:W * h + W]
            nc.vector.tensor_scalar_mul(out=tiles["xs", g, h][:, 4 * c0:].rearrange("p (c i t) -> p c t i", i=8, t=4),
                                        in0=rows.rearrange("p t (c i) -> p c t i", i=8), scalar1=-0.25)
            read(("xraw", g), 2)

        def weave_aside(g, h):
            free["stage"].insert(0, free["stage"].pop())
            rows = tiles["xraw", g][:].rearrange("p (t m) -> p m t", t=4)[:, W * h:W * h + SHARE, :]
            to = take(("xs", g, h), "stage", 2048, BF16)[:, :4 * SHARE].rearrange("p (c t) -> p c t", t=4)
            nc.gpsimd.tensor_scalar(out=to, in0=rows, scalar1=-0.25, scalar2=0.0, op0=ALU.mult, op1=ALU.add)
            read(("xraw", g), 2)

        def quant_x(g, h):
            quantize(("x", g), W * h, E4M3, ("xs", g, h))

        def weave_dz(g, c):
            weave(("dz", g, c), 0, ("ts", g, c))
            read(("dz", g, c), 3)

        def quant_tokens(g, c):
            quantize(("t", 3 * g + c), 0, E5M2, ("ts", g, c))

        def part(name, k):
            g, a, c = steps[k]
            key, c0, chunks = piece[name, g, a, c]
            return tiles[key][:].rearrange("p (i e) -> p i e", i=2)[:, :, W * (c - c0):W * (c - c0) + W]

        def whole(name, k):
            if 2 <= k < 6 and name == "gate":
                return tiles[piece["gate row", k - 2]][:].rearrange("p (i e) -> p i e", i=2)
            if 2 <= k < 6:
                key, c0, chunks = piece[(name,) + steps[k]]
                first = W * (chunks * (k % 2) + 1 - c0)
                return tiles[key][:, first:first + 1024].rearrange("p (i e) -> p i e", i=2)
            return part(name, k)

        def made_for(k, i):
            if 2 <= k < 6:
                return whole("gate", k - k % 2 + i)[:, k % 2, :]
            return part("gate", k)[:, i, :]

        def done_with(name, k, readers):
            key, c0, chunks = piece[(name,) + steps[k]]
            read(key, readers * chunks)

        def tanh(k):
            nc.scalar.activation(out=whole("gate", k), in_=whole("gate", k), func=ACT.Tanh, scale=0.5)

        def squared(k):
            return tiles["sq", k][:].rearrange("p (i e) -> p i e", i=2) if k in gate_of else whole("gate", k)

        def square(k):
            if k in gate_of:
                free["stage"].insert(0, free["stage"].pop())
                take(("sq", k), "stage", 1024, F32)
                nc.gpsimd.tensor_tensor(out=squared(k), in0=whole("gate", k), in1=whole("gate", k), op=ALU.mult)
            else:
                nc.scalar.activation(out=squared(k), in_=whole("gate", k), func=ACT.Square)

        def factor(k):
            nc.vector.scalar_tensor_tensor(out=whole("gate", k), in0=squared(k), scalar=1.0, op0=ALU.subtract,
                                           op1=ALU.mult, in1=whole("attn", k))
            done_with("attn", k, 1)
            if k in gate_of:
                give(("sq", k))

        def dg(k, i):
            g, a, c = steps[k]
            b = take(("dg", k, i), "bank", W, F32)
            for h in range(2):
                mx(b[:], ("g", g), W * a + 256 * h + P * i, E5M2, ("w", c), W * h, E4M3, h == 0, h == 1)

        def dz(k, i):
            g, a, c = steps[k]
            j = 2 * a + i
            if ("dz", g, c) not in tiles:
                take(("dz", g, c), "dz", 2048, BF16)
            nc.vector.tensor_tensor(out=tiles["dz", g, c][:, W * j:W * j + W].rearrange("p (u m i) -> p u m i", u=2, i=2),
                                    in0=tiles["dg", k, i][:].rearrange("p (m u i) -> p u m i", u=2, i=2),
                                    in1=made_for(k, i).rearrange("p (m u i) -> p u m i", u=2, i=2),
                                    op=ALU.mult)
            give(("dg", k, i))
            if 2 <= k < 6:
                read(piece["gate row", 2 * a + i], 2)
            else:
                done_with("gate", k, 2)

        def turn_dz(k):
            g, a, c = steps[k]
            rows = [tiles["dz", g, c][:, W * j:W * j + W].bitcast(F32) for j in (2 * a, 2 * a + 1)]
            turn(("tz", k), [row[:, P * u:P * u + P] for row in rows for u in range(2)])
            read(("dz", g, c), 3)

        def copy_dz(k):
            unturn(("tz", k), take(("es", k), "es", 1024, BF16)[:], True, drainer["tz", k] == "V")

        def quant_features(k):
            quantize(("e", k), 0, E5M2, ("es", k))

        def product(job, s0, s1):
            kind, a, b, half = job
            n = 3 if kind == "dx" else 2
            for s in range(s0, s1):
                if s == 0:
                    take(job, "bank", W, F32)
                if kind == "dx":
                    mx(tiles[job][:], ("e", steps.index((a, b // 2, s))), P * (b % 2), E5M2, ("q", half), W * s, E4M3, s == 0, s == n - 1)
                else:
                    mx(tiles[job][:], ("x", s), 256 * b + P * half, E4M3, ("t", 3 * s + a), 0, E5M2, s == 0, s == n - 1)

        def spare(job):
            return [s for s in (SPENT[:1] if job in dx0 else SPENT[1:]) if free[s]]

        def copy_out(job):
            kind, a, b, half = job
            o = ("o", kind, a, b)
            if o not in tiles:
                take(o, spare(job)[0], 1024, F32)
            to, src = tiles[o][:, W * half:W * half + W], tiles[job][:]
            if kind == "dw":
                to, src = to.rearrange("p (m u i) -> p m u i", u=2, i=2), src.rearrange("p (u m i) -> p m u i", u=2, i=2)
            if kind == "dw" and drainer[job] == "V":
                nc.vector.tensor_copy(out=to, in_=src)
            elif kind == "dw":
                nc.scalar.copy(out=to, in_=src)
            elif drainer[job] == "V":
                nc.vector.tensor_scalar_mul(out=to, in0=src, scalar1=-0.25)
            else:
                nc.scalar.activation(out=to, in_=src, func=ACT.Copy, scale=-0.25)
            give(job)

        def store(job):
            kind, a, b, half = job
            o = ("o", kind, a, b)
            if kind == "dx":
                nc.sync.dma_start(out=dx_v[a, b], in_=tiles[o][:])
            else:
                nc.sync.dma_start(out=dw_v[b][:, :, W * a:W * a + W], in_=tiles[o][:].rearrange("p (i e) -> p i e", i=2))
            give(o)

        def store_bank(job):
            kind, a, b, half = job
            to = dx_v[a, b][:, W * half:W * half + W] if kind == "dx" else dw_v[b][:, half, W * a:W * a + W]
            nc.sync.dma_start(out=to, in_=tiles["o", kind, a, b][:, W * half:W * half + W])

        def warm(n):
            b = take(("warm", n), "bank", W, F32)
            nc.tensor.matmul(out=b[:, 0:P], lhsT=ident[:], rhs=ident[:], start=True, stop=True)
            give(("warm", n))

        def needs(call):
            f, args = call[0], call[1:]
            if f == load:
                return [], [sources[args[0]][0]]
            if f == warm:
                return [], [lender(("warm",) + args)]
            if f == turn_in:
                return [(load, raw_of(args[0]))], [lender(args[0])]
            if f == copy_in:
                return [(turn_in,) + args], ([] if staged(args[0])[0] in tiles else ["stage"])
            if f == quant_in:
                kind, a, n = args
                return [(copy_in, (kind, a, n, i) if kind == "g" else (kind, a, i, n)) for i in range(2)], []
            if f == tanh:
                k = args[0]
                return [(load, piece["gate row", k - 2] if 2 <= k < 6 else piece[("gate",) + steps[k]][0])], []
            if f == square:
                return ([(tanh,) + args, gate_of[args[0]]], ["stage"]) if args[0] in gate_of else ([(tanh,) + args], [])
            if f == factor:
                return [(square,) + args, (load, piece[("attn",) + steps[args[0]]][0])], []
            if f == dg:
                g, a, c = steps[args[0]]
                return [(quant_in, "g", g, a), (quant_in, "w", c, 0), (quant_in, "w", c, 1)], [lender(("dg",) + args)]
            if f == dz:
                g, a, c = steps[args[0]]
                return [(dg,) + args, (factor, args[0] - args[0] % 2 + args[1] if 2 <= args[0] < 6 else args[0])], ([] if ("dz", g, c) in tiles else ["dz"])
            if f == turn_dz:
                return [(dz, args[0], 0), (dz, args[0], 1)], [lender(("tz", args[0]))]
            if f == copy_dz:
                return [(turn_dz,) + args], ["es"]
            if f == quant_features:
                return [(copy_dz,) + args], []
            if f == weave_aside:
                return [(load, ("xraw", args[0])), gate_of[args]], ["stage"]
            if f == weave_x:
                return ([(weave_aside,) + args], []) if args in gate_of else ([(load, ("xraw", args[0]))], ["stage"])
            if f == weave_dz:
                return [(dz, steps.index((args[0], a, args[1])), i) for a in range(2) for i in range(2)], ["stage"]
            if f == quant_x:
                return [(weave_aside if args in gate_of else weave_x,) + args], []
            if f == quant_tokens:
                return [(weave_dz,) + args], []
            if f == product:
                (kind, a, b, half), s0, s1 = args
                if kind == "dx":
                    before = [(quant_features, steps.index((a, b // 2, s))) for s in range(s0, s1)]
                    before += [(quant_in, "q", half, s) for s in range(s0, s1)]
                else:
                    before = [(quant_x, s, b // 2) for s in range(s0, s1)] + [(quant_tokens, s, a) for s in range(s0, s1)]
                return before, ([lender(args[0])] if s0 == 0 else [])
            if f == copy_out:
                return [last[args[0]]], ([] if ("o",) + args[0][:3] in tiles else spare(args[0])[:1] or ["none"])
            if f == store:
                return [(copy_out, args[0][:3] + (half,)) for half in range(2)], []
            return [(copy_out,) + args], []

        def each(f, jobs):
            return [(f, job) for job in jobs]

        def both(f, k):
            return [(f, k, 0), (f, k, 1)]

        def rows(k):
            return [(dz, k + c, i) for i in range(2) for c in range(2)]

        def passes(jobs, s0=0, s1=None):
            return [(product, job, s0, s1 or (3 if job[0] == "dx" else 2)) for job in jobs]

        def quants(kind, a, ns):
            return [(quant_in, kind, a, n) for n in ns]

        g0, g1 = [[("g", g, a, h) for a in range(2) for h in range(2)] for g in range(2)]
        w0, w1, w2 = [[("w", c, a, h) for a in range(2) for h in range(2)] for c in range(3)]
        q0, q1 = [[("q", n, b, h) for b in range(2) for h in range(3)] for n in range(2)]
        dx0, dx1 = [[("dx", g, j, n) for j in range(4) for n in range(2)] for g in range(2)]
        dw0, dw1, dw2 = [[("dw", c, t, i) for t in range(4) for i in range(2)] for c in range(3)]

        tensor = each(turn_in, g0[:2] + w0) + both(dg, 0) + each(turn_in, g0[2:] + w1) + both(dg, 1) + each(turn_in, w2[:2]) + [(turn_dz, 0), (dg, 2, 0)]
        tensor += each(turn_in, w2[2:]) + [(dg, 2, 1), (turn_dz, 1)] + each(turn_in, q0[:2]) + [(dg, 3, 0)] + each(turn_in, q0[2:3]) + [(dg, 3, 1)]
        tensor += each(turn_in, q0[3:5]) + [(dg, 4, 0)] + each(turn_in, q0[5:]) + [(turn_dz, 2), (dg, 4, 1), (turn_dz, 3), (dg, 5, 0)] + each(turn_in, g1[:2]) + [(dg, 5, 1)] + each(turn_in, g1[2:])
        tensor += passes(dx0[:1]) + each(turn_in, q1[:2]) + passes(dx0[2:3]) + each(turn_in, q1[2:4]) + [(dg, 6, 0)] + each(turn_in, q1[4:]) + [(dg, 6, 1)]
        tensor += each(turn_dz, [4, 5]) + both(dg, 7)
        tensor += passes([dx0[1], dx0[3], dx0[4], dx0[6], dx0[5], dx0[7]])
        tensor += both(dg, 8) + each(turn_dz, [6, 7]) + both(dg, 9) + passes(dw0[:2], 0, 1) + passes(dw0[:2], 1) + passes(dw0[2:])
        tensor += both(dg, 10) + both(dg, 11) + each(turn_dz, [8, 9]) + passes(dw1[:2], 0, 1) + passes(dw1[:2], 1) + passes(dw1[2:5]) + [(turn_dz, 10)] + passes(dw1[5:6])
        tensor += passes(dw1[6:]) + passes(dx1[:2], 0, 2) + passes(dx1[:2], 2) + [(turn_dz, 11)] + passes(dx1[2:4])
        tail = dx1[4:6] + dw2[:6] + dx1[6:] + dw2[6:]
        tensor += passes(tail)

        scalar = [(copy_in, g0[1]), (copy_in, w0[1]), (tanh, 0), (copy_in, w0[3]), (square, 0), (tanh, 1), (square, 1)] + each(copy_in, g0[2:] + w1[:1])
        scalar += [(tanh, 2), (tanh, 3), (square, 2)] + each(copy_in, w2[:2]) + [(square, 3)] + each(copy_in, w2[2:]) + [(copy_dz, 0)]
        scalar += each(copy_in, q0[:5]) + [(tanh, 4), (copy_dz, 2), (tanh, 5), (square, 4), (copy_dz, 3), (copy_in, g1[1]), (square, 5)]
        scalar += each(copy_in, g1[2:]) + [(copy_out, dx0[0]), (tanh, 6)] + each(copy_in, q1[:2]) + [(square, 6)] + each(copy_in, q1[2:]) + [(tanh, 7)] + each(copy_dz, [4, 5])
        scalar += [(square, 7), (copy_out, dx0[1]), (copy_out, dx0[3]), (tanh, 8), (tanh, 9), (copy_out, dx0[6]), (square, 8)] + each(copy_out, [dx0[5], dx0[7]])
        scalar += [(square, 9), (copy_dz, 6), (tanh, 10), (copy_dz, 7)] + each(copy_out, dw0[:6]) + [(tanh, 11)] + each(copy_out, dw0[6:]) + [(square, 11)] + each(copy_dz, [8, 9])
        scalar += each(copy_out, dw1[:4]) + [(copy_dz, 10)] + each(copy_out, dw1[4:] + dx1[:1]) + [(copy_dz, 11)] + each(copy_out, dx1[1:4] + tail[1::2])

        vector = [(copy_in, g0[0]), (quant_in, "g", 0, 0)] + each(copy_in, w0[0::2]) + quants("w", 0, [0, 1]) + [(factor, 0)] + both(dz, 0)
        vector += [(factor, 1)] + quants("g", 0, [1]) + each(copy_in, w1[1:]) + quants("w", 1, [0, 1]) + both(dz, 1)
        vector += [(factor, 2), (weave_dz, 0, 0)] + quants("w", 2, [0, 1]) + [(quant_features, 0), (quant_tokens, 0, 0), (factor, 3)]
        vector += [(copy_dz, 1)] + rows(2) + [(quant_features, 1), (quant_x, 0, 0)] + quants("q", 0, [0]) + [(copy_in, q0[5])] + quants("q", 0, [1, 2]) + [(quant_features, 2), (copy_in, g1[0])]
        vector += [(factor, 4), (quant_features, 3)] + quants("g", 1, [0]) + [(factor, 5)]
        vector += rows(4) + [(copy_out, dx0[2])] + quants("g", 1, [1]) + [(quant_x, 0, 1), (factor, 6)]
        vector += quants("q", 1, [0, 1, 2]) + [(weave_x, 1, 0), (quant_features, 4), (quant_features, 5), (quant_x, 1, 0), (factor, 7)]
        vector += both(dz, 6) + both(dz, 7) + [(copy_out, dx0[4]), (weave_dz, 1, 0), (quant_x, 1, 1), (quant_tokens, 1, 0), (weave_dz, 0, 1), (factor, 8), (quant_tokens, 0, 1), (factor, 9)]
        vector += both(dz, 8) + both(dz, 9) + [(quant_features, 6), (weave_dz, 1, 1), (quant_features, 7), (quant_tokens, 1, 1), (factor, 10), (quant_features, 8)]
        vector += both(dz, 10) + [(factor, 11), (quant_features, 9)] + both(dz, 11) + [(quant_features, 10), (weave_dz, 0, 2), (weave_dz, 1, 2), (quant_features, 11), (quant_tokens, 0, 2), (quant_tokens, 1, 2)]
        vector += [] + each(copy_out, tail[0::2])

        dma = each(load, [key for kind, key, src in loads]) + each(store, (dx0 + dw0 + dw1 + dx1[:4] + tail[:-2])[1::2]) + each(store_bank, tail[-2:])
        lent = {("tz", 1): "S", q1[3]: "V", dx0[4]: "S", ("tz", 6): "V", dw1[5]: "V"}
        gate_of = {(0, 0): (quant_tokens, 0, 0), (0, 1): (quant_in, "g", 1, 0), (1, 1): (quant_x, 1, 0), 10: (quant_tokens, 0, 1)}
        extra = [[(weave_aside, 0, 0), (weave_aside, 0, 1), (weave_aside, 1, 1), (square, 10)]]


        drainer = {("warm", call[1]): "S" for call in tensor if call[0] == warm}
        for name, queue in (("V", vector), ("S", scalar)):
            for call in queue:
                if call[0] in (copy_in, copy_out):
                    drainer[call[1]] = name
                elif call[0] == copy_dz:
                    drainer["tz", call[1]] = name
                elif call[0] == dz:
                    drainer[("dg",) + call[1:]] = name
        last = {call[1]: call for call in tensor if call[0] == product}
        free["none"] = []


        def lender(key):
            return lent.get(key, drainer[key])


        made = set()
        queues = [dma, tensor, scalar, vector] + extra
        while any(queues):
            moved = False
            for queue in queues:
                if queue:
                    before, kinds = needs(queue[0])
                    if all(call in made for call in before) and all(free[kind] for kind in kinds):
                        call = queue.pop(0)
                        call[0](*call[1:])
                        made.add(call)
                        moved = True
            assert moved, [(queue[0][0], queue[0][1:], needs(queue[0])[1]) for queue in queues if queue]
